import numpy as np
import ml_dtypes


def mxq(x, axis, fmt="e4m3"):
    dtype, down = {"e4m3": (ml_dtypes.float8_e4m3fn, 7), "e5m2": (ml_dtypes.float8_e5m2, 14)}[fmt]
    v = np.moveaxis(np.asarray(x, np.float32).astype(ml_dtypes.bfloat16).astype(np.float64), axis, -1)
    blocks = v.reshape(v.shape[:-1] + (-1, 32))
    amax = np.abs(blocks).max(-1, keepdims=True)
    byte = np.maximum(np.where(amax > 0, np.frexp(amax)[1] - 1 + 127, 0) - down, 1)
    scale = np.exp2(byte - 127.0)
    codes = (blocks / scale).astype(np.float32).astype(dtype).astype(np.float64)
    return np.moveaxis((codes * scale).reshape(v.shape), -1, axis)


WIDE = False


def mx_kscale(k):
    if not WIDE:
        return np.ones(k)
    levels = np.array([10, -10, 5, -5, 0])
    a = np.random.permutation(np.resize(levels, k // 512 * 4)).reshape(k // 512, 4)
    idx = np.arange(k)
    return np.exp2(a[idx // 512, idx % 128 // 32])


BF16 = ml_dtypes.bfloat16


def bf(x):
    return np.asarray(x, np.float32).astype(BF16)


def f64(x):
    return np.asarray(x).astype(np.float64)


N, DIN, DI, DH, DO, G = 8192, 1024, 512, 256, 512, 16
DH2 = 2 * DH
EPS = 1e-5


def erf(v):
    a = np.minimum(np.abs(v), 6.0)
    term = a.copy()
    tot = a.copy()
    for n in range(1, 120):
        term = term * (2.0 * a * a / (2 * n + 1))
        tot = tot + term
    return np.sign(v) * (2.0 / np.sqrt(np.pi)) * np.exp(-a * a) * tot


def gelu_erf(v):
    return 0.5 * v * (1.0 + erf(v / np.sqrt(2.0)))


def setup_inputs():
    s, u = mx_kscale(DI), mx_kscale(DO)
    tt = np.array(mx_kscale(DH2), dtype=np.float64)
    tt[:DH] = 1.0
    t = tt[DH:]
    return {"h_ret": bf(np.random.standard_normal((N, DI)) * 0.6 * s),
            "h_prime": bf(np.random.standard_normal((N, DO)) * u),
            "Wr": bf(np.random.standard_normal((DH, DI)) * 2.0 / np.sqrt(DI) / s[None, :]),
            "br": bf(np.random.standard_normal(DH) * 0.2),
            "Wc": bf(np.random.standard_normal((DH, DO)) / np.sqrt(DO) * t[:, None] / u[None, :]),
            "bc": bf(np.random.standard_normal(DH) * 0.2 * t),
            "Wp": bf(np.random.standard_normal((DO, DH2)) / np.sqrt(DH2) / tt[None, :]),
            "bp": bf(np.random.standard_normal(DO) * 0.2),
            "prelu_w": bf(0.25 + 0.1 * np.random.standard_normal(DO)),
            "gn_w": bf(1.0 + 0.1 * np.random.standard_normal(DO)),
            "gn_b": bf(0.1 * np.random.standard_normal(DO))}


def reference(h_ret, h_prime, Wr, br, Wc, bc, Wp, bp, prelu_w, gn_w, gn_b):
    a = gelu_erf((mxq(f64(h_ret), 1, "e4m3") @ mxq(f64(Wr), 1, "e4m3").T) + f64(br))
    c = (mxq(f64(h_prime), 1, "e4m3") @ mxq(f64(Wc), 1, "e4m3").T) + f64(bc)
    combined = np.concatenate([a, c], axis=-1)
    x = (mxq(combined, 1, "e4m3") @ mxq(f64(Wp), 1, "e4m3").T) + f64(bp)
    x = np.where(x >= 0, x, f64(prelu_w)[None, :] * x)
    xg = x.T.reshape(G, -1)
    mean = xg.mean(axis=1, keepdims=True)
    var = xg.var(axis=1, keepdims=True)
    xg = (xg - mean) / np.sqrt(var + EPS)
    xt = xg.reshape(DO, N) * f64(gn_w)[:, None] + f64(gn_b)[:, None]
    return np.ascontiguousarray(xt.T)

@@ -1,0 +1,318 @@
+from contextlib import ExitStack
+
+import concourse.mybir as mybir
+from concourse.masks import make_identity
+
+F32 = mybir.dt.float32
+BF16 = mybir.dt.bfloat16
+U32 = mybir.dt.uint32
+U8 = mybir.dt.uint8
+FP8X4 = mybir.dt.float8_e4m3fn_x4
+ACT = mybir.ActivationFunctionType
+ALU = mybir.AluOpType
+
+P = 128
+ROWS = 8192
+K = 512
+CHANNELS = 512
+GROUP = 32
+EPS = 1e-5
+
+BLOCK = 1024
+TILES = BLOCK // P
+N_BLOCKS = ROWS // BLOCK
+HALF = 512
+N_HALVES = ROWS // HALF
+PAIR = 256
+N_CB = CHANNELS // P
+LAG = N_BLOCKS + 1
+
+FLOPS = 2 * ROWS * (K * 256 * 2 + K * CHANNELS)
+
+
+def transpose_row_tiles(nc, bank, words, first_tile, ident):
+    for i in range(2):
+        for u in range(2):
+            start = (first_tile + i) * (K // 2) + u * P
+            nc.tensor.transpose(bank[:, u, i * P : (i + 1) * P], words[:, start : start + P], ident[:])
+
+
+def tile_parallelretention_pb_t_kernel(
+    tc, h_ret, h_prime, Wr, br, Wc, bc, Wp, bp, prelu_w, gn_w, gn_b, out
+):
+    nc = tc.nc
+    with ExitStack() as whole:
+        keep = whole.enter_context(tc.tile_pool(name="keep", bufs=1))
+
+        ident = keep.tile([P, P], F32)
+        make_identity(nc, ident[:])
+
+        group_avg = keep.tile([P, P], F32)
+        nc.vector.memset(group_avg[:], 0.0)
+        for g in range(P // GROUP):
+            span = slice(g * GROUP, (g + 1) * GROUP)
+            nc.vector.memset(group_avg[span, span], 1.0 / GROUP)
+        neg_half = keep.tile([P, 1], F32)
+        nc.vector.memset(neg_half[:], -0.5)
+
+        w1_codes = keep.tile([P, 4 * P], U32, align_bytes=64)
+        w1_scales = keep.tile([P, 4 * P], U8, align_bytes=64)
+        wp_codes = keep.tile([P, 2 * CHANNELS], U32, align_bytes=64)
+        wp_scales = keep.tile([P, 2 * CHANNELS], U8, align_bytes=64)
+        ac_codes = []
+        ac_scales = []
+        for h in range(N_HALVES):
+            ac_codes.append(keep.tile([P, 2 * HALF], U32, name="ac_codes%d" % h, align_bytes=64))
+            ac_scales.append(keep.tile([P, 2 * HALF], U8, name="ac_scales%d" % h, align_bytes=64))
+        bias1 = keep.tile([P, 4], F32)
+        chan = keep.tile([P, 16], F32)
+        neg_bp = keep.tile([P, N_CB], F32)
+        one_minus_w = keep.tile([P, N_CB], F32)
+        bp_c = chan[:, 0:4]
+        gn_w_c = chan[:, 8:12]
+        gn_b_c = chan[:, 12:16]
+
+        with ExitStack() as stage1:
+            once = stage1.enter_context(tc.tile_pool(name="once", bufs=1))
+            loads = stage1.enter_context(tc.tile_pool(name="loads", bufs=3))
+            work = stage1.enter_context(tc.tile_pool(name="work", bufs=2))
+            ps_t = stage1.enter_context(tc.psum_pool(name="ps_t", bufs=4))
+            ps_1 = stage1.enter_context(tc.psum_pool(name="ps_1", bufs=4))
+
+            w1_sb = once.tile([P, 4 * K], BF16)
+            nc.sync.dma_start(out=w1_sb[:, 0 : 2 * K], in_=Wr.rearrange("(p t) k -> p (t k)", t=2))
+            nc.sync.dma_start(out=w1_sb[:, 2 * K : 4 * K], in_=Wc.rearrange("(p t) k -> p (t k)", t=2))
+            br_bf = once.tile([P, 2], BF16)
+            bc_bf = once.tile([P, 2], BF16)
+            nc.scalar.dma_start(out=br_bf[:], in_=br.rearrange("(p t) -> p t", t=2))
+            nc.scalar.dma_start(out=bc_bf[:], in_=bc.rearrange("(p t) -> p t", t=2))
+            nc.vector.tensor_copy(out=bias1[:, 0:2], in_=br_bf[:])
+            nc.vector.tensor_copy(out=bias1[:, 2:4], in_=bc_bf[:])
+
+            h_tiles = {}
+
+            def load_block(b):
+                rows = slice(b * BLOCK, (b + 1) * BLOCK)
+                hr = loads.tile([P, TILES * K], BF16)
+                nc.sync.dma_start(out=hr[:], in_=h_ret[rows, :].rearrange("(p j) k -> p (j k)", j=TILES))
+                hp = loads.tile([P, TILES * K], BF16)
+                nc.sync.dma_start(out=hp[:], in_=h_prime[rows, :].rearrange("(p j) k -> p (j k)", j=TILES))
+                h_tiles[b] = (hr, hp)
+
+            load_block(0)
+
+            wp_sb = once.tile([P, N_CB * K], BF16)
+            nc.sync.dma_start(
+                out=wp_sb[:].rearrange("p (c k) -> p c k", c=N_CB), in_=Wp.rearrange("(c p) k -> p c k", p=P)
+            )
+            rows_bf = once.tile([P, P], BF16)
+            nc.vector.memset(rows_bf[:], 0.0)
+            for v, vec in enumerate((bp, prelu_w, gn_w, gn_b)):
+                nc.scalar.dma_start(out=rows_bf[4 * v : 4 * v + 4, :], in_=vec.rearrange("(c p) -> c p", p=P))
+
+            w1_grouped = once.tile([P, 4 * P * 4], BF16, align_bytes=64)
+            w1_g32 = w1_grouped[:].bitcast(F32).rearrange("p (c u) -> p c u", u=2)
+            for pair in range(2):
+                bank = ps_t.tile([P, 2, PAIR], F32, tag="ht")
+                transpose_row_tiles(nc, bank, w1_sb[:].bitcast(F32), 2 * pair, ident)
+                nc.vector.tensor_copy(
+                    out=w1_g32[:, pair * PAIR : (pair + 1) * PAIR, :], in_=bank[:].rearrange("p u c -> p c u")
+                )
+            nc.vector.quantize_mx(out=w1_codes[:].bitcast(FP8X4), scales=w1_scales[:], in_=w1_grouped[:])
+
+            ac_grouped = []
+            for i in range(2):
+                ac_grouped.append(once.tile([P, 2, HALF, 4], BF16, name="ac_grouped%d" % i, align_bytes=64))
+                nc.vector.memset(ac_grouped[i][:], 0.0)
+
+            h_quantised = {}
+
+            def front(h):
+                b, half = divmod(h, 2)
+                if half == 0 and b + 1 < N_BLOCKS:
+                    load_block(b + 1)
+                grouped = work.tile([P, 2 * HALF * 4], BF16, align_bytes=64)
+                g32 = grouped[:].bitcast(F32).rearrange("p (i c u) -> p i c u", i=2, u=2)
+                for i in range(2):
+                    words = h_tiles[b][i][:].bitcast(F32)
+                    for pair in range(2):
+                        bank = ps_t.tile([P, 2, PAIR], F32, tag="ht")
+                        transpose_row_tiles(nc, bank, words, 4 * half + 2 * pair, ident)
+                        nc.scalar.copy(
+                            out=g32[:, i, pair * PAIR : (pair + 1) * PAIR, :],
+                            in_=bank[:].rearrange("p u c -> p c u"),
+                        )
+                h_codes = work.tile([P, 2 * HALF], U32, align_bytes=64)
+                h_scales = work.tile([P, 2 * HALF], U8, align_bytes=64)
+                nc.vector.quantize_mx(out=h_codes[:].bitcast(FP8X4), scales=h_scales[:], in_=grouped[:])
+                h_quantised[h] = (h_codes, h_scales)
+
+            def back(h):
+                h_codes, h_scales = h_quantised[h]
+                staged = work.tile([P, 4, HALF], BF16)
+                for m in range(4):
+                    i = m // 2
+                    acc = ps_1.tile([P, HALF], F32, tag="s1")
+                    nc.tensor.matmul_mx(
+                        out=acc[:],
+                        lhsT=w1_codes[:, m * P : (m + 1) * P].bitcast(FP8X4),
+                        lhsT_scale=w1_scales[:, m * P : (m + 1) * P],
+                        rhs=h_codes[:, i * HALF : (i + 1) * HALF].bitcast(FP8X4),
+                        rhs_scale=h_scales[:, i * HALF : (i + 1) * HALF],
+                        start=True,
+                        stop=True,
+                    )
+                    nc.scalar.activation(
+                        out=staged[:, m, :],
+                        in_=acc[:],
+                        func=ACT.Gelu if i == 0 else ACT.Identity,
+                        bias=bias1[:, m : m + 1],
+                        scale=1.0,
+                    )
+                grouped = ac_grouped[h % 2]
+                nc.vector.tensor_copy(
+                    out=grouped[:, :, :, 0:2], in_=staged[:].rearrange("p (i t) c -> p i c t", t=2)
+                )
+                nc.vector.quantize_mx(
+                    out=ac_codes[h][:].bitcast(FP8X4),
+                    scales=ac_scales[h][:],
+                    in_=grouped[:].rearrange("p i c t -> p (i c t)"),
+                )
+
+            front(0)
+
+            wp_grouped = once.tile([P, 2 * CHANNELS * 4], BF16, align_bytes=64)
+            nc.vector.memset(wp_grouped[:], 0.0)
+            wp_g32 = wp_grouped[:].bitcast(F32).rearrange("p (i c s) -> p i c s", i=2, s=2)
+            for pair in range(2):
+                bank = ps_t.tile([P, 2, PAIR], F32, tag="ht")
+                transpose_row_tiles(nc, bank, wp_sb[:].bitcast(F32), 2 * pair, ident)
+                nc.vector.tensor_copy(out=wp_g32[:, :, pair * PAIR : (pair + 1) * PAIR, 0], in_=bank[:])
+            nc.vector.quantize_mx(out=wp_codes[:].bitcast(FP8X4), scales=wp_scales[:], in_=wp_grouped[:])
+
+            rows_f32 = once.tile([P, P], F32)
+            nc.vector.tensor_copy(out=rows_f32[:], in_=rows_bf[:])
+            bank = ps_t.tile([P, 2, PAIR], F32, tag="ht")
+            nc.tensor.transpose(bank[:, 0, 0:P], rows_f32[:], ident[:])
+            nc.vector.tensor_copy(out=chan[:], in_=bank[:, 0, 0:16])
+            nc.vector.tensor_scalar(
+                out=neg_bp[:], in0=chan[:, 0:4], scalar1=-1.0, scalar2=None, op0=ALU.mult
+            )
+            nc.vector.tensor_scalar(
+                out=one_minus_w[:], in0=chan[:, 4:8], scalar1=-1.0, scalar2=1.0, op0=ALU.mult, op1=ALU.add
+            )
+
+            for h in range(1, N_HALVES + 1):
+                if h < N_HALVES:
+                    front(h)
+                back(h - 1)
+
+        with ExitStack() as stage2:
+            y_pool = stage2.enter_context(tc.tile_pool(name="y_pool", bufs=LAG + 2))
+            work2 = stage2.enter_context(tc.tile_pool(name="work2", bufs=3))
+            small = stage2.enter_context(tc.tile_pool(name="small", bufs=2))
+            ps_x = stage2.enter_context(tc.psum_pool(name="ps_x", bufs=4))
+            ps_z = stage2.enter_context(tc.psum_pool(name="ps_z", bufs=3))
+            ps_g = stage2.enter_context(tc.psum_pool(name="ps_g", bufs=1))
+
+            y_tiles = {}
+            stats_tiles = {}
+            coefficients = {}
+
+            def prelu_block(cb, b):
+                if b == 0:
+                    stats = small.tile([P, N_HALVES, 6], F32)
+                    stats_tiles[cb] = stats
+                stats = stats_tiles[cb]
+                neg = work2.tile([P, BLOCK], F32)
+                y = y_pool.tile([P, BLOCK], F32)
+                y_tiles[(cb, b)] = y
+                for half in range(2):
+                    h = 2 * b + half
+                    cols = slice(half * HALF, (half + 1) * HALF)
+                    x = ps_x.tile([P, HALF], F32, tag="x")
+                    for i in range(2):
+                        w_cols = slice(i * CHANNELS + cb * P, i * CHANNELS + (cb + 1) * P)
+                        nc.tensor.matmul_mx(
+                            out=x[:],
+                            lhsT=wp_codes[:, w_cols].bitcast(FP8X4),
+                            lhsT_scale=wp_scales[:, w_cols],
+                            rhs=ac_codes[h][:, i * HALF : (i + 1) * HALF].bitcast(FP8X4),
+                            rhs_scale=ac_scales[h][:, i * HALF : (i + 1) * HALF],
+                            start=(i == 0),
+                            stop=(i == 1),
+                        )
+                    nc.scalar.activation(
+                        out=neg[:, cols], in_=x[:], func=ACT.Relu, bias=neg_bp[:, cb : cb + 1], scale=-1.0
+                    )
+                    nc.vector.scalar_tensor_tensor(
+                        out=y[:, cols],
+                        in0=neg[:, cols],
+                        scalar=one_minus_w[:, cb : cb + 1],
+                        in1=x[:],
+                        op0=ALU.mult,
+                        op1=ALU.add,
+                    )
+                    nc.vector.bn_stats(out=stats[:, h, :], in_=y[:, cols])
+
+            def group_statistics(cb):
+                one = slice(cb, cb + 1)
+                mv = small.tile([P, 2], F32)
+                nc.vector.bn_aggr(out=mv[:], in_=stats_tiles[cb][:].rearrange("p n s -> p (n s)"))
+                nc.vector.tensor_add(out=mv[:, 0:1], in0=mv[:, 0:1], in1=bp_c[:, one])
+                g1 = ps_g.tile([P, 2], F32, tag="g")
+                nc.tensor.matmul(out=g1[:], lhsT=group_avg[:], rhs=mv[:], start=True, stop=True)
+                gm = small.tile([P, 2], F32)
+                nc.vector.tensor_copy(out=gm[:], in_=g1[:])
+                dev = small.tile([P, 2], F32)
+                nc.vector.tensor_sub(out=dev[:], in0=mv[:], in1=gm[:])
+                nc.vector.tensor_mul(out=dev[:], in0=dev[:], in1=dev[:])
+                g2 = ps_g.tile([P, 2], F32, tag="g")
+                nc.tensor.matmul(out=g2[:], lhsT=group_avg[:], rhs=dev[:], start=True, stop=True)
+                var_eps = small.tile([P, 1], F32)
+                nc.vector.scalar_tensor_tensor(
+                    out=var_eps[:], in0=g2[:, 0:1], scalar=EPS, in1=gm[:, 1:2], op0=ALU.add, op1=ALU.add
+                )
+                centre = small.tile([P, 1], F32)
+                nc.vector.tensor_sub(out=centre[:], in0=bp_c[:, one], in1=gm[:, 0:1])
+                rstd = small.tile([P, 1], F32)
+                nc.gpsimd.tensor_tensor(out=rstd[:], in0=var_eps[:], in1=neg_half[:], op=ALU.pow)
+                scale = small.tile([P, 1], F32)
+                nc.gpsimd.tensor_tensor(out=scale[:], in0=rstd[:], in1=gn_w_c[:, one], op=ALU.mult)
+                shift = small.tile([P, 1], F32)
+                nc.gpsimd.tensor_scalar(
+                    out=shift[:], in0=centre[:], scalar1=scale[:, 0:1], scalar2=gn_b_c[:, one],
+                    op0=ALU.mult, op1=ALU.add,
+                )
+                coefficients[cb] = (scale, shift)
+
+            def normalise_block(cb, b):
+                y = y_tiles[(cb, b)]
+                scale, shift = coefficients[cb]
+                nc.gpsimd.tensor_scalar(
+                    out=y[:], in0=y[:], scalar1=scale[:, 0:1], scalar2=shift[:, 0:1], op0=ALU.mult, op1=ALU.add
+                )
+                z = work2.tile([P, TILES, P], F32)
+                for half in range(2):
+                    zt = ps_z.tile([P, 4, P], F32, tag="zt")
+                    for j in range(4):
+                        col = (4 * half + j) * P
+                        nc.tensor.transpose(zt[:, j, :], y[:, col : col + P], ident[:])
+                    nc.scalar.copy(out=z[:, 4 * half : 4 * half + 4, :], in_=zt[:])
+                nc.sync.dma_start(
+                    out=out[b * BLOCK : (b + 1) * BLOCK, cb * P : (cb + 1) * P].rearrange(
+                        "(p j) c -> p j c", j=TILES
+                    ),
+                    in_=z[:],
+                )
+
+            steps = N_CB * N_BLOCKS
+            for step in range(steps + LAG):
+                if step < steps:
+                    cb, b = divmod(step, N_BLOCKS)
+                    prelu_block(cb, b)
+                    if b == N_BLOCKS - 1:
+                        group_statistics(cb)
+                if step >= LAG:
+                    cb, b = divmod(step - LAG, N_BLOCKS)
+                    normalise_block(cb, b)

@@ -7,6 +7,7 @@ F32 = mybir.dt.float32
 BF16 = mybir.dt.bfloat16
 U32 = mybir.dt.uint32
 U8 = mybir.dt.uint8
+I32 = mybir.dt.int32
 FP8X4 = mybir.dt.float8_e4m3fn_x4
 ACT = mybir.ActivationFunctionType
 ALU = mybir.AluOpType
@@ -25,7 +26,8 @@ HALF = 512
 N_HALVES = ROWS // HALF
 PAIR = 256
 N_CB = CHANNELS // P
-LAG = N_BLOCKS + 1
+STAT_PARTS = 3
+LAG = N_BLOCKS + STAT_PARTS
 
 FLOPS = 2 * ROWS * (K * 256 * 2 + K * CHANNELS)
 
@@ -42,6 +44,7 @@ def tile_parallelretention_pb_t_kernel(
 ):
     nc = tc.nc
     with ExitStack() as whole:
+        whole.enter_context(tc.manual_schedule())
         keep = whole.enter_context(tc.tile_pool(name="keep", bufs=1))
 
         ident = keep.tile([P, P], F32)
@@ -74,10 +77,23 @@ def tile_parallelretention_pb_t_kernel(
 
         with ExitStack() as stage1:
             once = stage1.enter_context(tc.tile_pool(name="once", bufs=1))
-            loads = stage1.enter_context(tc.tile_pool(name="loads", bufs=3))
+            loads = stage1.enter_context(tc.tile_pool(name="loads", bufs=4))
             work = stage1.enter_context(tc.tile_pool(name="work", bufs=2))
             ps_t = stage1.enter_context(tc.psum_pool(name="ps_t", bufs=4))
             ps_1 = stage1.enter_context(tc.psum_pool(name="ps_1", bufs=4))
+
+            warm = once.tile([P, 1], F32)
+            nc.vector.memset(warm[:], 0.0)
+            nc.scalar.activation(out=warm[:], in_=warm[:], func=ACT.Gelu)
+
+            rows_bf = once.tile([P, P], BF16)
+            nc.vector.memset(rows_bf[:], 0.0)
+            ac_grouped = []
+            for i in range(2):
+                ac_grouped.append(once.tile([P, 2, HALF, 4], BF16, name="ac_grouped%d" % i, align_bytes=64))
+                nc.vector.memset(ac_grouped[i][:].rearrange("p i c t -> p (i c t)").bitcast(I32), 0)
+            wp_grouped = once.tile([P, 2 * CHANNELS * 4], BF16, align_bytes=64)
+            nc.vector.memset(wp_grouped[:].bitcast(I32), 0)
 
             w1_sb = once.tile([P, 4 * K], BF16)
             nc.sync.dma_start(out=w1_sb[:, 0 : 2 * K], in_=Wr.rearrange("(p t) k -> p (t k)", t=2))
@@ -86,27 +102,26 @@ def tile_parallelretention_pb_t_kernel(
             bc_bf = once.tile([P, 2], BF16)
             nc.scalar.dma_start(out=br_bf[:], in_=br.rearrange("(p t) -> p t", t=2))
             nc.scalar.dma_start(out=bc_bf[:], in_=bc.rearrange("(p t) -> p t", t=2))
-            nc.vector.tensor_copy(out=bias1[:, 0:2], in_=br_bf[:])
-            nc.vector.tensor_copy(out=bias1[:, 2:4], in_=bc_bf[:])
 
             h_tiles = {}
 
-            def load_block(b):
+            def load_half(h):
+                b, half = divmod(h, 2)
                 rows = slice(b * BLOCK, (b + 1) * BLOCK)
-                hr = loads.tile([P, TILES * K], BF16)
-                nc.sync.dma_start(out=hr[:], in_=h_ret[rows, :].rearrange("(p j) k -> p (j k)", j=TILES))
-                hp = loads.tile([P, TILES * K], BF16)
-                nc.sync.dma_start(out=hp[:], in_=h_prime[rows, :].rearrange("(p j) k -> p (j k)", j=TILES))
-                h_tiles[b] = (hr, hp)
+                tiles = slice(4 * half, 4 * half + 4)
+                hr = loads.tile([P, 4, K], BF16)
+                nc.sync.dma_start(out=hr[:], in_=h_ret[rows, :].rearrange("(p j) k -> p j k", j=TILES)[:, tiles, :])
+                hp = loads.tile([P, 4, K], BF16)
+                nc.sync.dma_start(out=hp[:], in_=h_prime[rows, :].rearrange("(p j) k -> p j k", j=TILES)[:, tiles, :])
+                h_tiles[h] = (hr, hp)
 
-            load_block(0)
-
+            load_half(0)
+            load_half(1)
             wp_sb = once.tile([P, N_CB * K], BF16)
             nc.sync.dma_start(
                 out=wp_sb[:].rearrange("p (c k) -> p c k", c=N_CB), in_=Wp.rearrange("(c p) k -> p c k", p=P)
             )
-            rows_bf = once.tile([P, P], BF16)
-            nc.vector.memset(rows_bf[:], 0.0)
+            load_half(2)
             for v, vec in enumerate((bp, prelu_w, gn_w, gn_b)):
                 nc.scalar.dma_start(out=rows_bf[4 * v : 4 * v + 4, :], in_=vec.rearrange("(c p) -> c p", p=P))
 
@@ -119,25 +134,21 @@ def tile_parallelretention_pb_t_kernel(
                     out=w1_g32[:, pair * PAIR : (pair + 1) * PAIR, :], in_=bank[:].rearrange("p u c -> p c u")
                 )
             nc.vector.quantize_mx(out=w1_codes[:].bitcast(FP8X4), scales=w1_scales[:], in_=w1_grouped[:])
-
-            ac_grouped = []
-            for i in range(2):
-                ac_grouped.append(once.tile([P, 2, HALF, 4], BF16, name="ac_grouped%d" % i, align_bytes=64))
-                nc.vector.memset(ac_grouped[i][:], 0.0)
+            nc.vector.tensor_copy(out=bias1[:, 0:2], in_=br_bf[:])
+            nc.vector.tensor_copy(out=bias1[:, 2:4], in_=bc_bf[:])
 
             h_quantised = {}
 
-            def front(h):
-                b, half = divmod(h, 2)
-                if half == 0 and b + 1 < N_BLOCKS:
-                    load_block(b + 1)
+            def transpose_and_quantise(h):
+                if h + 3 < N_HALVES:
+                    load_half(h + 3)
                 grouped = work.tile([P, 2 * HALF * 4], BF16, align_bytes=64)
                 g32 = grouped[:].bitcast(F32).rearrange("p (i c u) -> p i c u", i=2, u=2)
                 for i in range(2):
-                    words = h_tiles[b][i][:].bitcast(F32)
+                    words = h_tiles[h][i][:].rearrange("p j k -> p (j k)").bitcast(F32)
                     for pair in range(2):
                         bank = ps_t.tile([P, 2, PAIR], F32, tag="ht")
-                        transpose_row_tiles(nc, bank, words, 4 * half + 2 * pair, ident)
+                        transpose_row_tiles(nc, bank, words, 2 * pair, ident)
                         nc.scalar.copy(
                             out=g32[:, i, pair * PAIR : (pair + 1) * PAIR, :],
                             in_=bank[:].rearrange("p u c -> p c u"),
@@ -147,89 +158,84 @@ def tile_parallelretention_pb_t_kernel(
                 nc.vector.quantize_mx(out=h_codes[:].bitcast(FP8X4), scales=h_scales[:], in_=grouped[:])
                 h_quantised[h] = (h_codes, h_scales)
 
-            def back(h):
+            def first_matmuls(h):
                 h_codes, h_scales = h_quantised[h]
                 staged = work.tile([P, 4, HALF], BF16)
-                for m in range(4):
-                    i = m // 2
-                    acc = ps_1.tile([P, HALF], F32, tag="s1")
-                    nc.tensor.matmul_mx(
-                        out=acc[:],
-                        lhsT=w1_codes[:, m * P : (m + 1) * P].bitcast(FP8X4),
-                        lhsT_scale=w1_scales[:, m * P : (m + 1) * P],
-                        rhs=h_codes[:, i * HALF : (i + 1) * HALF].bitcast(FP8X4),
-                        rhs_scale=h_scales[:, i * HALF : (i + 1) * HALF],
-                        start=True,
-                        stop=True,
+                for i in range(2):
+                    for t in range(2):
+                        m = 2 * i + t
+                        acc = ps_1.tile([P, HALF], F32, tag="s1")
+                        nc.tensor.matmul_mx(
+                            out=acc[:],
+                            lhsT=w1_codes[:, m * P : (m + 1) * P].bitcast(FP8X4),
+                            lhsT_scale=w1_scales[:, m * P : (m + 1) * P],
+                            rhs=h_codes[:, i * HALF : (i + 1) * HALF].bitcast(FP8X4),
+                            rhs_scale=h_scales[:, i * HALF : (i + 1) * HALF],
+                            start=True,
+                            stop=True,
+                        )
+                        nc.scalar.activation(
+                            out=staged[:, m, :],
+                            in_=acc[:],
+                            func=ACT.Gelu if i == 0 else ACT.Identity,
+                            bias=bias1[:, m : m + 1],
+                            scale=1.0,
+                        )
+                    nc.vector.tensor_copy(
+                        out=ac_grouped[h % 2][:, i, :, 0:2],
+                        in_=staged[:, 2 * i : 2 * i + 2, :].rearrange("p t c -> p c t"),
                     )
-                    nc.scalar.activation(
-                        out=staged[:, m, :],
-                        in_=acc[:],
-                        func=ACT.Gelu if i == 0 else ACT.Identity,
-                        bias=bias1[:, m : m + 1],
-                        scale=1.0,
-                    )
-                grouped = ac_grouped[h % 2]
-                nc.vector.tensor_copy(
-                    out=grouped[:, :, :, 0:2], in_=staged[:].rearrange("p (i t) c -> p i c t", t=2)
-                )
+
+            def quantise_ac(h):
                 nc.vector.quantize_mx(
                     out=ac_codes[h][:].bitcast(FP8X4),
                     scales=ac_scales[h][:],
-                    in_=grouped[:].rearrange("p i c t -> p (i c t)"),
+                    in_=ac_grouped[h % 2][:].rearrange("p i c t -> p (i c t)"),
                 )
 
-            front(0)
-
-            wp_grouped = once.tile([P, 2 * CHANNELS * 4], BF16, align_bytes=64)
-            nc.vector.memset(wp_grouped[:], 0.0)
-            wp_g32 = wp_grouped[:].bitcast(F32).rearrange("p (i c s) -> p i c s", i=2, s=2)
-            for pair in range(2):
+            def prepare_wp_and_channel_vectors():
+                wp_g32 = wp_grouped[:].bitcast(F32).rearrange("p (i c s) -> p i c s", i=2, s=2)
+                for pair in range(2):
+                    bank = ps_t.tile([P, 2, PAIR], F32, tag="ht")
+                    transpose_row_tiles(nc, bank, wp_sb[:].bitcast(F32), 2 * pair, ident)
+                    nc.vector.tensor_copy(out=wp_g32[:, :, pair * PAIR : (pair + 1) * PAIR, 0], in_=bank[:])
+                nc.vector.quantize_mx(out=wp_codes[:].bitcast(FP8X4), scales=wp_scales[:], in_=wp_grouped[:])
+                rows_f32 = once.tile([P, P], F32)
+                nc.vector.tensor_copy(out=rows_f32[:], in_=rows_bf[:])
                 bank = ps_t.tile([P, 2, PAIR], F32, tag="ht")
-                transpose_row_tiles(nc, bank, wp_sb[:].bitcast(F32), 2 * pair, ident)
-                nc.vector.tensor_copy(out=wp_g32[:, :, pair * PAIR : (pair + 1) * PAIR, 0], in_=bank[:])
-            nc.vector.quantize_mx(out=wp_codes[:].bitcast(FP8X4), scales=wp_scales[:], in_=wp_grouped[:])
+                nc.tensor.transpose(bank[:, 0, 0:P], rows_f32[:], ident[:])
+                nc.vector.tensor_copy(out=chan[:], in_=bank[:, 0, 0:16])
+                nc.vector.tensor_scalar(out=neg_bp[:], in0=chan[:, 0:4], scalar1=-1.0, scalar2=None, op0=ALU.mult)
+                nc.vector.tensor_scalar(
+                    out=one_minus_w[:], in0=chan[:, 4:8], scalar1=-1.0, scalar2=1.0, op0=ALU.mult, op1=ALU.add
+                )
 
-            rows_f32 = once.tile([P, P], F32)
-            nc.vector.tensor_copy(out=rows_f32[:], in_=rows_bf[:])
-            bank = ps_t.tile([P, 2, PAIR], F32, tag="ht")
-            nc.tensor.transpose(bank[:, 0, 0:P], rows_f32[:], ident[:])
-            nc.vector.tensor_copy(out=chan[:], in_=bank[:, 0, 0:16])
-            nc.vector.tensor_scalar(
-                out=neg_bp[:], in0=chan[:, 0:4], scalar1=-1.0, scalar2=None, op0=ALU.mult
-            )
-            nc.vector.tensor_scalar(
-                out=one_minus_w[:], in0=chan[:, 4:8], scalar1=-1.0, scalar2=1.0, op0=ALU.mult, op1=ALU.add
-            )
-
-            for h in range(1, N_HALVES + 1):
-                if h < N_HALVES:
-                    front(h)
-                back(h - 1)
+            for i in range(N_HALVES + 2):
+                if i < N_HALVES:
+                    transpose_and_quantise(i)
+                if i == 0:
+                    prepare_wp_and_channel_vectors()
+                if i >= 2:
+                    quantise_ac(i - 2)
+                if 1 <= i <= N_HALVES:
+                    first_matmuls(i - 1)
 
         with ExitStack() as stage2:
             y_pool = stage2.enter_context(tc.tile_pool(name="y_pool", bufs=LAG + 2))
             work2 = stage2.enter_context(tc.tile_pool(name="work2", bufs=3))
             small = stage2.enter_context(tc.tile_pool(name="small", bufs=2))
             ps_x = stage2.enter_context(tc.psum_pool(name="ps_x", bufs=4))
-            ps_z = stage2.enter_context(tc.psum_pool(name="ps_z", bufs=3))
-            ps_g = stage2.enter_context(tc.psum_pool(name="ps_g", bufs=1))
+            ps_z = stage2.enter_context(tc.psum_pool(name="ps_z", bufs=4))
 
+            x_tiles = {}
             y_tiles = {}
             stats_tiles = {}
+            moments = {}
             coefficients = {}
 
-            def prelu_block(cb, b):
-                if b == 0:
-                    stats = small.tile([P, N_HALVES, 6], F32)
-                    stats_tiles[cb] = stats
-                stats = stats_tiles[cb]
-                neg = work2.tile([P, BLOCK], F32)
-                y = y_pool.tile([P, BLOCK], F32)
-                y_tiles[(cb, b)] = y
+            def second_matmuls(cb, b):
                 for half in range(2):
                     h = 2 * b + half
-                    cols = slice(half * HALF, (half + 1) * HALF)
                     x = ps_x.tile([P, HALF], F32, tag="x")
                     for i in range(2):
                         w_cols = slice(i * CHANNELS + cb * P, i * CHANNELS + (cb + 1) * P)
@@ -242,6 +248,18 @@ def tile_parallelretention_pb_t_kernel(
                             start=(i == 0),
                             stop=(i == 1),
                         )
+                    x_tiles[(cb, b, half)] = x
+
+            def prelu_block(cb, b):
+                if b == 0:
+                    stats = small.tile([P, N_HALVES, 6], F32)
+                    stats_tiles[cb] = stats
+                neg = work2.tile([P, BLOCK], F32)
+                y = y_pool.tile([P, BLOCK], F32)
+                y_tiles[(cb, b)] = y
+                for half in range(2):
+                    cols = slice(half * HALF, (half + 1) * HALF)
+                    x = x_tiles[(cb, b, half)]
                     nc.scalar.activation(
                         out=neg[:, cols], in_=x[:], func=ACT.Relu, bias=neg_bp[:, cb : cb + 1], scale=-1.0
                     )
@@ -253,22 +271,32 @@ def tile_parallelretention_pb_t_kernel(
                         op0=ALU.mult,
                         op1=ALU.add,
                     )
-                    nc.vector.bn_stats(out=stats[:, h, :], in_=y[:, cols])
+                for half in range(2):
+                    cols = slice(half * HALF, (half + 1) * HALF)
+                    nc.vector.bn_stats(out=stats_tiles[cb][:, 2 * b + half, :], in_=y[:, cols])
 
-            def group_statistics(cb):
-                one = slice(cb, cb + 1)
+            def channel_moments(cb):
                 mv = small.tile([P, 2], F32)
                 nc.vector.bn_aggr(out=mv[:], in_=stats_tiles[cb][:].rearrange("p n s -> p (n s)"))
-                nc.vector.tensor_add(out=mv[:, 0:1], in0=mv[:, 0:1], in1=bp_c[:, one])
-                g1 = ps_g.tile([P, 2], F32, tag="g")
+                nc.vector.tensor_add(out=mv[:, 0:1], in0=mv[:, 0:1], in1=bp_c[:, cb : cb + 1])
+                g1 = ps_z.tile([P, 2], F32, tag="zt")
                 nc.tensor.matmul(out=g1[:], lhsT=group_avg[:], rhs=mv[:], start=True, stop=True)
+                moments[cb] = [mv, g1]
+
+            def spread_of_means(cb):
+                mv, g1 = moments[cb]
                 gm = small.tile([P, 2], F32)
                 nc.vector.tensor_copy(out=gm[:], in_=g1[:])
                 dev = small.tile([P, 2], F32)
                 nc.vector.tensor_sub(out=dev[:], in0=mv[:], in1=gm[:])
                 nc.vector.tensor_mul(out=dev[:], in0=dev[:], in1=dev[:])
-                g2 = ps_g.tile([P, 2], F32, tag="g")
+                g2 = ps_z.tile([P, 2], F32, tag="zt")
                 nc.tensor.matmul(out=g2[:], lhsT=group_avg[:], rhs=dev[:], start=True, stop=True)
+                moments[cb] = [gm, g2]
+
+            def scale_and_shift(cb):
+                gm, g2 = moments[cb]
+                one = slice(cb, cb + 1)
                 var_eps = small.tile([P, 1], F32)
                 nc.vector.scalar_tensor_tensor(
                     out=var_eps[:], in0=g2[:, 0:1], scalar=EPS, in1=gm[:, 1:2], op0=ALU.add, op1=ALU.add
@@ -289,7 +317,8 @@ def tile_parallelretention_pb_t_kernel(
             def normalise_block(cb, b):
                 y = y_tiles[(cb, b)]
                 scale, shift = coefficients[cb]
-                nc.gpsimd.tensor_scalar(
+                engine = nc.vector if cb == N_CB - 1 else nc.gpsimd
+                engine.tensor_scalar(
                     out=y[:], in0=y[:], scalar1=scale[:, 0:1], scalar2=shift[:, 0:1], op0=ALU.mult, op1=ALU.add
                 )
                 z = work2.tile([P, TILES, P], F32)
@@ -306,13 +335,20 @@ def tile_parallelretention_pb_t_kernel(
                     in_=z[:],
                 )
 
+            parts = (channel_moments, spread_of_means, scale_and_shift)
             steps = N_CB * N_BLOCKS
+            second_matmuls(0, 0)
             for step in range(steps + LAG):
                 if step < steps:
                     cb, b = divmod(step, N_BLOCKS)
                     prelu_block(cb, b)
-                    if b == N_BLOCKS - 1:
-                        group_statistics(cb)
                 if step >= LAG:
                     cb, b = divmod(step - LAG, N_BLOCKS)
                     normalise_block(cb, b)
+                if step + 1 < steps:
+                    cb, b = divmod(step + 1, N_BLOCKS)
+                    second_matmuls(cb, b)
+                for part in range(STAT_PARTS):
+                    cb, b = divmod(step - part, N_BLOCKS)
+                    if b == N_BLOCKS - 1 and 0 <= cb < N_CB:
+                        parts[part](cb)

@@ -44,7 +44,6 @@ def tile_parallelretention_pb_t_kernel(
 ):
     nc = tc.nc
     with ExitStack() as whole:
-        whole.enter_context(tc.manual_schedule())
         keep = whole.enter_context(tc.tile_pool(name="keep", bufs=1))
 
         ident = keep.tile([P, P], F32)

@@ -13,8 +13,11 @@ ACT = mybir.ActivationFunctionType
 ALU = mybir.AluOpType
 
 P = 128
+PACK = 4
 ROWS = 8192
 K = 512
+WORDS = K // 2
+FEATURES = 256
 CHANNELS = 512
 GROUP = 32
 EPS = 1e-5
@@ -23,19 +26,21 @@ BLOCK = 1024
 TILES = BLOCK // P
 N_BLOCKS = ROWS // BLOCK
 HALF = 512
+HALF_TILES = HALF // P
 N_HALVES = ROWS // HALF
-PAIR = 256
+PAIR = 2 * P
 N_CB = CHANNELS // P
 STAT_PARTS = 3
 LAG = N_BLOCKS + STAT_PARTS
+BN_STATS_DIM = 6
 
-FLOPS = 2 * ROWS * (K * 256 * 2 + K * CHANNELS)
+FLOPS = 2 * ROWS * (K * FEATURES * 2 + K * CHANNELS)
 
 
 def transpose_row_tiles(nc, bank, words, first_tile, ident):
     for i in range(2):
         for u in range(2):
-            start = (first_tile + i) * (K // 2) + u * P
+            start = (first_tile + i) * WORDS + u * P
             nc.tensor.transpose(bank[:, u, i * P : (i + 1) * P], words[:, start : start + P], ident[:])
 
 
@@ -43,12 +48,20 @@ def tile_parallelretention_pb_t_kernel(
     tc, h_ret, h_prime, Wr, br, Wc, bc, Wp, bp, prelu_w, gn_w, gn_b, out
 ):
     nc = tc.nc
-    with ExitStack() as whole:
-        keep = whole.enter_context(tc.tile_pool(name="keep", bufs=1))
+    with ExitStack() as pools:
+        keep = pools.enter_context(tc.tile_pool(name="keep", bufs=1))
+        streamed = pools.enter_context(tc.tile_pool(name="streamed", bufs=3))
+        work = pools.enter_context(tc.tile_pool(name="work", bufs=2))
+        y_pool = pools.enter_context(tc.tile_pool(name="y_pool", bufs=LAG + 2))
+        small = pools.enter_context(tc.tile_pool(name="small", bufs=2))
+        ps_t = pools.enter_context(tc.psum_pool(name="ps_t", bufs=4))
+        ps_mx = pools.enter_context(tc.psum_pool(name="ps_mx", bufs=4))
 
         ident = keep.tile([P, P], F32)
         make_identity(nc, ident[:])
-
+        warm = keep.tile([P, 1], F32)
+        nc.vector.memset(warm[:], 0.0)
+        nc.scalar.activation(out=warm[:], in_=warm[:], func=ACT.Gelu)
         group_avg = keep.tile([P, P], F32)
         nc.vector.memset(group_avg[:], 0.0)
         for g in range(P // GROUP):
@@ -56,6 +69,12 @@ def tile_parallelretention_pb_t_kernel(
             nc.vector.memset(group_avg[span, span], 1.0 / GROUP)
         neg_half = keep.tile([P, 1], F32)
         nc.vector.memset(neg_half[:], -0.5)
+        rows_bf = keep.tile([P, P], BF16)
+        nc.vector.memset(rows_bf[:], 0.0)
+        ac_grouped = []
+        for i in range(2):
+            ac_grouped.append(keep.tile([P, 2, HALF, PACK], BF16, name="ac_grouped%d" % i, align_bytes=64))
+            nc.vector.memset(ac_grouped[i][:].rearrange("p i c t -> p (i c t)").bitcast(I32), 0)
 
         w1_codes = keep.tile([P, 4 * P], U32, align_bytes=64)
         w1_scales = keep.tile([P, 4 * P], U8, align_bytes=64)
@@ -67,287 +86,269 @@ def tile_parallelretention_pb_t_kernel(
             ac_codes.append(keep.tile([P, 2 * HALF], U32, name="ac_codes%d" % h, align_bytes=64))
             ac_scales.append(keep.tile([P, 2 * HALF], U8, name="ac_scales%d" % h, align_bytes=64))
         bias1 = keep.tile([P, 4], F32)
-        chan = keep.tile([P, 16], F32)
+        chan = keep.tile([P, 4 * N_CB], F32)
         neg_bp = keep.tile([P, N_CB], F32)
         one_minus_w = keep.tile([P, N_CB], F32)
-        bp_c = chan[:, 0:4]
-        gn_w_c = chan[:, 8:12]
-        gn_b_c = chan[:, 12:16]
+        bp_c = chan[:, 0:N_CB]
+        prelu_w_c = chan[:, N_CB : 2 * N_CB]
+        gn_w_c = chan[:, 2 * N_CB : 3 * N_CB]
+        gn_b_c = chan[:, 3 * N_CB : 4 * N_CB]
 
-        with ExitStack() as stage1:
-            once = stage1.enter_context(tc.tile_pool(name="once", bufs=1))
-            loads = stage1.enter_context(tc.tile_pool(name="loads", bufs=4))
-            work = stage1.enter_context(tc.tile_pool(name="work", bufs=2))
-            ps_t = stage1.enter_context(tc.psum_pool(name="ps_t", bufs=4))
-            ps_1 = stage1.enter_context(tc.psum_pool(name="ps_1", bufs=4))
+        h_tiles = {}
+        h_quantised = {}
+        x_tiles = {}
+        y_tiles = {}
+        stats_tiles = {}
+        moments = {}
+        coefficients = {}
 
-            warm = once.tile([P, 1], F32)
-            nc.vector.memset(warm[:], 0.0)
-            nc.scalar.activation(out=warm[:], in_=warm[:], func=ACT.Gelu)
-
-            rows_bf = once.tile([P, P], BF16)
-            nc.vector.memset(rows_bf[:], 0.0)
-            ac_grouped = []
-            for i in range(2):
-                ac_grouped.append(once.tile([P, 2, HALF, 4], BF16, name="ac_grouped%d" % i, align_bytes=64))
-                nc.vector.memset(ac_grouped[i][:].rearrange("p i c t -> p (i c t)").bitcast(I32), 0)
-            wp_grouped = once.tile([P, 2 * CHANNELS * 4], BF16, align_bytes=64)
-            nc.vector.memset(wp_grouped[:].bitcast(I32), 0)
-
-            w1_sb = once.tile([P, 4 * K], BF16)
-            nc.sync.dma_start(out=w1_sb[:, 0 : 2 * K], in_=Wr.rearrange("(p t) k -> p (t k)", t=2))
-            nc.sync.dma_start(out=w1_sb[:, 2 * K : 4 * K], in_=Wc.rearrange("(p t) k -> p (t k)", t=2))
-            br_bf = once.tile([P, 2], BF16)
-            bc_bf = once.tile([P, 2], BF16)
-            nc.scalar.dma_start(out=br_bf[:], in_=br.rearrange("(p t) -> p t", t=2))
-            nc.scalar.dma_start(out=bc_bf[:], in_=bc.rearrange("(p t) -> p t", t=2))
-
-            h_tiles = {}
-
-            def load_half(h):
-                b, half = divmod(h, 2)
-                rows = slice(b * BLOCK, (b + 1) * BLOCK)
-                tiles = slice(4 * half, 4 * half + 4)
-                hr = loads.tile([P, 4, K], BF16)
-                nc.sync.dma_start(out=hr[:], in_=h_ret[rows, :].rearrange("(p j) k -> p j k", j=TILES)[:, tiles, :])
-                hp = loads.tile([P, 4, K], BF16)
-                nc.sync.dma_start(out=hp[:], in_=h_prime[rows, :].rearrange("(p j) k -> p j k", j=TILES)[:, tiles, :])
-                h_tiles[h] = (hr, hp)
-
-            load_half(0)
-            load_half(1)
-            wp_sb = once.tile([P, N_CB * K], BF16)
+        def load_half(h):
+            b, half = divmod(h, 2)
+            rows = slice(b * BLOCK, (b + 1) * BLOCK)
+            tiles = slice(HALF_TILES * half, HALF_TILES * (half + 1))
+            hr = streamed.tile([P, HALF_TILES * K], BF16, tag="first")
             nc.sync.dma_start(
-                out=wp_sb[:].rearrange("p (c k) -> p c k", c=N_CB), in_=Wp.rearrange("(c p) k -> p c k", p=P)
+                out=hr[:].rearrange("p (j k) -> p j k", j=HALF_TILES),
+                in_=h_ret[rows, :].rearrange("(p j) k -> p j k", j=TILES)[:, tiles, :],
             )
-            load_half(2)
-            for v, vec in enumerate((bp, prelu_w, gn_w, gn_b)):
-                nc.scalar.dma_start(out=rows_bf[4 * v : 4 * v + 4, :], in_=vec.rearrange("(c p) -> c p", p=P))
+            hp = streamed.tile([P, HALF_TILES * K], BF16, tag="second")
+            nc.sync.dma_start(
+                out=hp[:].rearrange("p (j k) -> p j k", j=HALF_TILES),
+                in_=h_prime[rows, :].rearrange("(p j) k -> p j k", j=TILES)[:, tiles, :],
+            )
+            h_tiles[h] = (hr, hp)
 
-            w1_grouped = once.tile([P, 4 * P * 4], BF16, align_bytes=64)
-            w1_g32 = w1_grouped[:].bitcast(F32).rearrange("p (c u) -> p c u", u=2)
-            for pair in range(2):
-                bank = ps_t.tile([P, 2, PAIR], F32, tag="ht")
-                transpose_row_tiles(nc, bank, w1_sb[:].bitcast(F32), 2 * pair, ident)
-                nc.vector.tensor_copy(
-                    out=w1_g32[:, pair * PAIR : (pair + 1) * PAIR, :], in_=bank[:].rearrange("p u c -> p c u")
-                )
-            nc.vector.quantize_mx(out=w1_codes[:].bitcast(FP8X4), scales=w1_scales[:], in_=w1_grouped[:])
-            nc.vector.tensor_copy(out=bias1[:, 0:2], in_=br_bf[:])
-            nc.vector.tensor_copy(out=bias1[:, 2:4], in_=bc_bf[:])
-
-            h_quantised = {}
-
-            def transpose_and_quantise(h):
-                if h + 3 < N_HALVES:
-                    load_half(h + 3)
-                grouped = work.tile([P, 2 * HALF * 4], BF16, align_bytes=64)
-                g32 = grouped[:].bitcast(F32).rearrange("p (i c u) -> p i c u", i=2, u=2)
-                for i in range(2):
-                    words = h_tiles[h][i][:].rearrange("p j k -> p (j k)").bitcast(F32)
-                    for pair in range(2):
-                        bank = ps_t.tile([P, 2, PAIR], F32, tag="ht")
-                        transpose_row_tiles(nc, bank, words, 2 * pair, ident)
-                        nc.scalar.copy(
-                            out=g32[:, i, pair * PAIR : (pair + 1) * PAIR, :],
-                            in_=bank[:].rearrange("p u c -> p c u"),
-                        )
-                h_codes = work.tile([P, 2 * HALF], U32, align_bytes=64)
-                h_scales = work.tile([P, 2 * HALF], U8, align_bytes=64)
-                nc.vector.quantize_mx(out=h_codes[:].bitcast(FP8X4), scales=h_scales[:], in_=grouped[:])
-                h_quantised[h] = (h_codes, h_scales)
-
-            def first_matmuls(h):
-                h_codes, h_scales = h_quantised[h]
-                staged = work.tile([P, 4, HALF], BF16)
-                for i in range(2):
-                    for t in range(2):
-                        m = 2 * i + t
-                        acc = ps_1.tile([P, HALF], F32, tag="s1")
-                        nc.tensor.matmul_mx(
-                            out=acc[:],
-                            lhsT=w1_codes[:, m * P : (m + 1) * P].bitcast(FP8X4),
-                            lhsT_scale=w1_scales[:, m * P : (m + 1) * P],
-                            rhs=h_codes[:, i * HALF : (i + 1) * HALF].bitcast(FP8X4),
-                            rhs_scale=h_scales[:, i * HALF : (i + 1) * HALF],
-                            start=True,
-                            stop=True,
-                        )
-                        nc.scalar.activation(
-                            out=staged[:, m, :],
-                            in_=acc[:],
-                            func=ACT.Gelu if i == 0 else ACT.Identity,
-                            bias=bias1[:, m : m + 1],
-                            scale=1.0,
-                        )
-                    nc.vector.tensor_copy(
-                        out=ac_grouped[h % 2][:, i, :, 0:2],
-                        in_=staged[:, 2 * i : 2 * i + 2, :].rearrange("p t c -> p c t"),
-                    )
-
-            def quantise_ac(h):
-                nc.vector.quantize_mx(
-                    out=ac_codes[h][:].bitcast(FP8X4),
-                    scales=ac_scales[h][:],
-                    in_=ac_grouped[h % 2][:].rearrange("p i c t -> p (i c t)"),
-                )
-
-            def prepare_wp_and_channel_vectors():
-                wp_g32 = wp_grouped[:].bitcast(F32).rearrange("p (i c s) -> p i c s", i=2, s=2)
+        def transpose_and_quantise(h):
+            grouped = work.tile([P, 2 * HALF * PACK], BF16, tag="grouped", align_bytes=64)
+            g32 = grouped[:].bitcast(F32).rearrange("p (i c u) -> p i c u", i=2, u=2)
+            for i in range(2):
+                words = h_tiles[h][i][:].bitcast(F32)
                 for pair in range(2):
-                    bank = ps_t.tile([P, 2, PAIR], F32, tag="ht")
-                    transpose_row_tiles(nc, bank, wp_sb[:].bitcast(F32), 2 * pair, ident)
-                    nc.vector.tensor_copy(out=wp_g32[:, :, pair * PAIR : (pair + 1) * PAIR, 0], in_=bank[:])
-                nc.vector.quantize_mx(out=wp_codes[:].bitcast(FP8X4), scales=wp_scales[:], in_=wp_grouped[:])
-                rows_f32 = once.tile([P, P], F32)
-                nc.vector.tensor_copy(out=rows_f32[:], in_=rows_bf[:])
-                bank = ps_t.tile([P, 2, PAIR], F32, tag="ht")
-                nc.tensor.transpose(bank[:, 0, 0:P], rows_f32[:], ident[:])
-                nc.vector.tensor_copy(out=chan[:], in_=bank[:, 0, 0:16])
-                nc.vector.tensor_scalar(out=neg_bp[:], in0=chan[:, 0:4], scalar1=-1.0, scalar2=None, op0=ALU.mult)
-                nc.vector.tensor_scalar(
-                    out=one_minus_w[:], in0=chan[:, 4:8], scalar1=-1.0, scalar2=1.0, op0=ALU.mult, op1=ALU.add
-                )
+                    bank = ps_t.tile([P, 2, PAIR], F32, tag="t")
+                    transpose_row_tiles(nc, bank, words, 2 * pair, ident)
+                    nc.scalar.copy(
+                        out=g32[:, i, pair * PAIR : (pair + 1) * PAIR, :],
+                        in_=bank[:].rearrange("p u c -> p c u"),
+                    )
+            h_codes = work.tile([P, 2 * HALF], U32, align_bytes=64)
+            h_scales = work.tile([P, 2 * HALF], U8, align_bytes=64)
+            nc.vector.quantize_mx(out=h_codes[:].bitcast(FP8X4), scales=h_scales[:], in_=grouped[:])
+            h_quantised[h] = (h_codes, h_scales)
+            if h + 2 < N_HALVES:
+                load_half(h + 2)
 
-            for i in range(N_HALVES + 2):
-                if i < N_HALVES:
-                    transpose_and_quantise(i)
-                if i == 0:
-                    prepare_wp_and_channel_vectors()
-                if i >= 2:
-                    quantise_ac(i - 2)
-                if 1 <= i <= N_HALVES:
-                    first_matmuls(i - 1)
-
-        with ExitStack() as stage2:
-            y_pool = stage2.enter_context(tc.tile_pool(name="y_pool", bufs=LAG + 2))
-            work2 = stage2.enter_context(tc.tile_pool(name="work2", bufs=3))
-            small = stage2.enter_context(tc.tile_pool(name="small", bufs=2))
-            ps_x = stage2.enter_context(tc.psum_pool(name="ps_x", bufs=4))
-            ps_z = stage2.enter_context(tc.psum_pool(name="ps_z", bufs=4))
-
-            x_tiles = {}
-            y_tiles = {}
-            stats_tiles = {}
-            moments = {}
-            coefficients = {}
-
-            def second_matmuls(cb, b):
-                for half in range(2):
-                    h = 2 * b + half
-                    x = ps_x.tile([P, HALF], F32, tag="x")
-                    for i in range(2):
-                        w_cols = slice(i * CHANNELS + cb * P, i * CHANNELS + (cb + 1) * P)
-                        nc.tensor.matmul_mx(
-                            out=x[:],
-                            lhsT=wp_codes[:, w_cols].bitcast(FP8X4),
-                            lhsT_scale=wp_scales[:, w_cols],
-                            rhs=ac_codes[h][:, i * HALF : (i + 1) * HALF].bitcast(FP8X4),
-                            rhs_scale=ac_scales[h][:, i * HALF : (i + 1) * HALF],
-                            start=(i == 0),
-                            stop=(i == 1),
-                        )
-                    x_tiles[(cb, b, half)] = x
-
-            def prelu_block(cb, b):
-                if b == 0:
-                    stats = small.tile([P, N_HALVES, 6], F32)
-                    stats_tiles[cb] = stats
-                neg = work2.tile([P, BLOCK], F32)
-                y = y_pool.tile([P, BLOCK], F32)
-                y_tiles[(cb, b)] = y
-                for half in range(2):
-                    cols = slice(half * HALF, (half + 1) * HALF)
-                    x = x_tiles[(cb, b, half)]
+        def first_matmuls(h):
+            h_codes, h_scales = h_quantised[h]
+            staged = work.tile([P, 4, HALF], BF16)
+            for i in range(2):
+                for t in range(2):
+                    m = 2 * i + t
+                    acc = ps_mx.tile([P, HALF], F32, tag="mx")
+                    nc.tensor.matmul_mx(
+                        out=acc[:],
+                        lhsT=w1_codes[:, m * P : (m + 1) * P].bitcast(FP8X4),
+                        lhsT_scale=w1_scales[:, m * P : (m + 1) * P],
+                        rhs=h_codes[:, i * HALF : (i + 1) * HALF].bitcast(FP8X4),
+                        rhs_scale=h_scales[:, i * HALF : (i + 1) * HALF],
+                        start=True,
+                        stop=True,
+                    )
                     nc.scalar.activation(
-                        out=neg[:, cols], in_=x[:], func=ACT.Relu, bias=neg_bp[:, cb : cb + 1], scale=-1.0
+                        out=staged[:, m, :],
+                        in_=acc[:],
+                        func=ACT.Gelu if i == 0 else ACT.Identity,
+                        bias=bias1[:, m : m + 1],
+                        scale=1.0,
                     )
-                    nc.vector.scalar_tensor_tensor(
-                        out=y[:, cols],
-                        in0=neg[:, cols],
-                        scalar=one_minus_w[:, cb : cb + 1],
-                        in1=x[:],
-                        op0=ALU.mult,
-                        op1=ALU.add,
+                nc.vector.tensor_copy(
+                    out=ac_grouped[h % 2][:, i, :, 0:2],
+                    in_=staged[:, 2 * i : 2 * i + 2, :].rearrange("p t c -> p c t"),
+                )
+
+        def quantise_ac(h):
+            nc.vector.quantize_mx(
+                out=ac_codes[h][:].bitcast(FP8X4),
+                scales=ac_scales[h][:],
+                in_=ac_grouped[h % 2][:].rearrange("p i c t -> p (i c t)"),
+            )
+
+        def second_matmuls(cb, b):
+            for half in range(2):
+                h = 2 * b + half
+                x = ps_mx.tile([P, HALF], F32, tag="mx")
+                for i in range(2):
+                    w_cols = slice(i * CHANNELS + cb * P, i * CHANNELS + (cb + 1) * P)
+                    nc.tensor.matmul_mx(
+                        out=x[:],
+                        lhsT=wp_codes[:, w_cols].bitcast(FP8X4),
+                        lhsT_scale=wp_scales[:, w_cols],
+                        rhs=ac_codes[h][:, i * HALF : (i + 1) * HALF].bitcast(FP8X4),
+                        rhs_scale=ac_scales[h][:, i * HALF : (i + 1) * HALF],
+                        start=(i == 0),
+                        stop=(i == 1),
                     )
-                for half in range(2):
-                    cols = slice(half * HALF, (half + 1) * HALF)
-                    nc.vector.bn_stats(out=stats_tiles[cb][:, 2 * b + half, :], in_=y[:, cols])
+                x_tiles[(cb, b, half)] = x
 
-            def channel_moments(cb):
-                mv = small.tile([P, 2], F32)
-                nc.vector.bn_aggr(out=mv[:], in_=stats_tiles[cb][:].rearrange("p n s -> p (n s)"))
-                nc.vector.tensor_add(out=mv[:, 0:1], in0=mv[:, 0:1], in1=bp_c[:, cb : cb + 1])
-                g1 = ps_z.tile([P, 2], F32, tag="zt")
-                nc.tensor.matmul(out=g1[:], lhsT=group_avg[:], rhs=mv[:], start=True, stop=True)
-                moments[cb] = [mv, g1]
-
-            def spread_of_means(cb):
-                mv, g1 = moments[cb]
-                gm = small.tile([P, 2], F32)
-                nc.vector.tensor_copy(out=gm[:], in_=g1[:])
-                dev = small.tile([P, 2], F32)
-                nc.vector.tensor_sub(out=dev[:], in0=mv[:], in1=gm[:])
-                nc.vector.tensor_mul(out=dev[:], in0=dev[:], in1=dev[:])
-                g2 = ps_z.tile([P, 2], F32, tag="zt")
-                nc.tensor.matmul(out=g2[:], lhsT=group_avg[:], rhs=dev[:], start=True, stop=True)
-                moments[cb] = [gm, g2]
-
-            def scale_and_shift(cb):
-                gm, g2 = moments[cb]
-                one = slice(cb, cb + 1)
-                var_eps = small.tile([P, 1], F32)
+        def prelu_block(cb, b):
+            if b == 0:
+                stats = small.tile([P, N_HALVES, BN_STATS_DIM], F32)
+                stats_tiles[cb] = stats
+            neg = work.tile([P, BLOCK], F32)
+            y = y_pool.tile([P, BLOCK], F32)
+            y_tiles[(cb, b)] = y
+            for half in range(2):
+                cols = slice(half * HALF, (half + 1) * HALF)
+                x = x_tiles[(cb, b, half)]
+                nc.scalar.activation(
+                    out=neg[:, cols], in_=x[:], func=ACT.Relu, bias=neg_bp[:, cb : cb + 1], scale=-1.0
+                )
                 nc.vector.scalar_tensor_tensor(
-                    out=var_eps[:], in0=g2[:, 0:1], scalar=EPS, in1=gm[:, 1:2], op0=ALU.add, op1=ALU.add
+                    out=y[:, cols],
+                    in0=neg[:, cols],
+                    scalar=one_minus_w[:, cb : cb + 1],
+                    in1=x[:],
+                    op0=ALU.mult,
+                    op1=ALU.add,
                 )
-                centre = small.tile([P, 1], F32)
-                nc.vector.tensor_sub(out=centre[:], in0=bp_c[:, one], in1=gm[:, 0:1])
-                rstd = small.tile([P, 1], F32)
-                nc.gpsimd.tensor_tensor(out=rstd[:], in0=var_eps[:], in1=neg_half[:], op=ALU.pow)
-                scale = small.tile([P, 1], F32)
-                nc.gpsimd.tensor_tensor(out=scale[:], in0=rstd[:], in1=gn_w_c[:, one], op=ALU.mult)
-                shift = small.tile([P, 1], F32)
-                nc.gpsimd.tensor_scalar(
-                    out=shift[:], in0=centre[:], scalar1=scale[:, 0:1], scalar2=gn_b_c[:, one],
-                    op0=ALU.mult, op1=ALU.add,
-                )
-                coefficients[cb] = (scale, shift)
+            for half in range(2):
+                cols = slice(half * HALF, (half + 1) * HALF)
+                nc.vector.bn_stats(out=stats_tiles[cb][:, 2 * b + half, :], in_=y[:, cols])
 
-            def normalise_block(cb, b):
-                y = y_tiles[(cb, b)]
-                scale, shift = coefficients[cb]
-                engine = nc.vector if cb == N_CB - 1 else nc.gpsimd
-                engine.tensor_scalar(
-                    out=y[:], in0=y[:], scalar1=scale[:, 0:1], scalar2=shift[:, 0:1], op0=ALU.mult, op1=ALU.add
-                )
-                z = work2.tile([P, TILES, P], F32)
-                for half in range(2):
-                    zt = ps_z.tile([P, 4, P], F32, tag="zt")
-                    for j in range(4):
-                        col = (4 * half + j) * P
-                        nc.tensor.transpose(zt[:, j, :], y[:, col : col + P], ident[:])
-                    nc.scalar.copy(out=z[:, 4 * half : 4 * half + 4, :], in_=zt[:])
-                nc.sync.dma_start(
-                    out=out[b * BLOCK : (b + 1) * BLOCK, cb * P : (cb + 1) * P].rearrange(
-                        "(p j) c -> p j c", j=TILES
-                    ),
-                    in_=z[:],
-                )
+        def channel_moments(cb):
+            mv = small.tile([P, 2], F32)
+            nc.vector.bn_aggr(out=mv[:], in_=stats_tiles[cb][:].rearrange("p n s -> p (n s)"))
+            nc.vector.tensor_add(out=mv[:, 0:1], in0=mv[:, 0:1], in1=bp_c[:, cb : cb + 1])
+            g1 = ps_t.tile([P, 2], F32, tag="t")
+            nc.tensor.matmul(out=g1[:], lhsT=group_avg[:], rhs=mv[:], start=True, stop=True)
+            moments[cb] = [mv, g1]
 
-            parts = (channel_moments, spread_of_means, scale_and_shift)
-            steps = N_CB * N_BLOCKS
-            second_matmuls(0, 0)
-            for step in range(steps + LAG):
-                if step < steps:
-                    cb, b = divmod(step, N_BLOCKS)
-                    prelu_block(cb, b)
-                if step >= LAG:
-                    cb, b = divmod(step - LAG, N_BLOCKS)
-                    normalise_block(cb, b)
-                if step + 1 < steps:
-                    cb, b = divmod(step + 1, N_BLOCKS)
-                    second_matmuls(cb, b)
-                for part in range(STAT_PARTS):
-                    cb, b = divmod(step - part, N_BLOCKS)
-                    if b == N_BLOCKS - 1 and 0 <= cb < N_CB:
-                        parts[part](cb)
+        def spread_of_means(cb):
+            mv, g1 = moments[cb]
+            gm = small.tile([P, 2], F32)
+            nc.vector.tensor_copy(out=gm[:], in_=g1[:])
+            dev = small.tile([P, 2], F32)
+            nc.vector.tensor_sub(out=dev[:], in0=mv[:], in1=gm[:])
+            nc.vector.tensor_mul(out=dev[:], in0=dev[:], in1=dev[:])
+            g2 = ps_t.tile([P, 2], F32, tag="t")
+            nc.tensor.matmul(out=g2[:], lhsT=group_avg[:], rhs=dev[:], start=True, stop=True)
+            moments[cb] = [gm, g2]
+
+        def scale_and_shift(cb):
+            gm, g2 = moments[cb]
+            one = slice(cb, cb + 1)
+            var_eps = small.tile([P, 1], F32)
+            nc.vector.scalar_tensor_tensor(
+                out=var_eps[:], in0=g2[:, 0:1], scalar=EPS, in1=gm[:, 1:2], op0=ALU.add, op1=ALU.add
+            )
+            centre = small.tile([P, 1], F32)
+            nc.vector.tensor_sub(out=centre[:], in0=bp_c[:, one], in1=gm[:, 0:1])
+            rstd = small.tile([P, 1], F32)
+            nc.gpsimd.tensor_tensor(out=rstd[:], in0=var_eps[:], in1=neg_half[:], op=ALU.pow)
+            scale = small.tile([P, 1], F32)
+            nc.gpsimd.tensor_tensor(out=scale[:], in0=rstd[:], in1=gn_w_c[:, one], op=ALU.mult)
+            shift = small.tile([P, 1], F32)
+            nc.gpsimd.tensor_scalar(
+                out=shift[:], in0=centre[:], scalar1=scale[:, 0:1], scalar2=gn_b_c[:, one],
+                op0=ALU.mult, op1=ALU.add,
+            )
+            coefficients[cb] = (scale, shift)
+
+        def normalise_block(cb, b):
+            y = y_tiles[(cb, b)]
+            scale, shift = coefficients[cb]
+            engine = nc.vector if cb == N_CB - 1 else nc.gpsimd
+            engine.tensor_scalar(
+                out=y[:], in0=y[:], scalar1=scale[:, 0:1], scalar2=shift[:, 0:1], op0=ALU.mult, op1=ALU.add
+            )
+            z = streamed.tile([P, TILES, P], F32, tag="first")
+            for half in range(2):
+                zt = ps_t.tile([P, HALF_TILES, P], F32, tag="t")
+                for j in range(HALF_TILES):
+                    col = (HALF_TILES * half + j) * P
+                    nc.tensor.transpose(zt[:, j, :], y[:, col : col + P], ident[:])
+                nc.scalar.copy(out=z[:, HALF_TILES * half : HALF_TILES * (half + 1), :], in_=zt[:])
+            nc.sync.dma_start(
+                out=out[b * BLOCK : (b + 1) * BLOCK, cb * P : (cb + 1) * P].rearrange(
+                    "(p j) c -> p j c", j=TILES
+                ),
+                in_=z[:],
+            )
+
+        def prepare_wp_and_channel_vectors():
+            wp_grouped = work.tile([P, 2 * CHANNELS * PACK], BF16, tag="grouped", align_bytes=64)
+            nc.vector.memset(wp_grouped[:].bitcast(I32), 0)
+            wp_g32 = wp_grouped[:].bitcast(F32).rearrange("p (i c s) -> p i c s", i=2, s=2)
+            for pair in range(2):
+                bank = ps_t.tile([P, 2, PAIR], F32, tag="t")
+                transpose_row_tiles(nc, bank, wp_sb[:].bitcast(F32), 2 * pair, ident)
+                nc.vector.tensor_copy(out=wp_g32[:, :, pair * PAIR : (pair + 1) * PAIR, 0], in_=bank[:])
+            nc.vector.quantize_mx(out=wp_codes[:].bitcast(FP8X4), scales=wp_scales[:], in_=wp_grouped[:])
+            rows_f32 = keep.tile([P, P], F32)
+            nc.vector.tensor_copy(out=rows_f32[:], in_=rows_bf[:])
+            bank = ps_t.tile([P, 2, PAIR], F32, tag="t")
+            nc.tensor.transpose(bank[:, 0, 0:P], rows_f32[:], ident[:])
+            nc.vector.tensor_copy(out=chan[:], in_=bank[:, 0, 0 : 4 * N_CB])
+            nc.vector.tensor_scalar(out=neg_bp[:], in0=bp_c, scalar1=-1.0, scalar2=None, op0=ALU.mult)
+            nc.vector.tensor_scalar(
+                out=one_minus_w[:], in0=prelu_w_c, scalar1=-1.0, scalar2=1.0, op0=ALU.mult, op1=ALU.add
+            )
+
+        load_half(0)
+        w1_sb = streamed.tile([P, 4 * K], BF16, tag="first")
+        nc.sync.dma_start(out=w1_sb[:, 0 : 2 * K], in_=Wr.rearrange("(p t) k -> p (t k)", t=2))
+        nc.sync.dma_start(out=w1_sb[:, 2 * K : 4 * K], in_=Wc.rearrange("(p t) k -> p (t k)", t=2))
+        br_bf = keep.tile([P, 2], BF16)
+        bc_bf = keep.tile([P, 2], BF16)
+        nc.scalar.dma_start(out=br_bf[:], in_=br.rearrange("(p t) -> p t", t=2))
+        nc.scalar.dma_start(out=bc_bf[:], in_=bc.rearrange("(p t) -> p t", t=2))
+        load_half(1)
+        wp_sb = streamed.tile([P, N_CB * K], BF16, tag="second")
+        nc.sync.dma_start(
+            out=wp_sb[:].rearrange("p (c k) -> p c k", c=N_CB), in_=Wp.rearrange("(c p) k -> p c k", p=P)
+        )
+        for v, vec in enumerate((bp, prelu_w, gn_w, gn_b)):
+            nc.scalar.dma_start(
+                out=rows_bf[N_CB * v : N_CB * (v + 1), :], in_=vec.rearrange("(c p) -> c p", p=P)
+            )
+
+        w1_grouped = work.tile([P, 4 * P * PACK], BF16, tag="grouped", align_bytes=64)
+        w1_g32 = w1_grouped[:].bitcast(F32).rearrange("p (c u) -> p c u", u=2)
+        for pair in range(2):
+            bank = ps_t.tile([P, 2, PAIR], F32, tag="t")
+            transpose_row_tiles(nc, bank, w1_sb[:].bitcast(F32), 2 * pair, ident)
+            nc.vector.tensor_copy(
+                out=w1_g32[:, pair * PAIR : (pair + 1) * PAIR, :], in_=bank[:].rearrange("p u c -> p c u")
+            )
+        nc.vector.quantize_mx(out=w1_codes[:].bitcast(FP8X4), scales=w1_scales[:], in_=w1_grouped[:])
+        nc.vector.tensor_copy(out=bias1[:, 0:2], in_=br_bf[:])
+        nc.vector.tensor_copy(out=bias1[:, 2:4], in_=bc_bf[:])
+
+        for i in range(N_HALVES + 3):
+            if i < N_HALVES:
+                transpose_and_quantise(i)
+            if i == 0:
+                prepare_wp_and_channel_vectors()
+            if 2 <= i < N_HALVES + 2:
+                quantise_ac(i - 2)
+            if 1 <= i <= N_HALVES:
+                first_matmuls(i - 1)
+            if i >= 3 and i % 2 == 0:
+                second_matmuls(0, (i - 3) // 2)
+                prelu_block(0, (i - 3) // 2)
+        channel_moments(0)
+
+        steps = N_CB * N_BLOCKS
+        second_matmuls(1, 0)
+        for step in range(N_BLOCKS, steps + LAG):
+            if step < steps:
+                prelu_block(step // N_BLOCKS, step % N_BLOCKS)
+            if step >= LAG:
+                normalise_block((step - LAG) // N_BLOCKS, (step - LAG) % N_BLOCKS)
+            if step + 1 < steps:
+                second_matmuls((step + 1) // N_BLOCKS, (step + 1) % N_BLOCKS)
+            if step % N_BLOCKS == N_BLOCKS - 1 and step < steps:
+                channel_moments(step // N_BLOCKS)
+            if step % N_BLOCKS == 0 and step <= steps:
+                spread_of_means(step // N_BLOCKS - 1)
+            if step % N_BLOCKS == 1 and step <= steps + 1:
+                scale_and_shift(step // N_BLOCKS - 1)

@@ -13,6 +13,7 @@ ACT = mybir.ActivationFunctionType
 ALU = mybir.AluOpType
 
 P = 128
+LOW = 64
 PACK = 4
 ROWS = 8192
 K = 512
@@ -30,8 +31,10 @@ HALF_TILES = HALF // P
 N_HALVES = ROWS // HALF
 PAIR = 2 * P
 N_CB = CHANNELS // P
+WP_VERSION = {(0, 0): 0, (1, 1): 1, (1, 0): 2, (0, 1): 3}
 STAT_PARTS = 3
 LAG = N_BLOCKS + STAT_PARTS
+BLOCK32 = 16
 BN_STATS_DIM = 6
 
 FLOPS = 2 * ROWS * (K * FEATURES * 2 + K * CHANNELS)
@@ -44,6 +47,15 @@ def transpose_row_tiles(nc, bank, words, first_tile, ident):
             nc.tensor.transpose(bank[:, u, i * P : (i + 1) * P], words[:, start : start + P], ident[:])
 
 
+def transpose_row_tiles_by_fours(nc, bank, words, first_tile, ident):
+    for i in range(2):
+        for u in range(2):
+            start = (first_tile + i) * WORDS
+            nc.tensor.transpose(
+                bank[:, u, i * P : (i + 1) * P], words[:, start + u : start + WORDS : 2], ident[:]
+            )
+
+
 def tile_parallelretention_pb_t_kernel(
     tc, h_ret, h_prime, Wr, br, Wc, bc, Wp, bp, prelu_w, gn_w, gn_b, out
 ):
@@ -52,6 +64,7 @@ def tile_parallelretention_pb_t_kernel(
         keep = pools.enter_context(tc.tile_pool(name="keep", bufs=1))
         streamed = pools.enter_context(tc.tile_pool(name="streamed", bufs=3))
         work = pools.enter_context(tc.tile_pool(name="work", bufs=2))
+        halves = pools.enter_context(tc.tile_pool(name="halves", bufs=4))
         y_pool = pools.enter_context(tc.tile_pool(name="y_pool", bufs=LAG + 2))
         small = pools.enter_context(tc.tile_pool(name="small", bufs=2))
         ps_t = pools.enter_context(tc.psum_pool(name="ps_t", bufs=4))
@@ -71,21 +84,19 @@ def tile_parallelretention_pb_t_kernel(
         nc.vector.memset(neg_half[:], -0.5)
         rows_bf = keep.tile([P, P], BF16)
         nc.vector.memset(rows_bf[:], 0.0)
-        ac_grouped = []
-        for i in range(2):
-            ac_grouped.append(keep.tile([P, 2, HALF, PACK], BF16, name="ac_grouped%d" % i, align_bytes=64))
-            nc.vector.memset(ac_grouped[i][:].rearrange("p i c t -> p (i c t)").bitcast(I32), 0)
-
-        w1_codes = keep.tile([P, 4 * P], U32, align_bytes=64)
-        w1_scales = keep.tile([P, 4 * P], U8, align_bytes=64)
-        wp_codes = keep.tile([P, 2 * CHANNELS], U32, align_bytes=64)
-        wp_scales = keep.tile([P, 2 * CHANNELS], U8, align_bytes=64)
-        ac_codes = []
-        ac_scales = []
-        for h in range(N_HALVES):
-            ac_codes.append(keep.tile([P, 2 * HALF], U32, name="ac_codes%d" % h, align_bytes=64))
-            ac_scales.append(keep.tile([P, 2 * HALF], U8, name="ac_scales%d" % h, align_bytes=64))
-        bias1 = keep.tile([P, 4], F32)
+        w1_codes = keep.tile([P, 8 * P + LOW], U32, align_bytes=64)
+        w1_scales = keep.tile([P, 8 * P + LOW], U8, align_bytes=64)
+        nc.vector.memset(w1_codes[:, 8 * P :], 0)
+        nc.vector.memset(w1_scales[:, 8 * P :].bitcast(I32), 0)
+        wp_codes = keep.tile([P, 4 * CHANNELS], U32, align_bytes=64)
+        wp_scales = keep.tile([P, 4 * CHANNELS], U8, align_bytes=64)
+        ac_codes = {}
+        ac_scales = {}
+        for b in range(N_BLOCKS):
+            for i in range(2):
+                ac_codes[(b, i)] = keep.tile([P, HALF], U32, name="ac_codes%d_%d" % (b, i), align_bytes=64)
+                ac_scales[(b, i)] = keep.tile([P, HALF], U8, name="ac_scales%d_%d" % (b, i), align_bytes=64)
+        bias1 = keep.tile([P, 2 * PACK], F32)
         chan = keep.tile([P, 4 * N_CB], F32)
         neg_bp = keep.tile([P, N_CB], F32)
         one_minus_w = keep.tile([P, N_CB], F32)
@@ -96,6 +107,8 @@ def tile_parallelretention_pb_t_kernel(
 
         h_tiles = {}
         h_quantised = {}
+        staged_a = {}
+        grouped_ac = {}
         x_tiles = {}
         y_tiles = {}
         stats_tiles = {}
@@ -130,60 +143,77 @@ def tile_parallelretention_pb_t_kernel(
                         out=g32[:, i, pair * PAIR : (pair + 1) * PAIR, :],
                         in_=bank[:].rearrange("p u c -> p c u"),
                     )
-            h_codes = work.tile([P, 2 * HALF], U32, align_bytes=64)
-            h_scales = work.tile([P, 2 * HALF], U8, align_bytes=64)
+            h_codes = halves.tile([P, 2 * HALF], U32, align_bytes=64)
+            h_scales = halves.tile([P, 2 * HALF], U8, align_bytes=64)
             nc.vector.quantize_mx(out=h_codes[:].bitcast(FP8X4), scales=h_scales[:], in_=grouped[:])
             h_quantised[h] = (h_codes, h_scales)
             if h + 2 < N_HALVES:
                 load_half(h + 2)
 
-        def first_matmuls(h):
-            h_codes, h_scales = h_quantised[h]
-            staged = work.tile([P, 4, HALF], BF16)
-            for i in range(2):
-                for t in range(2):
-                    m = 2 * i + t
-                    acc = ps_mx.tile([P, HALF], F32, tag="mx")
-                    nc.tensor.matmul_mx(
-                        out=acc[:],
-                        lhsT=w1_codes[:, m * P : (m + 1) * P].bitcast(FP8X4),
-                        lhsT_scale=w1_scales[:, m * P : (m + 1) * P],
-                        rhs=h_codes[:, i * HALF : (i + 1) * HALF].bitcast(FP8X4),
-                        rhs_scale=h_scales[:, i * HALF : (i + 1) * HALF],
-                        start=True,
-                        stop=True,
-                    )
-                    nc.scalar.activation(
-                        out=staged[:, m, :],
-                        in_=acc[:],
-                        func=ACT.Gelu if i == 0 else ACT.Identity,
-                        bias=bias1[:, m : m + 1],
-                        scale=1.0,
-                    )
-                nc.vector.tensor_copy(
-                    out=ac_grouped[h % 2][:, i, :, 0:2],
-                    in_=staged[:, 2 * i : 2 * i + 2, :].rearrange("p t c -> p c t"),
+        def first_pass_pair(acc, b, i, t, cols):
+            for odd in range(2):
+                h_codes, h_scales = h_quantised[2 * b + odd]
+                start = (PACK * i + t) * P + (0 if odd else LOW)
+                w = slice(start, start + P)
+                r = slice(i * HALF + cols.start, i * HALF + cols.stop)
+                nc.tensor.matmul_mx(
+                    out=acc,
+                    lhsT=w1_codes[:, w].bitcast(FP8X4),
+                    lhsT_scale=w1_scales[:, w],
+                    rhs=h_codes[:, r].bitcast(FP8X4),
+                    rhs_scale=h_scales[:, r],
+                    start=(odd == 0),
+                    stop=(odd == 1),
                 )
 
-        def quantise_ac(h):
+        def first_matmuls_a(b):
+            staged = work.tile([P, PACK, HALF], BF16, tag="staged")
+            for t in range(PACK):
+                acc = ps_mx.tile([P, HALF], F32, tag="mx")
+                first_pass_pair(acc[:], b, 0, t, slice(0, HALF))
+                nc.scalar.activation(
+                    out=staged[:, t, :], in_=acc[:], func=ACT.Gelu, bias=bias1[:, t : t + 1], scale=1.0
+                )
+            staged_a[b] = staged
+
+        def first_matmuls_c(b):
+            grouped = work.tile([P, HALF, PACK], BF16, tag="c_grouped", align_bytes=64)
+            for q in range(HALF // P):
+                acc = ps_mx.tile([P, PACK, P], F32, tag="mx")
+                for t in range(PACK):
+                    first_pass_pair(acc[:, t, :], b, 1, t, slice(q * P, (q + 1) * P))
+                nc.vector.tensor_tensor(
+                    out=grouped[:, q * P : (q + 1) * P, :],
+                    in0=acc[:].rearrange("p t c -> p c t"),
+                    in1=bias1[:, PACK : 2 * PACK].unsqueeze(1).to_broadcast([P, P, PACK]),
+                    op=ALU.add,
+                )
+            grouped_ac[(b, 1)] = grouped
+
+        def group_a(b):
+            grouped = work.tile([P, HALF, PACK], BF16, tag="a_grouped", align_bytes=64)
+            nc.vector.tensor_copy(out=grouped[:], in_=staged_a[b][:].rearrange("p t c -> p c t"))
+            grouped_ac[(b, 0)] = grouped
+
+        def quantise_ac(b, i):
             nc.vector.quantize_mx(
-                out=ac_codes[h][:].bitcast(FP8X4),
-                scales=ac_scales[h][:],
-                in_=ac_grouped[h % 2][:].rearrange("p i c t -> p (i c t)"),
+                out=ac_codes[(b, i)][:].bitcast(FP8X4),
+                scales=ac_scales[(b, i)][:],
+                in_=grouped_ac[(b, i)][:].rearrange("p c t -> p (c t)"),
             )
 
         def second_matmuls(cb, b):
             for half in range(2):
-                h = 2 * b + half
                 x = ps_mx.tile([P, HALF], F32, tag="mx")
                 for i in range(2):
-                    w_cols = slice(i * CHANNELS + cb * P, i * CHANNELS + (cb + 1) * P)
+                    start = WP_VERSION[(i, half)] * CHANNELS + cb * P
+                    w_cols = slice(start, start + P)
                     nc.tensor.matmul_mx(
                         out=x[:],
                         lhsT=wp_codes[:, w_cols].bitcast(FP8X4),
                         lhsT_scale=wp_scales[:, w_cols],
-                        rhs=ac_codes[h][:, i * HALF : (i + 1) * HALF].bitcast(FP8X4),
-                        rhs_scale=ac_scales[h][:, i * HALF : (i + 1) * HALF],
+                        rhs=ac_codes[(b, i)][:].bitcast(FP8X4),
+                        rhs_scale=ac_scales[(b, i)][:],
                         start=(i == 0),
                         stop=(i == 1),
                     )
@@ -275,14 +305,23 @@ def tile_parallelretention_pb_t_kernel(
             )
 
         def prepare_wp_and_channel_vectors():
-            wp_grouped = work.tile([P, 2 * CHANNELS * PACK], BF16, tag="grouped", align_bytes=64)
-            nc.vector.memset(wp_grouped[:].bitcast(I32), 0)
-            wp_g32 = wp_grouped[:].bitcast(F32).rearrange("p (i c s) -> p i c s", i=2, s=2)
-            for pair in range(2):
-                bank = ps_t.tile([P, 2, PAIR], F32, tag="t")
-                transpose_row_tiles(nc, bank, wp_sb[:].bitcast(F32), 2 * pair, ident)
-                nc.vector.tensor_copy(out=wp_g32[:, :, pair * PAIR : (pair + 1) * PAIR, 0], in_=bank[:])
-            nc.vector.quantize_mx(out=wp_codes[:].bitcast(FP8X4), scales=wp_scales[:], in_=wp_grouped[:])
+            for s, source in enumerate((wp_sb, wp_swapped)):
+                wp_grouped = work.tile([P, 2 * CHANNELS * PACK], BF16, tag="wp_grouped", align_bytes=64)
+                nc.vector.memset(wp_grouped[:].bitcast(I32), 0)
+                wp_g32 = wp_grouped[:].bitcast(F32).rearrange("p (v c u) -> p v c u", v=2, u=2)
+                for pair in range(2):
+                    bank = ps_t.tile([P, 2, PAIR], F32, tag="t")
+                    transpose_row_tiles_by_fours(nc, bank, source[:].bitcast(F32), 2 * pair, ident)
+                    cols = slice(pair * PAIR, (pair + 1) * PAIR)
+                    for v in range(2):
+                        part = slice(v * LOW, (v + 1) * LOW)
+                        nc.vector.tensor_copy(
+                            out=wp_g32[part, v, cols, :], in_=bank[part].rearrange("p u c -> p c u")
+                        )
+                v_cols = slice(2 * s * CHANNELS, 2 * (s + 1) * CHANNELS)
+                nc.vector.quantize_mx(
+                    out=wp_codes[:, v_cols].bitcast(FP8X4), scales=wp_scales[:, v_cols], in_=wp_grouped[:]
+                )
             rows_f32 = keep.tile([P, P], F32)
             nc.vector.tensor_copy(out=rows_f32[:], in_=rows_bf[:])
             bank = ps_t.tile([P, 2, PAIR], F32, tag="t")
@@ -294,47 +333,73 @@ def tile_parallelretention_pb_t_kernel(
             )
 
         load_half(0)
-        w1_sb = streamed.tile([P, 4 * K], BF16, tag="first")
-        nc.sync.dma_start(out=w1_sb[:, 0 : 2 * K], in_=Wr.rearrange("(p t) k -> p (t k)", t=2))
-        nc.sync.dma_start(out=w1_sb[:, 2 * K : 4 * K], in_=Wc.rearrange("(p t) k -> p (t k)", t=2))
-        br_bf = keep.tile([P, 2], BF16)
-        bc_bf = keep.tile([P, 2], BF16)
-        nc.scalar.dma_start(out=br_bf[:], in_=br.rearrange("(p t) -> p t", t=2))
-        nc.scalar.dma_start(out=bc_bf[:], in_=bc.rearrange("(p t) -> p t", t=2))
+        w1_sb = streamed.tile([P, PACK * K], BF16, tag="first")
+        nc.sync.dma_start(out=w1_sb[0:LOW, :], in_=Wr.rearrange("(m t) k -> m (t k)", t=PACK))
+        nc.sync.dma_start(out=w1_sb[LOW:P, :], in_=Wc.rearrange("(m t) k -> m (t k)", t=PACK))
+        bias_bf = keep.tile([P, 2, BLOCK32], BF16)
+        for part in range(2):
+            for i, vec in enumerate((br, bc)):
+                nc.scalar.dma_start(
+                    out=bias_bf[part * LOW : (part + 1) * LOW, i, 0:PACK],
+                    in_=vec.rearrange("(m t) -> m t", t=PACK),
+                )
         load_half(1)
         wp_sb = streamed.tile([P, N_CB * K], BF16, tag="second")
         nc.sync.dma_start(
             out=wp_sb[:].rearrange("p (c k) -> p c k", c=N_CB), in_=Wp.rearrange("(c p) k -> p c k", p=P)
         )
+        wp_swapped = keep.tile([P, N_CB * K], BF16)
+        for part in range(2):
+            nc.sync.dma_start(
+                out=wp_swapped[:].rearrange("p (c k) -> p c k", c=N_CB)[
+                    :, :, part * FEATURES : (part + 1) * FEATURES
+                ],
+                in_=Wp.rearrange("(c p) k -> p c k", p=P)[:, :, (1 - part) * FEATURES : (2 - part) * FEATURES],
+            )
         for v, vec in enumerate((bp, prelu_w, gn_w, gn_b)):
             nc.scalar.dma_start(
                 out=rows_bf[N_CB * v : N_CB * (v + 1), :], in_=vec.rearrange("(c p) -> c p", p=P)
             )
 
-        w1_grouped = work.tile([P, 4 * P * PACK], BF16, tag="grouped", align_bytes=64)
-        w1_g32 = w1_grouped[:].bitcast(F32).rearrange("p (c u) -> p c u", u=2)
+        w1_grouped = work.tile([P, 8 * P * PACK], BF16, tag="grouped", align_bytes=64)
+        nc.vector.memset(w1_grouped[:].bitcast(I32), 0)
+        w1_g32 = w1_grouped[:].bitcast(F32).rearrange("p (i t c u) -> p i t c u", i=2, t=PACK, u=2)
         for pair in range(2):
             bank = ps_t.tile([P, 2, PAIR], F32, tag="t")
             transpose_row_tiles(nc, bank, w1_sb[:].bitcast(F32), 2 * pair, ident)
-            nc.vector.tensor_copy(
-                out=w1_g32[:, pair * PAIR : (pair + 1) * PAIR, :], in_=bank[:].rearrange("p u c -> p c u")
-            )
-        nc.vector.quantize_mx(out=w1_codes[:].bitcast(FP8X4), scales=w1_scales[:], in_=w1_grouped[:])
-        nc.vector.tensor_copy(out=bias1[:, 0:2], in_=br_bf[:])
-        nc.vector.tensor_copy(out=bias1[:, 2:4], in_=bc_bf[:])
+            for j in range(2):
+                nc.vector.tensor_copy(
+                    out=w1_g32[:, :, 2 * pair + j, LOW:P, :],
+                    in_=bank[:, :, j * P : (j + 1) * P].rearrange("p u (i c) -> p i c u", i=2),
+                )
+        nc.vector.quantize_mx(
+            out=w1_codes[:, 0 : 8 * P].bitcast(FP8X4), scales=w1_scales[:, 0 : 8 * P], in_=w1_grouped[:]
+        )
+        nc.vector.tensor_copy(
+            out=bias1[:].rearrange("p (i t) -> p i t", i=2),
+            in_=bias_bf[:, :, 0:PACK],
+        )
 
-        for i in range(N_HALVES + 3):
-            if i < N_HALVES:
-                transpose_and_quantise(i)
+        for i in range(N_BLOCKS + 3):
+            if i < N_BLOCKS:
+                transpose_and_quantise(2 * i)
             if i == 0:
                 prepare_wp_and_channel_vectors()
-            if 2 <= i < N_HALVES + 2:
-                quantise_ac(i - 2)
-            if 1 <= i <= N_HALVES:
-                first_matmuls(i - 1)
-            if i >= 3 and i % 2 == 0:
-                second_matmuls(0, (i - 3) // 2)
-                prelu_block(0, (i - 3) // 2)
+            if 2 <= i < N_BLOCKS + 2:
+                quantise_ac(i - 2, 1)
+            if 1 <= i <= N_BLOCKS:
+                first_matmuls_a(i - 1)
+            if i < N_BLOCKS:
+                transpose_and_quantise(2 * i + 1)
+            if 1 <= i <= N_BLOCKS:
+                first_matmuls_c(i - 1)
+                group_a(i - 1)
+            if i >= 3:
+                prelu_block(0, i - 3)
+            if 2 <= i < N_BLOCKS + 2:
+                second_matmuls(0, i - 2)
+            if 1 <= i <= N_BLOCKS:
+                quantise_ac(i - 1, 0)
         channel_moments(0)
 
         steps = N_CB * N_BLOCKS

@@ -28,13 +28,24 @@ TILES = BLOCK // P
 N_BLOCKS = ROWS // BLOCK
 HALF = 512
 HALF_TILES = HALF // P
-N_HALVES = ROWS // HALF
 PAIR = 2 * P
 N_CB = CHANNELS // P
-WP_VERSION = {(0, 0): 0, (1, 1): 1, (1, 0): 2, (0, 1): 3}
-STAT_PARTS = 3
-LAG = N_BLOCKS + STAT_PARTS
+GROUPS = 4
+N_GROUPS = GROUPS * N_BLOCKS
+UNITS = 2 * N_BLOCKS
+WP_VERSION = {(0, 0): (0, 0), (1, 1): (0, 1), (1, 0): (1, 0), (0, 1): (1, 1)}
 BLOCK32 = 16
+A_LAG = 4
+C_LAG = 6
+X_LAG = 12
+Z_LAG = 11
+N_LEAD = 3
+AHEAD = 7
+WP_TICK = 4
+MEANS = 5
+SPREAD = 7
+TAIL_SHARE = 4
+BY_SCALAR = (range(1, UNITS, 2), range(1, 8, 2), range(0), range(0))
 BN_STATS_DIM = 6
 
 FLOPS = 2 * ROWS * (K * FEATURES * 2 + K * CHANNELS)
@@ -62,10 +73,10 @@ def tile_parallelretention_pb_t_kernel(
     nc = tc.nc
     with ExitStack() as pools:
         keep = pools.enter_context(tc.tile_pool(name="keep", bufs=1))
-        streamed = pools.enter_context(tc.tile_pool(name="streamed", bufs=3))
+        streamed = pools.enter_context(tc.tile_pool(name="streamed", bufs=8))
         work = pools.enter_context(tc.tile_pool(name="work", bufs=2))
-        halves = pools.enter_context(tc.tile_pool(name="halves", bufs=4))
-        y_pool = pools.enter_context(tc.tile_pool(name="y_pool", bufs=LAG + 2))
+        quantised = pools.enter_context(tc.tile_pool(name="quantised", bufs=8))
+        y_pool = pools.enter_context(tc.tile_pool(name="y_pool", bufs=18))
         small = pools.enter_context(tc.tile_pool(name="small", bufs=2))
         ps_t = pools.enter_context(tc.psum_pool(name="ps_t", bufs=4))
         ps_mx = pools.enter_context(tc.psum_pool(name="ps_mx", bufs=4))
@@ -84,6 +95,7 @@ def tile_parallelretention_pb_t_kernel(
         nc.vector.memset(neg_half[:], -0.5)
         rows_bf = keep.tile([P, P], BF16)
         nc.vector.memset(rows_bf[:], 0.0)
+
         w1_codes = keep.tile([P, 8 * P + LOW], U32, align_bytes=64)
         w1_scales = keep.tile([P, 8 * P + LOW], U8, align_bytes=64)
         nc.vector.memset(w1_codes[:, 8 * P :], 0)
@@ -105,166 +117,241 @@ def tile_parallelretention_pb_t_kernel(
         gn_w_c = chan[:, 2 * N_CB : 3 * N_CB]
         gn_b_c = chan[:, 3 * N_CB : 4 * N_CB]
 
+        sums = []
+        squares = []
+        minus_first = []
+        for cb in range(N_CB):
+            sums.append(keep.tile([P, UNITS], F32, name="sums%d" % cb))
+            squares.append(keep.tile([P, UNITS], F32, name="squares%d" % cb))
+            minus_first.append(keep.tile([P, 1], F32, name="minus_first%d" % cb))
+
         h_tiles = {}
+        h_banks = {}
+        h_grouped = {}
         h_quantised = {}
-        staged_a = {}
-        grouped_ac = {}
-        x_tiles = {}
+        a_sums = {}
+        a_staged = {}
+        c_sums = {}
+        ac_grouped = {}
+        x_sums = {}
+        negs = {}
         y_tiles = {}
         stats_tiles = {}
         moments = {}
+        group_moments = {}
+        spreads = {}
+        group_spreads = {}
         coefficients = {}
+        z_banks = {}
+        z_tiles = {}
 
-        def load_half(h):
-            b, half = divmod(h, 2)
-            rows = slice(b * BLOCK, (b + 1) * BLOCK)
-            tiles = slice(HALF_TILES * half, HALF_TILES * (half + 1))
-            hr = streamed.tile([P, HALF_TILES * K], BF16, tag="first")
-            nc.sync.dma_start(
-                out=hr[:].rearrange("p (j k) -> p j k", j=HALF_TILES),
-                in_=h_ret[rows, :].rearrange("(p j) k -> p j k", j=TILES)[:, tiles, :],
-            )
-            hp = streamed.tile([P, HALF_TILES * K], BF16, tag="second")
-            nc.sync.dma_start(
-                out=hp[:].rearrange("p (j k) -> p j k", j=HALF_TILES),
-                in_=h_prime[rows, :].rearrange("(p j) k -> p j k", j=TILES)[:, tiles, :],
-            )
-            h_tiles[h] = (hr, hp)
+        def load_group(g, pieces=1):
+            b, r = divmod(g, GROUPS)
+            i, half = divmod(r, 2)
+            source = (h_ret, h_prime)[i][b * BLOCK : (b + 1) * BLOCK, :].rearrange("(p j) k -> p j k", j=TILES)
+            tile = streamed.tile([P, HALF_TILES * K], BF16, tag="rows")
+            view = tile[:].rearrange("p (j k) -> p j k", j=HALF_TILES)
+            step = HALF_TILES // pieces
+            for j in range(0, HALF_TILES, step):
+                nc.sync.dma_start(
+                    out=view[:, j : j + step, :],
+                    in_=source[:, HALF_TILES * half + j : HALF_TILES * half + j + step, :],
+                )
+            h_tiles[g] = tile
 
-        def transpose_and_quantise(h):
-            grouped = work.tile([P, 2 * HALF * PACK], BF16, tag="grouped", align_bytes=64)
-            g32 = grouped[:].bitcast(F32).rearrange("p (i c u) -> p i c u", i=2, u=2)
-            for i in range(2):
-                words = h_tiles[h][i][:].bitcast(F32)
-                for pair in range(2):
-                    bank = ps_t.tile([P, 2, PAIR], F32, tag="t")
-                    transpose_row_tiles(nc, bank, words, 2 * pair, ident)
-                    nc.scalar.copy(
-                        out=g32[:, i, pair * PAIR : (pair + 1) * PAIR, :],
-                        in_=bank[:].rearrange("p u c -> p c u"),
-                    )
-            h_codes = halves.tile([P, 2 * HALF], U32, align_bytes=64)
-            h_scales = halves.tile([P, 2 * HALF], U8, align_bytes=64)
-            nc.vector.quantize_mx(out=h_codes[:].bitcast(FP8X4), scales=h_scales[:], in_=grouped[:])
-            h_quantised[h] = (h_codes, h_scales)
-            if h + 2 < N_HALVES:
-                load_half(h + 2)
+        def transpose_group(g):
+            h_banks[g] = []
+            for pair in range(2):
+                bank = ps_t.tile([P, 2, PAIR], F32, tag="t")
+                transpose_row_tiles(nc, bank, h_tiles[g][:].bitcast(F32), 2 * pair, ident)
+                h_banks[g].append(bank)
+
+        def copy_group(g):
+            grouped = work.tile([P, HALF * PACK], BF16, tag="h_grouped", align_bytes=64, bufs=3)
+            g32 = grouped[:].bitcast(F32).rearrange("p (c u) -> p c u", u=2)
+            for pair in range(2):
+                nc.scalar.copy(
+                    out=g32[:, pair * PAIR : (pair + 1) * PAIR, :],
+                    in_=h_banks[g][pair][:].rearrange("p u c -> p c u"),
+                )
+            h_grouped[g] = grouped
+
+        def quantise_group(g):
+            codes = quantised.tile([P, HALF], U32, tag="codes", align_bytes=64)
+            scales = quantised.tile([P, HALF], U8, tag="scales", align_bytes=64)
+            nc.vector.quantize_mx(out=codes[:].bitcast(FP8X4), scales=scales[:], in_=h_grouped[g][:])
+            h_quantised[g] = (codes, scales)
 
         def first_pass_pair(acc, b, i, t, cols):
             for odd in range(2):
-                h_codes, h_scales = h_quantised[2 * b + odd]
-                start = (PACK * i + t) * P + (0 if odd else LOW)
+                codes, scales = h_quantised[GROUPS * b + 2 * i + odd]
+                start = (2 * t + i) * P + (0 if odd else LOW)
                 w = slice(start, start + P)
-                r = slice(i * HALF + cols.start, i * HALF + cols.stop)
                 nc.tensor.matmul_mx(
                     out=acc,
                     lhsT=w1_codes[:, w].bitcast(FP8X4),
                     lhsT_scale=w1_scales[:, w],
-                    rhs=h_codes[:, r].bitcast(FP8X4),
-                    rhs_scale=h_scales[:, r],
+                    rhs=codes[:, cols].bitcast(FP8X4),
+                    rhs_scale=scales[:, cols],
                     start=(odd == 0),
                     stop=(odd == 1),
                 )
 
-        def first_matmuls_a(b):
-            staged = work.tile([P, PACK, HALF], BF16, tag="staged")
-            for t in range(PACK):
-                acc = ps_mx.tile([P, HALF], F32, tag="mx")
-                first_pass_pair(acc[:], b, 0, t, slice(0, HALF))
-                nc.scalar.activation(
-                    out=staged[:, t, :], in_=acc[:], func=ACT.Gelu, bias=bias1[:, t : t + 1], scale=1.0
-                )
-            staged_a[b] = staged
+        def multiply_a(b, t):
+            acc = ps_mx.tile([P, HALF], F32, tag="mx")
+            first_pass_pair(acc[:], b, 0, t, slice(0, HALF))
+            a_sums[(b, t)] = acc
 
-        def first_matmuls_c(b):
-            grouped = work.tile([P, HALF, PACK], BF16, tag="c_grouped", align_bytes=64)
-            for q in range(HALF // P):
-                acc = ps_mx.tile([P, PACK, P], F32, tag="mx")
-                for t in range(PACK):
-                    first_pass_pair(acc[:, t, :], b, 1, t, slice(q * P, (q + 1) * P))
-                nc.vector.tensor_tensor(
-                    out=grouped[:, q * P : (q + 1) * P, :],
-                    in0=acc[:].rearrange("p t c -> p c t"),
-                    in1=bias1[:, PACK : 2 * PACK].unsqueeze(1).to_broadcast([P, P, PACK]),
-                    op=ALU.add,
-                )
-            grouped_ac[(b, 1)] = grouped
+        def gelu_a(b, t):
+            if t == 0:
+                staged = work.tile([P, PACK, HALF], BF16, tag="a_staged")
+                a_staged[b] = staged
+            nc.scalar.activation(
+                out=a_staged[b][:, t, :], in_=a_sums[(b, t)][:], func=ACT.Gelu, bias=bias1[:, t : t + 1], scale=1.0
+            )
 
-        def group_a(b):
+        def interleave_a(b):
             grouped = work.tile([P, HALF, PACK], BF16, tag="a_grouped", align_bytes=64)
-            nc.vector.tensor_copy(out=grouped[:], in_=staged_a[b][:].rearrange("p t c -> p c t"))
-            grouped_ac[(b, 0)] = grouped
+            nc.vector.tensor_copy(out=grouped[:], in_=a_staged[b][:].rearrange("p t c -> p c t"))
+            ac_grouped[(b, 0)] = grouped
+
+        def multiply_c(b, q):
+            acc = ps_mx.tile([P, PACK, P], F32, tag="mx")
+            for t in range(PACK):
+                first_pass_pair(acc[:, t, :], b, 1, t, slice(q * P, (q + 1) * P))
+            c_sums[(b, q)] = acc
+
+        def bias_c(b, q):
+            if q == 0:
+                grouped = work.tile([P, HALF, PACK], BF16, tag="c_grouped", align_bytes=64)
+                ac_grouped[(b, 1)] = grouped
+            nc.vector.tensor_tensor(
+                out=ac_grouped[(b, 1)][:, q * P : (q + 1) * P, :],
+                in0=c_sums[(b, q)][:].rearrange("p t c -> p c t"),
+                in1=bias1[:, PACK : 2 * PACK].unsqueeze(1).to_broadcast([P, P, PACK]),
+                op=ALU.add,
+            )
 
         def quantise_ac(b, i):
             nc.vector.quantize_mx(
                 out=ac_codes[(b, i)][:].bitcast(FP8X4),
                 scales=ac_scales[(b, i)][:],
-                in_=grouped_ac[(b, i)][:].rearrange("p c t -> p (c t)"),
+                in_=ac_grouped[(b, i)][:].rearrange("p c t -> p (c t)"),
             )
 
-        def second_matmuls(cb, b):
-            for half in range(2):
-                x = ps_mx.tile([P, HALF], F32, tag="mx")
-                for i in range(2):
-                    start = WP_VERSION[(i, half)] * CHANNELS + cb * P
-                    w_cols = slice(start, start + P)
-                    nc.tensor.matmul_mx(
-                        out=x[:],
-                        lhsT=wp_codes[:, w_cols].bitcast(FP8X4),
-                        lhsT_scale=wp_scales[:, w_cols],
-                        rhs=ac_codes[(b, i)][:].bitcast(FP8X4),
-                        rhs_scale=ac_scales[(b, i)][:],
-                        start=(i == 0),
-                        stop=(i == 1),
-                    )
-                x_tiles[(cb, b, half)] = x
+        def multiply_x(cb, n):
+            b, half = divmod(n, 2)
+            x = ps_mx.tile([P, HALF], F32, tag="mx")
+            for i in range(2):
+                s, v = WP_VERSION[(i, half)]
+                start = ((2 * s + cb // 2) * 2 + v) * PAIR + cb % 2 * P
+                w = slice(start, start + P)
+                nc.tensor.matmul_mx(
+                    out=x[:],
+                    lhsT=wp_codes[:, w].bitcast(FP8X4),
+                    lhsT_scale=wp_scales[:, w],
+                    rhs=ac_codes[(b, i)][:].bitcast(FP8X4),
+                    rhs_scale=ac_scales[(b, i)][:],
+                    start=(i == 0),
+                    stop=(i == 1),
+                )
+            x_sums[(cb, n)] = x
 
-        def prelu_block(cb, b):
-            if b == 0:
-                stats = small.tile([P, N_HALVES, BN_STATS_DIM], F32)
+        def negative_part(cb, n):
+            neg = work.tile([P, HALF], F32, tag="neg", bufs=3)
+            nc.scalar.activation(
+                out=neg[:], in_=x_sums[(cb, n)][:], func=ACT.Relu, bias=neg_bp[:, cb : cb + 1], scale=-1.0
+            )
+            negs[(cb, n)] = neg
+
+        def prelu(cb, n):
+            b, half = divmod(n, 2)
+            if half == 0:
+                y = y_pool.tile([P, BLOCK], F32, tag="y")
+                y_tiles[(cb, b)] = y
+            nc.vector.scalar_tensor_tensor(
+                out=y_tiles[(cb, b)][:, half * HALF : (half + 1) * HALF],
+                in0=negs[(cb, n)][:],
+                scalar=one_minus_w[:, cb : cb + 1],
+                in1=x_sums[(cb, n)][:],
+                op0=ALU.mult,
+                op1=ALU.add,
+                accum_out=sums[cb][:, n : n + 1] if n in BY_SCALAR[cb] else None,
+            )
+
+        def statistics(cb, n):
+            b, half = divmod(n, 2)
+            y = y_tiles[(cb, b)][:, half * HALF : (half + 1) * HALF]
+            if n == 0:
+                stats = small.tile([P, UNITS, BN_STATS_DIM], F32)
                 stats_tiles[cb] = stats
-            neg = work.tile([P, BLOCK], F32)
-            y = y_pool.tile([P, BLOCK], F32)
-            y_tiles[(cb, b)] = y
-            for half in range(2):
-                cols = slice(half * HALF, (half + 1) * HALF)
-                x = x_tiles[(cb, b, half)]
+            if n in BY_SCALAR[cb]:
+                unused = work.tile([P, HALF], BF16, tag="unused")
                 nc.scalar.activation(
-                    out=neg[:, cols], in_=x[:], func=ACT.Relu, bias=neg_bp[:, cb : cb + 1], scale=-1.0
+                    out=unused[:], in_=y, func=ACT.Square, bias=minus_first[cb][:], scale=1.0,
+                    accum_out=squares[cb][:, n : n + 1],
                 )
+            else:
+                nc.vector.bn_stats(out=stats_tiles[cb][:, n, :], in_=y)
+            if n == 0 and len(BY_SCALAR[cb]) > 0:
+                first = small.tile([P, 2], F32)
+                nc.vector.bn_aggr(out=first[:], in_=stats_tiles[cb][:, 0, :])
+                nc.vector.tensor_scalar(
+                    out=minus_first[cb][:], in0=first[:, 0:1], scalar1=-1.0, scalar2=None, op0=ALU.mult
+                )
+
+        def sums_to_statistics(cb):
+            rest = slice(BY_SCALAR[cb].start, BY_SCALAR[cb].stop, BY_SCALAR[cb].step)
+            halves = stats_tiles[cb][:, rest, :].rearrange("p n (e s) -> p e n s", e=2)
+            mean = small.tile([P, UNITS], F32)
+            nc.vector.tensor_scalar(
+                out=mean[:, rest], in0=sums[cb][:, rest], scalar1=1.0 / HALF, scalar2=None, op0=ALU.mult
+            )
+            dev = small.tile([P, UNITS], F32)
+            nc.vector.tensor_scalar(
+                out=dev[:, rest], in0=mean[:, rest], scalar1=minus_first[cb][:, 0:1], scalar2=None, op0=ALU.add
+            )
+            nc.vector.tensor_mul(out=dev[:, rest], in0=dev[:, rest], in1=dev[:, rest])
+            nc.vector.tensor_scalar(
+                out=dev[:, rest], in0=dev[:, rest], scalar1=-0.5 * HALF, scalar2=None, op0=ALU.mult
+            )
+            for e in range(2):
+                nc.vector.memset(halves[:, e, :, 0], 0.5 * HALF)
+                nc.vector.tensor_copy(out=halves[:, e, :, 1], in_=mean[:, rest])
                 nc.vector.scalar_tensor_tensor(
-                    out=y[:, cols],
-                    in0=neg[:, cols],
-                    scalar=one_minus_w[:, cb : cb + 1],
-                    in1=x[:],
-                    op0=ALU.mult,
-                    op1=ALU.add,
+                    out=halves[:, e, :, 2], in0=squares[cb][:, rest], scalar=0.5, in1=dev[:, rest],
+                    op0=ALU.mult, op1=ALU.add,
                 )
-            for half in range(2):
-                cols = slice(half * HALF, (half + 1) * HALF)
-                nc.vector.bn_stats(out=stats_tiles[cb][:, 2 * b + half, :], in_=y[:, cols])
 
         def channel_moments(cb):
+            if len(BY_SCALAR[cb]) > 0:
+                sums_to_statistics(cb)
             mv = small.tile([P, 2], F32)
             nc.vector.bn_aggr(out=mv[:], in_=stats_tiles[cb][:].rearrange("p n s -> p (n s)"))
             nc.vector.tensor_add(out=mv[:, 0:1], in0=mv[:, 0:1], in1=bp_c[:, cb : cb + 1])
+            moments[cb] = mv
+
+        def average_moments(cb):
             g1 = ps_t.tile([P, 2], F32, tag="t")
-            nc.tensor.matmul(out=g1[:], lhsT=group_avg[:], rhs=mv[:], start=True, stop=True)
-            moments[cb] = [mv, g1]
+            nc.tensor.matmul(out=g1[:], lhsT=group_avg[:], rhs=moments[cb][:], start=True, stop=True)
+            group_moments[cb] = g1
 
         def spread_of_means(cb):
-            mv, g1 = moments[cb]
+            mv, g1 = moments[cb], group_moments[cb]
             gm = small.tile([P, 2], F32)
             nc.vector.tensor_copy(out=gm[:], in_=g1[:])
             dev = small.tile([P, 2], F32)
             nc.vector.tensor_sub(out=dev[:], in0=mv[:], in1=gm[:])
             nc.vector.tensor_mul(out=dev[:], in0=dev[:], in1=dev[:])
+            spreads[cb] = (gm, dev)
+
+        def average_spread(cb):
             g2 = ps_t.tile([P, 2], F32, tag="t")
-            nc.tensor.matmul(out=g2[:], lhsT=group_avg[:], rhs=dev[:], start=True, stop=True)
-            moments[cb] = [gm, g2]
+            nc.tensor.matmul(out=g2[:], lhsT=group_avg[:], rhs=spreads[cb][1][:], start=True, stop=True)
+            group_spreads[cb] = g2
 
         def scale_and_shift(cb):
-            gm, g2 = moments[cb]
+            gm, g2 = spreads[cb][0], group_spreads[cb]
             one = slice(cb, cb + 1)
             var_eps = small.tile([P, 1], F32)
             nc.vector.scalar_tensor_tensor(
@@ -283,57 +370,98 @@ def tile_parallelretention_pb_t_kernel(
             )
             coefficients[cb] = (scale, shift)
 
-        def normalise_block(cb, b):
-            y = y_tiles[(cb, b)]
+        def normalise(cb, n, engine):
+            b, half = divmod(n, 2)
             scale, shift = coefficients[cb]
-            engine = nc.vector if cb == N_CB - 1 else nc.gpsimd
+            y = y_tiles[(cb, b)][:, half * HALF : (half + 1) * HALF]
             engine.tensor_scalar(
-                out=y[:], in0=y[:], scalar1=scale[:, 0:1], scalar2=shift[:, 0:1], op0=ALU.mult, op1=ALU.add
-            )
-            z = streamed.tile([P, TILES, P], F32, tag="first")
-            for half in range(2):
-                zt = ps_t.tile([P, HALF_TILES, P], F32, tag="t")
-                for j in range(HALF_TILES):
-                    col = (HALF_TILES * half + j) * P
-                    nc.tensor.transpose(zt[:, j, :], y[:, col : col + P], ident[:])
-                nc.scalar.copy(out=z[:, HALF_TILES * half : HALF_TILES * (half + 1), :], in_=zt[:])
-            nc.sync.dma_start(
-                out=out[b * BLOCK : (b + 1) * BLOCK, cb * P : (cb + 1) * P].rearrange(
-                    "(p j) c -> p j c", j=TILES
-                ),
-                in_=z[:],
+                out=y, in0=y, scalar1=scale[:, 0:1], scalar2=shift[:, 0:1], op0=ALU.mult, op1=ALU.add
             )
 
-        def prepare_wp_and_channel_vectors():
-            for s, source in enumerate((wp_sb, wp_swapped)):
-                wp_grouped = work.tile([P, 2 * CHANNELS * PACK], BF16, tag="wp_grouped", align_bytes=64)
-                nc.vector.memset(wp_grouped[:].bitcast(I32), 0)
-                wp_g32 = wp_grouped[:].bitcast(F32).rearrange("p (v c u) -> p v c u", v=2, u=2)
-                for pair in range(2):
-                    bank = ps_t.tile([P, 2, PAIR], F32, tag="t")
-                    transpose_row_tiles_by_fours(nc, bank, source[:].bitcast(F32), 2 * pair, ident)
-                    cols = slice(pair * PAIR, (pair + 1) * PAIR)
-                    for v in range(2):
-                        part = slice(v * LOW, (v + 1) * LOW)
-                        nc.vector.tensor_copy(
-                            out=wp_g32[part, v, cols, :], in_=bank[part].rearrange("p u c -> p c u")
-                        )
-                v_cols = slice(2 * s * CHANNELS, 2 * (s + 1) * CHANNELS)
-                nc.vector.quantize_mx(
-                    out=wp_codes[:, v_cols].bitcast(FP8X4), scales=wp_scales[:, v_cols], in_=wp_grouped[:]
+        def transpose_back(cb, n):
+            b, half = divmod(n, 2)
+            zt = ps_t.tile([P, HALF_TILES, P], F32, tag="t")
+            for j in range(HALF_TILES):
+                col = (HALF_TILES * half + j) * P
+                nc.tensor.transpose(zt[:, j, :], y_tiles[(cb, b)][:, col : col + P], ident[:])
+            z_banks[(cb, n)] = zt
+
+        def copy_back(cb, n, on_vector):
+            b, half = divmod(n, 2)
+            if half == 0:
+                z = streamed.tile([P, TILES, P], F32, tag="rows")
+                z_tiles[(cb, b)] = z
+            part = z_tiles[(cb, b)][:, HALF_TILES * half : HALF_TILES * (half + 1), :]
+            if on_vector:
+                nc.vector.tensor_copy(out=part, in_=z_banks[(cb, n)][:])
+            else:
+                nc.scalar.copy(out=part, in_=z_banks[(cb, n)][:])
+            if half == 1:
+                nc.sync.dma_start(
+                    out=out[b * BLOCK : (b + 1) * BLOCK, cb * P : (cb + 1) * P].rearrange(
+                        "(p j) c -> p j c", j=TILES
+                    ),
+                    in_=z_tiles[(cb, b)][:],
                 )
-            rows_f32 = keep.tile([P, P], F32)
-            nc.vector.tensor_copy(out=rows_f32[:], in_=rows_bf[:])
+
+        def prepare_w1(pair):
+            grouped = work.tile([P, PAIR, 2, PACK], BF16, tag="w_grouped", align_bytes=64)
+            nc.gpsimd.memset(grouped[:].rearrange("p c i t -> p (c i t)").bitcast(I32), 0)
+            g32 = grouped[:].rearrange("p c i t -> p (c i t)").bitcast(F32)
+            g32 = g32.rearrange("p (j i c u) -> p j i c u", j=2, i=2, u=2)
             bank = ps_t.tile([P, 2, PAIR], F32, tag="t")
-            nc.tensor.transpose(bank[:, 0, 0:P], rows_f32[:], ident[:])
-            nc.vector.tensor_copy(out=chan[:], in_=bank[:, 0, 0 : 4 * N_CB])
+            transpose_row_tiles(nc, bank, w1_sb[:].bitcast(F32), 2 * pair, ident)
+            for j in range(2):
+                nc.vector.tensor_copy(
+                    out=g32[:, j, :, LOW:P, :],
+                    in_=bank[:, :, j * P : (j + 1) * P].rearrange("p u (i c) -> p i c u", i=2),
+                )
+            cols = slice(4 * P * pair, 4 * P * (pair + 1))
+            nc.vector.quantize_mx(
+                out=w1_codes[:, cols].bitcast(FP8X4),
+                scales=w1_scales[:, cols],
+                in_=grouped[:].rearrange("p c i t -> p (c i t)"),
+            )
+
+        def prepare_bias1():
+            for i in range(2):
+                nc.vector.tensor_copy(out=bias1[:, PACK * i : PACK * (i + 1)], in_=bias_bf[:, i, 0:PACK])
+
+        wp_grouped = {}
+
+        def transpose_wp(s, pair):
+            grouped = work.tile([P, 2, PAIR, PACK], BF16, tag="w_grouped", align_bytes=64)
+            flat = grouped[:].rearrange("p v c t -> p (v c t)")
+            nc.gpsimd.memset(flat.bitcast(I32), 0)
+            g32 = flat.bitcast(F32).rearrange("p (v c u) -> p v c u", v=2, u=2)
+            bank = ps_t.tile([P, 2, PAIR], F32, tag="t")
+            transpose_row_tiles_by_fours(nc, bank, (wp_sb, wp_swapped)[s][:].bitcast(F32), 2 * pair, ident)
+            for v in range(2):
+                part = slice(v * LOW, (v + 1) * LOW)
+                nc.vector.tensor_copy(out=g32[part, v, :, :], in_=bank[part].rearrange("p u c -> p c u"))
+            wp_grouped[(s, pair)] = flat
+
+        def quantise_wp(s, pair):
+            start = (2 * s + pair) * 2 * PAIR
+            cols = slice(start, start + 2 * PAIR)
+            nc.vector.quantize_mx(
+                out=wp_codes[:, cols].bitcast(FP8X4), scales=wp_scales[:, cols], in_=wp_grouped[(s, pair)]
+            )
+
+        rows_f32 = keep.tile([P, P], F32)
+
+        def prepare_channel_vectors():
+            bank = ps_t.tile([P, P], F32, tag="t")
+            nc.tensor.transpose(bank[:], rows_f32[:], ident[:])
+            nc.vector.tensor_copy(out=chan[:], in_=bank[:, 0 : 4 * N_CB])
             nc.vector.tensor_scalar(out=neg_bp[:], in0=bp_c, scalar1=-1.0, scalar2=None, op0=ALU.mult)
             nc.vector.tensor_scalar(
                 out=one_minus_w[:], in0=prelu_w_c, scalar1=-1.0, scalar2=1.0, op0=ALU.mult, op1=ALU.add
             )
 
-        load_half(0)
-        w1_sb = streamed.tile([P, PACK * K], BF16, tag="first")
+        load_group(0, pieces=2)
+        load_group(1)
+        w1_sb = y_pool.tile([P, PACK * K], BF16, tag="y")
         nc.sync.dma_start(out=w1_sb[0:LOW, :], in_=Wr.rearrange("(m t) k -> m (t k)", t=PACK))
         nc.sync.dma_start(out=w1_sb[LOW:P, :], in_=Wc.rearrange("(m t) k -> m (t k)", t=PACK))
         bias_bf = keep.tile([P, 2, BLOCK32], BF16)
@@ -343,12 +471,19 @@ def tile_parallelretention_pb_t_kernel(
                     out=bias_bf[part * LOW : (part + 1) * LOW, i, 0:PACK],
                     in_=vec.rearrange("(m t) -> m t", t=PACK),
                 )
-        load_half(1)
-        wp_sb = streamed.tile([P, N_CB * K], BF16, tag="second")
+        for v, vec in enumerate((bp, prelu_w, gn_w, gn_b)):
+            nc.scalar.dma_start(
+                out=rows_bf[N_CB * v : N_CB * (v + 1), :], in_=vec.rearrange("(c p) -> c p", p=P)
+            )
+        for g in range(2, GROUPS):
+            load_group(g)
+        wp_sb = y_pool.tile([P, N_CB * K], BF16, tag="y")
         nc.sync.dma_start(
             out=wp_sb[:].rearrange("p (c k) -> p c k", c=N_CB), in_=Wp.rearrange("(c p) k -> p c k", p=P)
         )
-        wp_swapped = keep.tile([P, N_CB * K], BF16)
+        for g in range(GROUPS, 7):
+            load_group(g)
+        wp_swapped = y_pool.tile([P, N_CB * K], BF16, tag="y")
         for part in range(2):
             nc.sync.dma_start(
                 out=wp_swapped[:].rearrange("p (c k) -> p c k", c=N_CB)[
@@ -356,64 +491,109 @@ def tile_parallelretention_pb_t_kernel(
                 ],
                 in_=Wp.rearrange("(c p) k -> p c k", p=P)[:, :, (1 - part) * FEATURES : (2 - part) * FEATURES],
             )
-        for v, vec in enumerate((bp, prelu_w, gn_w, gn_b)):
-            nc.scalar.dma_start(
-                out=rows_bf[N_CB * v : N_CB * (v + 1), :], in_=vec.rearrange("(c p) -> c p", p=P)
-            )
 
-        w1_grouped = work.tile([P, 8 * P * PACK], BF16, tag="grouped", align_bytes=64)
-        nc.vector.memset(w1_grouped[:].bitcast(I32), 0)
-        w1_g32 = w1_grouped[:].bitcast(F32).rearrange("p (i t c u) -> p i t c u", i=2, t=PACK, u=2)
-        for pair in range(2):
-            bank = ps_t.tile([P, 2, PAIR], F32, tag="t")
-            transpose_row_tiles(nc, bank, w1_sb[:].bitcast(F32), 2 * pair, ident)
-            for j in range(2):
-                nc.vector.tensor_copy(
-                    out=w1_g32[:, :, 2 * pair + j, LOW:P, :],
-                    in_=bank[:, :, j * P : (j + 1) * P].rearrange("p u (i c) -> p i c u", i=2),
-                )
-        nc.vector.quantize_mx(
-            out=w1_codes[:, 0 : 8 * P].bitcast(FP8X4), scales=w1_scales[:, 0 : 8 * P], in_=w1_grouped[:]
-        )
-        nc.vector.tensor_copy(
-            out=bias1[:].rearrange("p (i t) -> p i t", i=2),
-            in_=bias_bf[:, :, 0:PACK],
-        )
+        y_tick = {}
+        for n in range(UNITS):
+            y_tick[(0, n)] = GROUPS * (n // 2) + X_LAG + n % 2
+        tick = N_GROUPS
+        for cb in range(1, N_CB):
+            for n in range(0, UNITS, 2):
+                while tick in y_tick.values() or tick + 1 in y_tick.values():
+                    tick += 1
+                y_tick[(cb, n)] = tick
+                y_tick[(cb, n + 1)] = tick + 1
+        last_y = max(y_tick.values())
+        z_tick = {}
+        tick = 0
+        for cb in range(N_CB):
+            tick = max(tick, y_tick[(cb, UNITS - 1)] + Z_LAG)
+            for n in range(0, UNITS, 2):
+                z_tick[(cb, n)] = tick
+                z_tick[(cb, n + 1)] = tick
+                tick += 1 if tick > last_y else 2
 
-        for i in range(N_BLOCKS + 3):
-            if i < N_BLOCKS:
-                transpose_and_quantise(2 * i)
-            if i == 0:
-                prepare_wp_and_channel_vectors()
-            if 2 <= i < N_BLOCKS + 2:
-                quantise_ac(i - 2, 1)
-            if 1 <= i <= N_BLOCKS:
-                first_matmuls_a(i - 1)
-            if i < N_BLOCKS:
-                transpose_and_quantise(2 * i + 1)
-            if 1 <= i <= N_BLOCKS:
-                first_matmuls_c(i - 1)
-                group_a(i - 1)
-            if i >= 3:
-                prelu_block(0, i - 3)
-            if 2 <= i < N_BLOCKS + 2:
-                second_matmuls(0, i - 2)
-            if 1 <= i <= N_BLOCKS:
-                quantise_ac(i - 1, 0)
-        channel_moments(0)
+        def take_group(g):
+            if g < N_GROUPS:
+                transpose_group(g)
+                if g + AHEAD < N_GROUPS:
+                    load_group(g + AHEAD)
 
-        steps = N_CB * N_BLOCKS
-        second_matmuls(1, 0)
-        for step in range(N_BLOCKS, steps + LAG):
-            if step < steps:
-                prelu_block(step // N_BLOCKS, step % N_BLOCKS)
-            if step >= LAG:
-                normalise_block((step - LAG) // N_BLOCKS, (step - LAG) % N_BLOCKS)
-            if step + 1 < steps:
-                second_matmuls((step + 1) // N_BLOCKS, (step + 1) % N_BLOCKS)
-            if step % N_BLOCKS == N_BLOCKS - 1 and step < steps:
-                channel_moments(step // N_BLOCKS)
-            if step % N_BLOCKS == 0 and step <= steps:
-                spread_of_means(step // N_BLOCKS - 1)
-            if step % N_BLOCKS == 1 and step <= steps + 1:
-                scale_and_shift(step // N_BLOCKS - 1)
+        def units_at(ticks, tick):
+            return [unit for unit in ticks if ticks[unit] == tick]
+
+        with tc.manual_schedule():
+            for tick in range(max(z_tick.values()) + 3):
+                a_step = divmod(tick - A_LAG, PACK)
+                c_step = divmod(tick - C_LAG, PACK)
+                a_out = divmod(tick - 1 - A_LAG, PACK)
+                c_out = divmod(tick - 1 - C_LAG, PACK)
+                after = {}
+                for cb in range(N_CB):
+                    after[tick - y_tick[(cb, UNITS - 1)]] = cb
+                if 0 <= a_out[0] < N_BLOCKS:
+                    gelu_a(a_out[0], a_out[1])
+                if 0 <= tick - 1 < N_GROUPS:
+                    copy_group(tick - 1)
+                for cb, n in units_at(z_tick, tick - 1):
+                    if tick - 1 > last_y:
+                        copy_back(cb, n, n % TAIL_SHARE == 1)
+                    elif n % 2 == 0:
+                        copy_back(cb, n, False)
+                for cb, n in units_at(z_tick, tick - 2):
+                    if tick - 2 <= last_y and n % 2 == 1:
+                        copy_back(cb, n, False)
+                for cb, n in units_at(y_tick, tick - 1):
+                    negative_part(cb, n)
+                if 0 <= c_out[0] < N_BLOCKS:
+                    bias_c(c_out[0], c_out[1])
+                if 0 <= tick - 2 < N_GROUPS:
+                    quantise_group(tick - 2)
+                if a_out[1] == 0 and 1 <= a_out[0] <= N_BLOCKS:
+                    interleave_a(a_out[0] - 1)
+                if a_out[1] == 1 and 1 <= a_out[0] <= N_BLOCKS:
+                    quantise_ac(a_out[0] - 1, 0)
+                if c_out[1] == 0 and 1 <= c_out[0] <= N_BLOCKS:
+                    quantise_ac(c_out[0] - 1, 1)
+                for cb, n in units_at(y_tick, tick - 1):
+                    prelu(cb, n)
+                for cb, n in units_at(y_tick, tick - 1 - 1):
+                    statistics(cb, n)
+                if 1 + 1 in after:
+                    channel_moments(after[1 + 1])
+                if tick % 2 == 1:
+                    take_group(tick)
+                if 0 <= a_step[0] < N_BLOCKS:
+                    multiply_a(a_step[0], a_step[1])
+                if 0 <= c_step[0] < N_BLOCKS:
+                    multiply_c(c_step[0], c_step[1])
+                for cb, n in units_at(y_tick, tick):
+                    if cb == 0:
+                        multiply_x(cb, n)
+                    elif n % 2 == 0:
+                        multiply_x(cb, n)
+                        multiply_x(cb, n + 1)
+                if MEANS in after:
+                    average_moments(after[MEANS])
+                    spread_of_means(after[MEANS])
+                if SPREAD in after:
+                    average_spread(after[SPREAD])
+                    scale_and_shift(after[SPREAD])
+                if tick == 1:
+                    prepare_w1(0)
+                    prepare_bias1()
+                if tick == 2:
+                    prepare_w1(1)
+                if tick == 3:
+                    nc.vector.tensor_copy(out=rows_f32[:], in_=rows_bf[:])
+                if WP_TICK < tick <= WP_TICK + 4:
+                    quantise_wp((tick - WP_TICK - 1) // 2, (tick - WP_TICK - 1) % 2)
+                if WP_TICK <= tick < WP_TICK + 4:
+                    transpose_wp((tick - WP_TICK) // 2, (tick - WP_TICK) % 2)
+                if tick == WP_TICK + 4:
+                    prepare_channel_vectors()
+                if tick % 2 == 0:
+                    take_group(tick)
+                for cb, n in units_at(z_tick, tick):
+                    transpose_back(cb, n)
+                for cb, n in units_at(z_tick, tick + N_LEAD):
+                    normalise(cb, n, nc.vector if cb == N_CB - 1 else nc.gpsimd)

@@ -30,22 +30,23 @@ HALF = 512
 HALF_TILES = HALF // P
 PAIR = 2 * P
 N_CB = CHANNELS // P
-GROUPS = 4
-N_GROUPS = GROUPS * N_BLOCKS
+N_HALVES = ROWS // HALF
+N_GROUPS = 2 * N_HALVES
 UNITS = 2 * N_BLOCKS
-WP_VERSION = {(0, 0): (0, 0), (1, 1): (0, 1), (1, 0): (1, 0), (0, 1): (1, 1)}
 BLOCK32 = 16
-A_LAG = 4
-C_LAG = 6
+A_LAG = 3
+C_LAG = 4
 X_LAG = 12
 Z_LAG = 11
 N_LEAD = 3
 AHEAD = 7
-WP_TICK = 4
-MEANS = 5
-SPREAD = 7
+WP_TICK = 5
+I_LAG = 10
+MEANS = 6
+SPREAD = 8
 TAIL_SHARE = 4
-BY_SCALAR = (range(1, UNITS, 2), range(1, 8, 2), range(0), range(0))
+STAGED_BUFS = 5
+BY_SCALAR = (range(0), range(1, 8, 2), range(0), range(0))
 BN_STATS_DIM = 6
 
 FLOPS = 2 * ROWS * (K * FEATURES * 2 + K * CHANNELS)
@@ -96,19 +97,16 @@ def tile_parallelretention_pb_t_kernel(
         rows_bf = keep.tile([P, P], BF16)
         nc.vector.memset(rows_bf[:], 0.0)
 
-        w1_codes = keep.tile([P, 8 * P + LOW], U32, align_bytes=64)
-        w1_scales = keep.tile([P, 8 * P + LOW], U8, align_bytes=64)
-        nc.vector.memset(w1_codes[:, 8 * P :], 0)
-        nc.vector.memset(w1_scales[:, 8 * P :].bitcast(I32), 0)
-        wp_codes = keep.tile([P, 4 * CHANNELS], U32, align_bytes=64)
-        wp_scales = keep.tile([P, 4 * CHANNELS], U8, align_bytes=64)
+        w1_codes = keep.tile([P, 4 * P], U32, align_bytes=64)
+        w1_scales = keep.tile([P, 4 * P], U8, align_bytes=64)
+        wp_codes = keep.tile([P, CHANNELS], U32, align_bytes=64)
+        wp_scales = keep.tile([P, CHANNELS], U8, align_bytes=64)
         ac_codes = {}
         ac_scales = {}
-        for b in range(N_BLOCKS):
-            for i in range(2):
-                ac_codes[(b, i)] = keep.tile([P, HALF], U32, name="ac_codes%d_%d" % (b, i), align_bytes=64)
-                ac_scales[(b, i)] = keep.tile([P, HALF], U8, name="ac_scales%d_%d" % (b, i), align_bytes=64)
-        bias1 = keep.tile([P, 2 * PACK], F32)
+        for h in range(N_HALVES):
+            ac_codes[h] = keep.tile([P, HALF], U32, name="ac_codes%d" % h, align_bytes=64)
+            ac_scales[h] = keep.tile([P, HALF], U8, name="ac_scales%d" % h, align_bytes=64)
+        bias1 = keep.tile([P, 4], F32)
         chan = keep.tile([P, 4 * N_CB], F32)
         neg_bp = keep.tile([P, N_CB], F32)
         one_minus_w = keep.tile([P, N_CB], F32)
@@ -129,9 +127,9 @@ def tile_parallelretention_pb_t_kernel(
         h_banks = {}
         h_grouped = {}
         h_quantised = {}
-        a_sums = {}
+        ac_sums = {}
         a_staged = {}
-        c_sums = {}
+        c_staged = {}
         ac_grouped = {}
         x_sums = {}
         negs = {}
@@ -146,8 +144,8 @@ def tile_parallelretention_pb_t_kernel(
         z_tiles = {}
 
         def load_group(g, pieces=1):
-            b, r = divmod(g, GROUPS)
-            i, half = divmod(r, 2)
+            h, i = divmod(g, 2)
+            b, half = divmod(h, 2)
             source = (h_ret, h_prime)[i][b * BLOCK : (b + 1) * BLOCK, :].rearrange("(p j) k -> p j k", j=TILES)
             tile = streamed.tile([P, HALF_TILES * K], BF16, tag="rows")
             view = tile[:].rearrange("p (j k) -> p j k", j=HALF_TILES)
@@ -182,79 +180,71 @@ def tile_parallelretention_pb_t_kernel(
             nc.vector.quantize_mx(out=codes[:].bitcast(FP8X4), scales=scales[:], in_=h_grouped[g][:])
             h_quantised[g] = (codes, scales)
 
-        def first_pass_pair(acc, b, i, t, cols):
-            for odd in range(2):
-                codes, scales = h_quantised[GROUPS * b + 2 * i + odd]
-                start = (2 * t + i) * P + (0 if odd else LOW)
-                w = slice(start, start + P)
+        def multiply_ac(h, i):
+            codes, scales = h_quantised[2 * h + i]
+            for j in range(2):
+                acc = ps_mx.tile([P, HALF], F32, tag="mx")
+                w = slice((2 * i + j) * P, (2 * i + j + 1) * P)
                 nc.tensor.matmul_mx(
-                    out=acc,
+                    out=acc[:],
                     lhsT=w1_codes[:, w].bitcast(FP8X4),
                     lhsT_scale=w1_scales[:, w],
-                    rhs=codes[:, cols].bitcast(FP8X4),
-                    rhs_scale=scales[:, cols],
-                    start=(odd == 0),
-                    stop=(odd == 1),
+                    rhs=codes[:].bitcast(FP8X4),
+                    rhs_scale=scales[:],
+                    start=True,
+                    stop=True,
                 )
+                ac_sums[(h, i, j)] = acc
 
-        def multiply_a(b, t):
-            acc = ps_mx.tile([P, HALF], F32, tag="mx")
-            first_pass_pair(acc[:], b, 0, t, slice(0, HALF))
-            a_sums[(b, t)] = acc
+        def activate_a(h):
+            staged = work.tile([P, PACK, HALF], BF16, tag="staged", bufs=STAGED_BUFS)
+            for j in range(2):
+                nc.scalar.activation(
+                    out=staged[:, j, :], in_=ac_sums[(h, 0, j)][:], func=ACT.Gelu, bias=bias1[:, j : j + 1], scale=1.0
+                )
+            a_staged[h] = staged
 
-        def gelu_a(b, t):
-            if t == 0:
-                staged = work.tile([P, PACK, HALF], BF16, tag="a_staged")
-                a_staged[b] = staged
+        def activate_c(h):
+            staged = work.tile([P, 2, HALF], BF16, tag="c_staged", bufs=3)
+            c_staged[h] = staged
             nc.scalar.activation(
-                out=a_staged[b][:, t, :], in_=a_sums[(b, t)][:], func=ACT.Gelu, bias=bias1[:, t : t + 1], scale=1.0
+                out=staged[:, 0, :], in_=ac_sums[(h, 1, 0)][:], func=ACT.Identity, bias=bias1[:, 2:3], scale=1.0
+            )
+            nc.vector.tensor_scalar(
+                out=staged[:, 1, :], in0=ac_sums[(h, 1, 1)][:], scalar1=bias1[:, 3:4], scalar2=None, op0=ALU.add
             )
 
-        def interleave_a(b):
-            grouped = work.tile([P, HALF, PACK], BF16, tag="a_grouped", align_bytes=64)
-            nc.vector.tensor_copy(out=grouped[:], in_=a_staged[b][:].rearrange("p t c -> p c t"))
-            ac_grouped[(b, 0)] = grouped
+        def move_a(h):
+            nc.sync.dma_start(out=a_staged[h][0:LOW, 2:4, :], in_=a_staged[h][LOW:P, 0:2, :])
 
-        def multiply_c(b, q):
-            acc = ps_mx.tile([P, PACK, P], F32, tag="mx")
-            for t in range(PACK):
-                first_pass_pair(acc[:, t, :], b, 1, t, slice(q * P, (q + 1) * P))
-            c_sums[(b, q)] = acc
+        def move_c(h):
+            nc.sync.dma_start(out=a_staged[h][LOW:P, 0:2, :], in_=c_staged[h][0:LOW, :, :])
+            nc.sync.dma_start(out=a_staged[h][LOW:P, 2:4, :], in_=c_staged[h][LOW:P, :, :])
 
-        def bias_c(b, q):
-            if q == 0:
-                grouped = work.tile([P, HALF, PACK], BF16, tag="c_grouped", align_bytes=64)
-                ac_grouped[(b, 1)] = grouped
-            nc.vector.tensor_tensor(
-                out=ac_grouped[(b, 1)][:, q * P : (q + 1) * P, :],
-                in0=c_sums[(b, q)][:].rearrange("p t c -> p c t"),
-                in1=bias1[:, PACK : 2 * PACK].unsqueeze(1).to_broadcast([P, P, PACK]),
-                op=ALU.add,
-            )
+        def interleave_ac(h):
+            grouped = work.tile([P, HALF, PACK], BF16, tag="ac_grouped", align_bytes=64)
+            nc.vector.tensor_copy(out=grouped[:], in_=a_staged[h][:].rearrange("p t c -> p c t"))
+            ac_grouped[h] = grouped
 
-        def quantise_ac(b, i):
+        def quantise_ac(h):
             nc.vector.quantize_mx(
-                out=ac_codes[(b, i)][:].bitcast(FP8X4),
-                scales=ac_scales[(b, i)][:],
-                in_=ac_grouped[(b, i)][:].rearrange("p c t -> p (c t)"),
+                out=ac_codes[h][:].bitcast(FP8X4),
+                scales=ac_scales[h][:],
+                in_=ac_grouped[h][:].rearrange("p c t -> p (c t)"),
             )
 
         def multiply_x(cb, n):
-            b, half = divmod(n, 2)
             x = ps_mx.tile([P, HALF], F32, tag="mx")
-            for i in range(2):
-                s, v = WP_VERSION[(i, half)]
-                start = ((2 * s + cb // 2) * 2 + v) * PAIR + cb % 2 * P
-                w = slice(start, start + P)
-                nc.tensor.matmul_mx(
-                    out=x[:],
-                    lhsT=wp_codes[:, w].bitcast(FP8X4),
-                    lhsT_scale=wp_scales[:, w],
-                    rhs=ac_codes[(b, i)][:].bitcast(FP8X4),
-                    rhs_scale=ac_scales[(b, i)][:],
-                    start=(i == 0),
-                    stop=(i == 1),
-                )
+            w = slice(cb * P, (cb + 1) * P)
+            nc.tensor.matmul_mx(
+                out=x[:],
+                lhsT=wp_codes[:, w].bitcast(FP8X4),
+                lhsT_scale=wp_scales[:, w],
+                rhs=ac_codes[n][:].bitcast(FP8X4),
+                rhs_scale=ac_scales[n][:],
+                start=True,
+                stop=True,
+            )
             x_sums[(cb, n)] = x
 
         def negative_part(cb, n):
@@ -285,6 +275,8 @@ def tile_parallelretention_pb_t_kernel(
             if n == 0:
                 stats = small.tile([P, UNITS, BN_STATS_DIM], F32)
                 stats_tiles[cb] = stats
+                if len(BY_SCALAR[cb]) > 0:
+                    nc.gpsimd.memset(stats[:], 0.5 * HALF)
             if n in BY_SCALAR[cb]:
                 unused = work.tile([P, HALF], BF16, tag="unused")
                 nc.scalar.activation(
@@ -302,24 +294,23 @@ def tile_parallelretention_pb_t_kernel(
 
         def sums_to_statistics(cb):
             rest = slice(BY_SCALAR[cb].start, BY_SCALAR[cb].stop, BY_SCALAR[cb].step)
+            n = len(BY_SCALAR[cb])
             halves = stats_tiles[cb][:, rest, :].rearrange("p n (e s) -> p e n s", e=2)
-            mean = small.tile([P, UNITS], F32)
+            dev = small.tile([P, n], F32)
             nc.vector.tensor_scalar(
-                out=mean[:, rest], in0=sums[cb][:, rest], scalar1=1.0 / HALF, scalar2=None, op0=ALU.mult
+                out=dev[:], in0=sums[cb][:, rest], scalar1=1.0 / HALF, scalar2=minus_first[cb][:, 0:1],
+                op0=ALU.mult, op1=ALU.add,
             )
-            dev = small.tile([P, UNITS], F32)
             nc.vector.tensor_scalar(
-                out=dev[:, rest], in0=mean[:, rest], scalar1=minus_first[cb][:, 0:1], scalar2=None, op0=ALU.add
+                out=halves[:, :, :, 1], in0=sums[cb][:, rest].unsqueeze(1).to_broadcast([P, 2, n]),
+                scalar1=1.0 / HALF, scalar2=None, op0=ALU.mult,
             )
-            nc.vector.tensor_mul(out=dev[:, rest], in0=dev[:, rest], in1=dev[:, rest])
-            nc.vector.tensor_scalar(
-                out=dev[:, rest], in0=dev[:, rest], scalar1=-0.5 * HALF, scalar2=None, op0=ALU.mult
+            nc.vector.scalar_tensor_tensor(
+                out=dev[:], in0=dev[:], scalar=-0.5 * HALF, in1=dev[:], op0=ALU.mult, op1=ALU.mult
             )
             for e in range(2):
-                nc.vector.memset(halves[:, e, :, 0], 0.5 * HALF)
-                nc.vector.tensor_copy(out=halves[:, e, :, 1], in_=mean[:, rest])
                 nc.vector.scalar_tensor_tensor(
-                    out=halves[:, e, :, 2], in0=squares[cb][:, rest], scalar=0.5, in1=dev[:, rest],
+                    out=halves[:, e, :, 2], in0=squares[cb][:, rest], scalar=0.5, in1=dev[:],
                     op0=ALU.mult, op1=ALU.add,
                 )
 
@@ -404,49 +395,20 @@ def tile_parallelretention_pb_t_kernel(
                     in_=z_tiles[(cb, b)][:],
                 )
 
-        def prepare_w1(pair):
-            grouped = work.tile([P, PAIR, 2, PACK], BF16, tag="w_grouped", align_bytes=64)
-            nc.gpsimd.memset(grouped[:].rearrange("p c i t -> p (c i t)").bitcast(I32), 0)
-            g32 = grouped[:].rearrange("p c i t -> p (c i t)").bitcast(F32)
-            g32 = g32.rearrange("p (j i c u) -> p j i c u", j=2, i=2, u=2)
-            bank = ps_t.tile([P, 2, PAIR], F32, tag="t")
-            transpose_row_tiles(nc, bank, w1_sb[:].bitcast(F32), 2 * pair, ident)
-            for j in range(2):
+        def prepare_weights(source, transposes, codes, scales):
+            grouped = work.tile([P, HALF * PACK], BF16, tag="h_grouped", align_bytes=64, bufs=3)
+            g32 = grouped[:].bitcast(F32).rearrange("p (c u) -> p c u", u=2)
+            for pair in range(2):
+                bank = ps_t.tile([P, 2, PAIR], F32, tag="t")
+                transposes(nc, bank, source[:].bitcast(F32), 2 * pair, ident)
                 nc.vector.tensor_copy(
-                    out=g32[:, j, :, LOW:P, :],
-                    in_=bank[:, :, j * P : (j + 1) * P].rearrange("p u (i c) -> p i c u", i=2),
+                    out=g32[:, pair * PAIR : (pair + 1) * PAIR, :], in_=bank[:].rearrange("p u c -> p c u")
                 )
-            cols = slice(4 * P * pair, 4 * P * (pair + 1))
-            nc.vector.quantize_mx(
-                out=w1_codes[:, cols].bitcast(FP8X4),
-                scales=w1_scales[:, cols],
-                in_=grouped[:].rearrange("p c i t -> p (c i t)"),
-            )
+            nc.vector.quantize_mx(out=codes[:].bitcast(FP8X4), scales=scales[:], in_=grouped[:])
 
         def prepare_bias1():
             for i in range(2):
-                nc.vector.tensor_copy(out=bias1[:, PACK * i : PACK * (i + 1)], in_=bias_bf[:, i, 0:PACK])
-
-        wp_grouped = {}
-
-        def transpose_wp(s, pair):
-            grouped = work.tile([P, 2, PAIR, PACK], BF16, tag="w_grouped", align_bytes=64)
-            flat = grouped[:].rearrange("p v c t -> p (v c t)")
-            nc.gpsimd.memset(flat.bitcast(I32), 0)
-            g32 = flat.bitcast(F32).rearrange("p (v c u) -> p v c u", v=2, u=2)
-            bank = ps_t.tile([P, 2, PAIR], F32, tag="t")
-            transpose_row_tiles_by_fours(nc, bank, (wp_sb, wp_swapped)[s][:].bitcast(F32), 2 * pair, ident)
-            for v in range(2):
-                part = slice(v * LOW, (v + 1) * LOW)
-                nc.vector.tensor_copy(out=g32[part, v, :, :], in_=bank[part].rearrange("p u c -> p c u"))
-            wp_grouped[(s, pair)] = flat
-
-        def quantise_wp(s, pair):
-            start = (2 * s + pair) * 2 * PAIR
-            cols = slice(start, start + 2 * PAIR)
-            nc.vector.quantize_mx(
-                out=wp_codes[:, cols].bitcast(FP8X4), scales=wp_scales[:, cols], in_=wp_grouped[(s, pair)]
-            )
+                nc.vector.tensor_copy(out=bias1[:, 2 * i : 2 * i + 2], in_=bias_bf[:, i, 0:2])
 
         rows_f32 = keep.tile([P, P], F32)
 
@@ -461,56 +423,49 @@ def tile_parallelretention_pb_t_kernel(
 
         load_group(0, pieces=2)
         load_group(1)
-        w1_sb = y_pool.tile([P, PACK * K], BF16, tag="y")
-        nc.sync.dma_start(out=w1_sb[0:LOW, :], in_=Wr.rearrange("(m t) k -> m (t k)", t=PACK))
-        nc.sync.dma_start(out=w1_sb[LOW:P, :], in_=Wc.rearrange("(m t) k -> m (t k)", t=PACK))
+        w1_sb = y_pool.tile([P, 4 * K], BF16, tag="y")
         bias_bf = keep.tile([P, 2, BLOCK32], BF16)
-        for part in range(2):
-            for i, vec in enumerate((br, bc)):
+        for i, (weights, bias) in enumerate(((Wr, br), (Wc, bc))):
+            for s in range(2):
+                part = slice(s * LOW, (s + 1) * LOW)
+                nc.sync.dma_start(
+                    out=w1_sb[part, 2 * K * i : 2 * K * (i + 1)].rearrange("p (j k) -> p j k", j=2),
+                    in_=weights.rearrange("(m s j) k -> s m j k", s=2, j=2)[s, :, :, :],
+                )
                 nc.scalar.dma_start(
-                    out=bias_bf[part * LOW : (part + 1) * LOW, i, 0:PACK],
-                    in_=vec.rearrange("(m t) -> m t", t=PACK),
+                    out=bias_bf[part, i, 0:2], in_=bias.rearrange("(m s j) -> s m j", s=2, j=2)[s, :, :]
                 )
         for v, vec in enumerate((bp, prelu_w, gn_w, gn_b)):
             nc.scalar.dma_start(
                 out=rows_bf[N_CB * v : N_CB * (v + 1), :], in_=vec.rearrange("(c p) -> c p", p=P)
             )
-        for g in range(2, GROUPS):
+        for g in range(2, 4):
             load_group(g)
         wp_sb = y_pool.tile([P, N_CB * K], BF16, tag="y")
         nc.sync.dma_start(
             out=wp_sb[:].rearrange("p (c k) -> p c k", c=N_CB), in_=Wp.rearrange("(c p) k -> p c k", p=P)
         )
-        for g in range(GROUPS, 7):
+        for g in range(4, AHEAD):
             load_group(g)
-        wp_swapped = y_pool.tile([P, N_CB * K], BF16, tag="y")
-        for part in range(2):
-            nc.sync.dma_start(
-                out=wp_swapped[:].rearrange("p (c k) -> p c k", c=N_CB)[
-                    :, :, part * FEATURES : (part + 1) * FEATURES
-                ],
-                in_=Wp.rearrange("(c p) k -> p c k", p=P)[:, :, (1 - part) * FEATURES : (2 - part) * FEATURES],
-            )
 
-        y_tick = {}
+        x_tick = {}
         for n in range(UNITS):
-            y_tick[(0, n)] = GROUPS * (n // 2) + X_LAG + n % 2
+            x_tick[(0, n)] = 2 * n + X_LAG
         tick = N_GROUPS
         for cb in range(1, N_CB):
-            for n in range(0, UNITS, 2):
-                while tick in y_tick.values() or tick + 1 in y_tick.values():
+            for n in range(UNITS):
+                while tick in x_tick.values():
                     tick += 1
-                y_tick[(cb, n)] = tick
-                y_tick[(cb, n + 1)] = tick + 1
-        last_y = max(y_tick.values())
+                x_tick[(cb, n)] = tick
+        last_x = max(x_tick.values())
         z_tick = {}
         tick = 0
         for cb in range(N_CB):
-            tick = max(tick, y_tick[(cb, UNITS - 1)] + Z_LAG)
+            tick = max(tick, x_tick[(cb, UNITS - 1)] + Z_LAG)
             for n in range(0, UNITS, 2):
                 z_tick[(cb, n)] = tick
                 z_tick[(cb, n + 1)] = tick
-                tick += 1 if tick > last_y else 2
+                tick += 1 if tick > last_x else 2
 
         def take_group(g):
             if g < N_GROUPS:
@@ -521,57 +476,59 @@ def tile_parallelretention_pb_t_kernel(
         def units_at(ticks, tick):
             return [unit for unit in ticks if ticks[unit] == tick]
 
+        def half_at(lag):
+            h, rest = divmod(tick - lag, 2)
+            return [h] if rest == 0 and 0 <= h < N_HALVES else []
+
         with tc.manual_schedule():
             for tick in range(max(z_tick.values()) + 3):
-                a_step = divmod(tick - A_LAG, PACK)
-                c_step = divmod(tick - C_LAG, PACK)
-                a_out = divmod(tick - 1 - A_LAG, PACK)
-                c_out = divmod(tick - 1 - C_LAG, PACK)
                 after = {}
                 for cb in range(N_CB):
-                    after[tick - y_tick[(cb, UNITS - 1)]] = cb
-                if 0 <= a_out[0] < N_BLOCKS:
-                    gelu_a(a_out[0], a_out[1])
+                    after[tick - x_tick[(cb, UNITS - 1)]] = cb
+                for h in half_at(A_LAG + 1):
+                    activate_a(h)
+                for h in half_at(C_LAG + 1):
+                    activate_c(h)
                 if 0 <= tick - 1 < N_GROUPS:
                     copy_group(tick - 1)
                 for cb, n in units_at(z_tick, tick - 1):
-                    if tick - 1 > last_y:
+                    if tick - 1 > last_x:
                         copy_back(cb, n, n % TAIL_SHARE == 1)
                     elif n % 2 == 0:
                         copy_back(cb, n, False)
                 for cb, n in units_at(z_tick, tick - 2):
-                    if tick - 2 <= last_y and n % 2 == 1:
+                    if tick - 2 <= last_x and n % 2 == 1:
                         copy_back(cb, n, False)
-                for cb, n in units_at(y_tick, tick - 1):
+                for cb, n in units_at(x_tick, tick - 1):
                     negative_part(cb, n)
-                if 0 <= c_out[0] < N_BLOCKS:
-                    bias_c(c_out[0], c_out[1])
                 if 0 <= tick - 2 < N_GROUPS:
                     quantise_group(tick - 2)
-                if a_out[1] == 0 and 1 <= a_out[0] <= N_BLOCKS:
-                    interleave_a(a_out[0] - 1)
-                if a_out[1] == 1 and 1 <= a_out[0] <= N_BLOCKS:
-                    quantise_ac(a_out[0] - 1, 0)
-                if c_out[1] == 0 and 1 <= c_out[0] <= N_BLOCKS:
-                    quantise_ac(c_out[0] - 1, 1)
-                for cb, n in units_at(y_tick, tick - 1):
+                for h in half_at(I_LAG):
+                    interleave_ac(h)
+                for h in half_at(I_LAG + 1):
+                    quantise_ac(h)
+                for cb, n in units_at(x_tick, tick - 1):
                     prelu(cb, n)
-                for cb, n in units_at(y_tick, tick - 1 - 1):
+                for cb, n in units_at(x_tick, tick - 2):
                     statistics(cb, n)
-                if 1 + 1 in after:
-                    channel_moments(after[1 + 1])
+                if 2 in after:
+                    channel_moments(after[2])
+                for h in half_at(A_LAG + 2):
+                    move_a(h)
+                for h in half_at(C_LAG + 2):
+                    move_c(h)
                 if tick % 2 == 1:
                     take_group(tick)
-                if 0 <= a_step[0] < N_BLOCKS:
-                    multiply_a(a_step[0], a_step[1])
-                if 0 <= c_step[0] < N_BLOCKS:
-                    multiply_c(c_step[0], c_step[1])
-                for cb, n in units_at(y_tick, tick):
-                    if cb == 0:
+                for h in half_at(A_LAG):
+                    multiply_ac(h, 0)
+                for h in half_at(C_LAG):
+                    multiply_ac(h, 1)
+                if tick <= N_GROUPS + X_LAG:
+                    for cb, n in units_at(x_tick, tick):
                         multiply_x(cb, n)
-                    elif n % 2 == 0:
+                elif tick % 2 == 1:
+                    for cb, n in units_at(x_tick, tick) + units_at(x_tick, tick + 1):
                         multiply_x(cb, n)
-                        multiply_x(cb, n + 1)
                 if MEANS in after:
                     average_moments(after[MEANS])
                     spread_of_means(after[MEANS])
@@ -579,17 +536,13 @@ def tile_parallelretention_pb_t_kernel(
                     average_spread(after[SPREAD])
                     scale_and_shift(after[SPREAD])
                 if tick == 1:
-                    prepare_w1(0)
                     prepare_bias1()
-                if tick == 2:
-                    prepare_w1(1)
+                    prepare_weights(w1_sb, transpose_row_tiles, w1_codes, w1_scales)
                 if tick == 3:
                     nc.vector.tensor_copy(out=rows_f32[:], in_=rows_bf[:])
-                if WP_TICK < tick <= WP_TICK + 4:
-                    quantise_wp((tick - WP_TICK - 1) // 2, (tick - WP_TICK - 1) % 2)
-                if WP_TICK <= tick < WP_TICK + 4:
-                    transpose_wp((tick - WP_TICK) // 2, (tick - WP_TICK) % 2)
-                if tick == WP_TICK + 4:
+                if tick == WP_TICK:
+                    prepare_weights(wp_sb, transpose_row_tiles_by_fours, wp_codes, wp_scales)
+                if tick == WP_TICK + 1:
                     prepare_channel_vectors()
                 if tick % 2 == 0:
                     take_group(tick)

@@ -36,17 +36,16 @@ UNITS = 2 * N_BLOCKS
 BLOCK32 = 16
 A_LAG = 3
 C_LAG = 4
-X_LAG = 12
-Z_LAG = 11
-N_LEAD = 3
+X_LAG = 13
+Z_LAG = 14
+N_LEAD = 5
 AHEAD = 7
 WP_TICK = 5
-I_LAG = 10
-MEANS = 6
-SPREAD = 8
+I_LAG = 11
+STATS_LAGS = (4, 4, 5, 5, 6, 6, 7, 7, 8)
 TAIL_SHARE = 4
-STAGED_BUFS = 5
-BY_SCALAR = (range(0), range(1, 8, 2), range(0), range(0))
+STAGED_BUFS = 6
+BY_SCALAR = (range(0), range(1, 12), range(0), range(0))
 BN_STATS_DIM = 6
 
 FLOPS = 2 * ROWS * (K * FEATURES * 2 + K * CHANNELS)
@@ -76,8 +75,8 @@ def tile_parallelretention_pb_t_kernel(
         keep = pools.enter_context(tc.tile_pool(name="keep", bufs=1))
         streamed = pools.enter_context(tc.tile_pool(name="streamed", bufs=8))
         work = pools.enter_context(tc.tile_pool(name="work", bufs=2))
-        quantised = pools.enter_context(tc.tile_pool(name="quantised", bufs=8))
-        y_pool = pools.enter_context(tc.tile_pool(name="y_pool", bufs=18))
+        quantised = pools.enter_context(tc.tile_pool(name="quantised", bufs=5))
+        y_pool = pools.enter_context(tc.tile_pool(name="y_pool", bufs=20))
         small = pools.enter_context(tc.tile_pool(name="small", bufs=2))
         ps_t = pools.enter_context(tc.psum_pool(name="ps_t", bufs=4))
         ps_mx = pools.enter_context(tc.psum_pool(name="ps_mx", bufs=4))
@@ -87,11 +86,8 @@ def tile_parallelretention_pb_t_kernel(
         warm = keep.tile([P, 1], F32)
         nc.vector.memset(warm[:], 0.0)
         nc.scalar.activation(out=warm[:], in_=warm[:], func=ACT.Gelu)
-        group_avg = keep.tile([P, P], F32)
-        nc.vector.memset(group_avg[:], 0.0)
-        for g in range(P // GROUP):
-            span = slice(g * GROUP, (g + 1) * GROUP)
-            nc.vector.memset(group_avg[span, span], 1.0 / GROUP)
+        channel_mv = keep.tile([P, GROUP], F32, align_bytes=64)
+        nc.vector.memset(channel_mv[:], 0.0)
         neg_half = keep.tile([P, 1], F32)
         nc.vector.memset(neg_half[:], -0.5)
         rows_bf = keep.tile([P, P], BF16)
@@ -135,10 +131,7 @@ def tile_parallelretention_pb_t_kernel(
         negs = {}
         y_tiles = {}
         stats_tiles = {}
-        moments = {}
-        group_moments = {}
-        spreads = {}
-        group_spreads = {}
+        stats_values = {}
         coefficients = {}
         z_banks = {}
         z_tiles = {}
@@ -236,15 +229,16 @@ def tile_parallelretention_pb_t_kernel(
         def multiply_x(cb, n):
             x = ps_mx.tile([P, HALF], F32, tag="mx")
             w = slice(cb * P, (cb + 1) * P)
-            nc.tensor.matmul_mx(
-                out=x[:],
-                lhsT=wp_codes[:, w].bitcast(FP8X4),
-                lhsT_scale=wp_scales[:, w],
-                rhs=ac_codes[n][:].bitcast(FP8X4),
-                rhs_scale=ac_scales[n][:],
-                start=True,
-                stop=True,
-            )
+            for repeat in range(2 if n % 2 == 0 or cb == 0 else 1):
+                nc.tensor.matmul_mx(
+                    out=x[:],
+                    lhsT=wp_codes[:, w].bitcast(FP8X4),
+                    lhsT_scale=wp_scales[:, w],
+                    rhs=ac_codes[n][:].bitcast(FP8X4),
+                    rhs_scale=ac_scales[n][:],
+                    start=True,
+                    stop=True,
+                )
             x_sums[(cb, n)] = x
 
         def negative_part(cb, n):
@@ -314,59 +308,63 @@ def tile_parallelretention_pb_t_kernel(
                     op0=ALU.mult, op1=ALU.add,
                 )
 
-        def channel_moments(cb):
-            if len(BY_SCALAR[cb]) > 0:
-                sums_to_statistics(cb)
-            mv = small.tile([P, 2], F32)
-            nc.vector.bn_aggr(out=mv[:], in_=stats_tiles[cb][:].rearrange("p n s -> p (n s)"))
-            nc.vector.tensor_add(out=mv[:, 0:1], in0=mv[:, 0:1], in1=bp_c[:, cb : cb + 1])
-            moments[cb] = mv
-
-        def average_moments(cb):
-            g1 = ps_t.tile([P, 2], F32, tag="t")
-            nc.tensor.matmul(out=g1[:], lhsT=group_avg[:], rhs=moments[cb][:], start=True, stop=True)
-            group_moments[cb] = g1
-
-        def spread_of_means(cb):
-            mv, g1 = moments[cb], group_moments[cb]
-            gm = small.tile([P, 2], F32)
-            nc.vector.tensor_copy(out=gm[:], in_=g1[:])
-            dev = small.tile([P, 2], F32)
-            nc.vector.tensor_sub(out=dev[:], in0=mv[:], in1=gm[:])
-            nc.vector.tensor_mul(out=dev[:], in0=dev[:], in1=dev[:])
-            spreads[cb] = (gm, dev)
-
-        def average_spread(cb):
-            g2 = ps_t.tile([P, 2], F32, tag="t")
-            nc.tensor.matmul(out=g2[:], lhsT=group_avg[:], rhs=spreads[cb][1][:], start=True, stop=True)
-            group_spreads[cb] = g2
-
-        def scale_and_shift(cb):
-            gm, g2 = spreads[cb][0], group_spreads[cb]
+        def stats_step(step, cb):
             one = slice(cb, cb + 1)
-            var_eps = small.tile([P, 1], F32)
-            nc.vector.scalar_tensor_tensor(
-                out=var_eps[:], in0=g2[:, 0:1], scalar=EPS, in1=gm[:, 1:2], op0=ALU.add, op1=ALU.add
-            )
-            centre = small.tile([P, 1], F32)
-            nc.vector.tensor_sub(out=centre[:], in0=bp_c[:, one], in1=gm[:, 0:1])
-            rstd = small.tile([P, 1], F32)
-            nc.gpsimd.tensor_tensor(out=rstd[:], in0=var_eps[:], in1=neg_half[:], op=ALU.pow)
-            scale = small.tile([P, 1], F32)
-            nc.gpsimd.tensor_tensor(out=scale[:], in0=rstd[:], in1=gn_w_c[:, one], op=ALU.mult)
-            shift = small.tile([P, 1], F32)
-            nc.gpsimd.tensor_scalar(
-                out=shift[:], in0=centre[:], scalar1=scale[:, 0:1], scalar2=gn_b_c[:, one],
-                op0=ALU.mult, op1=ALU.add,
-            )
-            coefficients[cb] = (scale, shift)
+            v = stats_values.setdefault(cb, {})
+            if step == 0:
+                if len(BY_SCALAR[cb]) > 0:
+                    sums_to_statistics(cb)
+                nc.vector.bn_aggr(out=channel_mv[:, 0:2], in_=stats_tiles[cb][:].rearrange("p n s -> p (n s)"))
+            elif step == 1:
+                nc.vector.tensor_add(out=channel_mv[:, 0:1], in0=channel_mv[:, 0:1], in1=bp_c[:, one])
+            elif step == 2:
+                side_by_side = small.tile([P, GROUP], F32, align_bytes=64)
+                nc.vector.transpose(out=side_by_side[:], in_=channel_mv[:])
+                v["side"] = side_by_side
+            elif step == 3:
+                group_stats = small.tile([P, BN_STATS_DIM], F32)
+                nc.vector.bn_stats(out=group_stats[:], in_=v["side"][:])
+                v["stats"] = group_stats
+            elif step == 4:
+                group_mv = small.tile([P, 2], F32)
+                nc.vector.bn_aggr(out=group_mv[:], in_=v["stats"][:])
+                v["mv"] = group_mv
+            elif step == 5:
+                for i in range(2):
+                    wide = small.tile([P, GROUP], F32, tag="wide%d" % i, align_bytes=64)
+                    nc.vector.tensor_copy(out=wide[:], in_=v["mv"][:, i : i + 1].to_broadcast([P, GROUP]))
+                    v["wide", i] = wide
+            elif step == 6:
+                for i in range(2):
+                    spread = small.tile([P, GROUP], F32, tag="spread%d" % i, align_bytes=64)
+                    nc.vector.transpose(out=spread[:], in_=v["wide", i][:])
+                    v["spread", i] = spread
+            elif step == 7:
+                var_eps = small.tile([P, 1], F32)
+                nc.vector.scalar_tensor_tensor(
+                    out=var_eps[:], in0=v["spread", 1][:, 0:1], scalar=EPS, in1=v["spread", 0][:, 1:2],
+                    op0=ALU.add, op1=ALU.add,
+                )
+                centre = small.tile([P, 1], F32)
+                nc.vector.tensor_sub(out=centre[:], in0=bp_c[:, one], in1=v["spread", 0][:, 0:1])
+                v["var_eps"], v["centre"] = var_eps, centre
+            elif step == 8:
+                rstd = small.tile([P, 1], F32)
+                nc.gpsimd.tensor_tensor(out=rstd[:], in0=v["var_eps"][:], in1=neg_half[:], op=ALU.pow)
+                scale = small.tile([P, 1], F32)
+                nc.gpsimd.tensor_tensor(out=scale[:], in0=rstd[:], in1=gn_w_c[:, one], op=ALU.mult)
+                shift = small.tile([P, 1], F32)
+                nc.gpsimd.tensor_scalar(
+                    out=shift[:], in0=v["centre"][:], scalar1=scale[:, 0:1], scalar2=gn_b_c[:, one],
+                    op0=ALU.mult, op1=ALU.add,
+                )
+                coefficients[cb] = (scale, shift)
 
-        def normalise(cb, n, engine):
-            b, half = divmod(n, 2)
+        def normalise(cb, b, engine):
             scale, shift = coefficients[cb]
-            y = y_tiles[(cb, b)][:, half * HALF : (half + 1) * HALF]
+            y = y_tiles[(cb, b)]
             engine.tensor_scalar(
-                out=y, in0=y, scalar1=scale[:, 0:1], scalar2=shift[:, 0:1], op0=ALU.mult, op1=ALU.add
+                out=y[:], in0=y[:], scalar1=scale[:, 0:1], scalar2=shift[:, 0:1], op0=ALU.mult, op1=ALU.add
             )
 
         def transpose_back(cb, n):
@@ -451,7 +449,7 @@ def tile_parallelretention_pb_t_kernel(
         x_tick = {}
         for n in range(UNITS):
             x_tick[(0, n)] = 2 * n + X_LAG
-        tick = N_GROUPS
+        tick = N_GROUPS + 1
         for cb in range(1, N_CB):
             for n in range(UNITS):
                 while tick in x_tick.values():
@@ -462,16 +460,10 @@ def tile_parallelretention_pb_t_kernel(
         tick = 0
         for cb in range(N_CB):
             tick = max(tick, x_tick[(cb, UNITS - 1)] + Z_LAG)
-            for n in range(0, UNITS, 2):
+            for n in range(UNITS):
                 z_tick[(cb, n)] = tick
-                z_tick[(cb, n + 1)] = tick
-                tick += 1 if tick > last_x else 2
-
-        def take_group(g):
-            if g < N_GROUPS:
-                transpose_group(g)
-                if g + AHEAD < N_GROUPS:
-                    load_group(g + AHEAD)
+                if tick <= last_x or n % 2 == 1:
+                    tick += 1
 
         def units_at(ticks, tick):
             return [unit for unit in ticks if ticks[unit] == tick]
@@ -485,22 +477,16 @@ def tile_parallelretention_pb_t_kernel(
                 after = {}
                 for cb in range(N_CB):
                     after[tick - x_tick[(cb, UNITS - 1)]] = cb
+                if 0 <= tick - 1 < N_GROUPS:
+                    copy_group(tick - 1)
                 for h in half_at(A_LAG + 1):
                     activate_a(h)
                 for h in half_at(C_LAG + 1):
                     activate_c(h)
-                if 0 <= tick - 1 < N_GROUPS:
-                    copy_group(tick - 1)
-                for cb, n in units_at(z_tick, tick - 1):
-                    if tick - 1 > last_x:
-                        copy_back(cb, n, n % TAIL_SHARE == 1)
-                    elif n % 2 == 0:
-                        copy_back(cb, n, False)
-                for cb, n in units_at(z_tick, tick - 2):
-                    if tick - 2 <= last_x and n % 2 == 1:
-                        copy_back(cb, n, False)
                 for cb, n in units_at(x_tick, tick - 1):
                     negative_part(cb, n)
+                for cb, n in units_at(z_tick, tick - 1):
+                    copy_back(cb, n, tick - 1 > last_x and n % TAIL_SHARE == 1)
                 if 0 <= tick - 2 < N_GROUPS:
                     quantise_group(tick - 2)
                 for h in half_at(I_LAG):
@@ -509,32 +495,15 @@ def tile_parallelretention_pb_t_kernel(
                     quantise_ac(h)
                 for cb, n in units_at(x_tick, tick - 1):
                     prelu(cb, n)
-                for cb, n in units_at(x_tick, tick - 2):
+                for cb, n in units_at(x_tick, tick - 3):
                     statistics(cb, n)
-                if 2 in after:
-                    channel_moments(after[2])
-                for h in half_at(A_LAG + 2):
+                for step, lag in enumerate(STATS_LAGS):
+                    if lag in after:
+                        stats_step(step, after[lag])
+                for h in half_at(A_LAG + 1 + 1):
                     move_a(h)
-                for h in half_at(C_LAG + 2):
+                for h in half_at(C_LAG + 1 + 1):
                     move_c(h)
-                if tick % 2 == 1:
-                    take_group(tick)
-                for h in half_at(A_LAG):
-                    multiply_ac(h, 0)
-                for h in half_at(C_LAG):
-                    multiply_ac(h, 1)
-                if tick <= N_GROUPS + X_LAG:
-                    for cb, n in units_at(x_tick, tick):
-                        multiply_x(cb, n)
-                elif tick % 2 == 1:
-                    for cb, n in units_at(x_tick, tick) + units_at(x_tick, tick + 1):
-                        multiply_x(cb, n)
-                if MEANS in after:
-                    average_moments(after[MEANS])
-                    spread_of_means(after[MEANS])
-                if SPREAD in after:
-                    average_spread(after[SPREAD])
-                    scale_and_shift(after[SPREAD])
                 if tick == 1:
                     prepare_bias1()
                     prepare_weights(w1_sb, transpose_row_tiles, w1_codes, w1_scales)
@@ -544,9 +513,18 @@ def tile_parallelretention_pb_t_kernel(
                     prepare_weights(wp_sb, transpose_row_tiles_by_fours, wp_codes, wp_scales)
                 if tick == WP_TICK + 1:
                     prepare_channel_vectors()
-                if tick % 2 == 0:
-                    take_group(tick)
+                if tick < N_GROUPS:
+                    transpose_group(tick)
+                    if tick + AHEAD < N_GROUPS:
+                        load_group(tick + AHEAD)
+                for h in half_at(A_LAG):
+                    multiply_ac(h, 0)
+                for h in half_at(C_LAG):
+                    multiply_ac(h, 1)
+                for cb, n in units_at(x_tick, tick):
+                    multiply_x(cb, n)
                 for cb, n in units_at(z_tick, tick):
                     transpose_back(cb, n)
                 for cb, n in units_at(z_tick, tick + N_LEAD):
-                    normalise(cb, n, nc.vector if cb == N_CB - 1 else nc.gpsimd)
+                    if n % 2 == 0:
+                        normalise(cb, n // 2, nc.vector if cb == N_CB - 1 else nc.gpsimd)

@@ -36,16 +36,18 @@ UNITS = 2 * N_BLOCKS
 BLOCK32 = 16
 A_LAG = 3
 C_LAG = 4
-X_LAG = 13
-Z_LAG = 14
-N_LEAD = 5
+X_LAG = 12
+Z_LAG = 13
+N_LEAD = 4
 AHEAD = 7
 WP_TICK = 5
-I_LAG = 11
-STATS_LAGS = (4, 4, 5, 5, 6, 6, 7, 7, 8)
-TAIL_SHARE = 4
-STAGED_BUFS = 6
-BY_SCALAR = (range(0), range(1, 12), range(0), range(0))
+I_LAG = 10
+STATS_LAG = 4
+STATS_STEPS = 12
+C_BY_SCALAR = [0] * 5 + [1] * 11
+TAIL_SHARE = 3
+STAGED_BUFS = 5
+BY_SCALAR = (range(0), range(1, 16, 2), range(0), range(0))
 BN_STATS_DIM = 6
 
 FLOPS = 2 * ROWS * (K * FEATURES * 2 + K * CHANNELS)
@@ -200,19 +202,26 @@ def tile_parallelretention_pb_t_kernel(
         def activate_c(h):
             staged = work.tile([P, 2, HALF], BF16, tag="c_staged", bufs=3)
             c_staged[h] = staged
-            nc.scalar.activation(
-                out=staged[:, 0, :], in_=ac_sums[(h, 1, 0)][:], func=ACT.Identity, bias=bias1[:, 2:3], scale=1.0
-            )
-            nc.vector.tensor_scalar(
-                out=staged[:, 1, :], in0=ac_sums[(h, 1, 1)][:], scalar1=bias1[:, 3:4], scalar2=None, op0=ALU.add
-            )
+            for j in range(2):
+                bias = bias1[:, 2 + j : 3 + j]
+                if j < C_BY_SCALAR[h]:
+                    nc.scalar.activation(
+                        out=staged[:, j, :], in_=ac_sums[(h, 1, j)][:], func=ACT.Identity, bias=bias, scale=1.0
+                    )
+                else:
+                    nc.vector.tensor_scalar(
+                        out=staged[:, j, :], in0=ac_sums[(h, 1, j)][:], scalar1=bias, scalar2=None, op0=ALU.add
+                    )
 
         def move_a(h):
             nc.sync.dma_start(out=a_staged[h][0:LOW, 2:4, :], in_=a_staged[h][LOW:P, 0:2, :])
 
         def move_c(h):
             nc.sync.dma_start(out=a_staged[h][LOW:P, 0:2, :], in_=c_staged[h][0:LOW, :, :])
-            nc.sync.dma_start(out=a_staged[h][LOW:P, 2:4, :], in_=c_staged[h][LOW:P, :, :])
+            nc.gpsimd.tensor_scalar(
+                out=a_staged[h][LOW:P, 2:4, :], in0=c_staged[h][LOW:P, :, :], scalar1=1.0, scalar2=0.0,
+                op0=ALU.mult, op1=ALU.add,
+            )
 
         def interleave_ac(h):
             grouped = work.tile([P, HALF, PACK], BF16, tag="ac_grouped", align_bytes=64)
@@ -242,7 +251,7 @@ def tile_parallelretention_pb_t_kernel(
             x_sums[(cb, n)] = x
 
         def negative_part(cb, n):
-            neg = work.tile([P, HALF], F32, tag="neg", bufs=3)
+            neg = work.tile([P, HALF], F32, tag="neg", bufs=6)
             nc.scalar.activation(
                 out=neg[:], in_=x_sums[(cb, n)][:], func=ACT.Relu, bias=neg_bp[:, cb : cb + 1], scale=-1.0
             )
@@ -286,60 +295,67 @@ def tile_parallelretention_pb_t_kernel(
                     out=minus_first[cb][:], in0=first[:, 0:1], scalar1=-1.0, scalar2=None, op0=ALU.mult
                 )
 
-        def sums_to_statistics(cb):
+        def sums_to_statistics(step, cb):
             rest = slice(BY_SCALAR[cb].start, BY_SCALAR[cb].stop, BY_SCALAR[cb].step)
             n = len(BY_SCALAR[cb])
+            v = stats_values.setdefault(cb, {})
             halves = stats_tiles[cb][:, rest, :].rearrange("p n (e s) -> p e n s", e=2)
-            dev = small.tile([P, n], F32)
-            nc.vector.tensor_scalar(
-                out=dev[:], in0=sums[cb][:, rest], scalar1=1.0 / HALF, scalar2=minus_first[cb][:, 0:1],
-                op0=ALU.mult, op1=ALU.add,
-            )
-            nc.vector.tensor_scalar(
-                out=halves[:, :, :, 1], in0=sums[cb][:, rest].unsqueeze(1).to_broadcast([P, 2, n]),
-                scalar1=1.0 / HALF, scalar2=None, op0=ALU.mult,
-            )
-            nc.vector.scalar_tensor_tensor(
-                out=dev[:], in0=dev[:], scalar=-0.5 * HALF, in1=dev[:], op0=ALU.mult, op1=ALU.mult
-            )
-            for e in range(2):
-                nc.vector.scalar_tensor_tensor(
-                    out=halves[:, e, :, 2], in0=squares[cb][:, rest], scalar=0.5, in1=dev[:],
+            if step == 0:
+                dev = small.tile([P, n], F32)
+                nc.vector.tensor_scalar(
+                    out=dev[:], in0=sums[cb][:, rest], scalar1=1.0 / HALF, scalar2=minus_first[cb][:, 0:1],
                     op0=ALU.mult, op1=ALU.add,
                 )
+                v["unit_dev"] = dev
+                nc.vector.tensor_scalar(
+                    out=halves[:, :, :, 1], in0=sums[cb][:, rest].unsqueeze(1).to_broadcast([P, 2, n]),
+                    scalar1=1.0 / HALF, scalar2=None, op0=ALU.mult,
+                )
+            elif step == 1:
+                dev = v["unit_dev"]
+                nc.vector.scalar_tensor_tensor(
+                    out=dev[:], in0=dev[:], scalar=-0.5 * HALF, in1=dev[:], op0=ALU.mult, op1=ALU.mult
+                )
+            else:
+                for e in range(2):
+                    nc.vector.scalar_tensor_tensor(
+                        out=halves[:, e, :, 2], in0=squares[cb][:, rest], scalar=0.5, in1=v["unit_dev"][:],
+                        op0=ALU.mult, op1=ALU.add,
+                    )
 
         def stats_step(step, cb):
             one = slice(cb, cb + 1)
             v = stats_values.setdefault(cb, {})
-            if step == 0:
+            if step < 3:
                 if len(BY_SCALAR[cb]) > 0:
-                    sums_to_statistics(cb)
+                    sums_to_statistics(step, cb)
+            elif step == 3:
                 nc.vector.bn_aggr(out=channel_mv[:, 0:2], in_=stats_tiles[cb][:].rearrange("p n s -> p (n s)"))
-            elif step == 1:
+            elif step == 4:
                 nc.vector.tensor_add(out=channel_mv[:, 0:1], in0=channel_mv[:, 0:1], in1=bp_c[:, one])
-            elif step == 2:
+            elif step == 5:
                 side_by_side = small.tile([P, GROUP], F32, align_bytes=64)
                 nc.vector.transpose(out=side_by_side[:], in_=channel_mv[:])
                 v["side"] = side_by_side
-            elif step == 3:
+            elif step == 6:
                 group_stats = small.tile([P, BN_STATS_DIM], F32)
                 nc.vector.bn_stats(out=group_stats[:], in_=v["side"][:])
                 v["stats"] = group_stats
-            elif step == 4:
+            elif step == 7:
                 group_mv = small.tile([P, 2], F32)
                 nc.vector.bn_aggr(out=group_mv[:], in_=v["stats"][:])
                 v["mv"] = group_mv
-            elif step == 5:
+            elif step == 8:
                 for i in range(2):
                     wide = small.tile([P, GROUP], F32, tag="wide%d" % i, align_bytes=64)
                     nc.vector.tensor_copy(out=wide[:], in_=v["mv"][:, i : i + 1].to_broadcast([P, GROUP]))
                     v["wide", i] = wide
-            elif step == 6:
+            elif step == 9:
                 for i in range(2):
                     spread = small.tile([P, GROUP], F32, tag="spread%d" % i, align_bytes=64)
                     nc.vector.transpose(out=spread[:], in_=v["wide", i][:])
                     v["spread", i] = spread
-            elif step == 7:
+            elif step == 10:
                 var_eps = small.tile([P, 1], F32)
                 nc.vector.scalar_tensor_tensor(
                     out=var_eps[:], in0=v["spread", 1][:, 0:1], scalar=EPS, in1=v["spread", 0][:, 1:2],
@@ -348,7 +364,7 @@ def tile_parallelretention_pb_t_kernel(
                 centre = small.tile([P, 1], F32)
                 nc.vector.tensor_sub(out=centre[:], in0=bp_c[:, one], in1=v["spread", 0][:, 0:1])
                 v["var_eps"], v["centre"] = var_eps, centre
-            elif step == 8:
+            elif step == 11:
                 rstd = small.tile([P, 1], F32)
                 nc.gpsimd.tensor_tensor(out=rstd[:], in0=v["var_eps"][:], in1=neg_half[:], op=ALU.pow)
                 scale = small.tile([P, 1], F32)
@@ -449,7 +465,7 @@ def tile_parallelretention_pb_t_kernel(
         x_tick = {}
         for n in range(UNITS):
             x_tick[(0, n)] = 2 * n + X_LAG
-        tick = N_GROUPS + 1
+        tick = N_GROUPS
         for cb in range(1, N_CB):
             for n in range(UNITS):
                 while tick in x_tick.values():
@@ -459,7 +475,7 @@ def tile_parallelretention_pb_t_kernel(
         z_tick = {}
         tick = 0
         for cb in range(N_CB):
-            tick = max(tick, x_tick[(cb, UNITS - 1)] + Z_LAG)
+            tick = max(tick, x_tick[(cb, UNITS - 1)] + Z_LAG + (2 if len(BY_SCALAR[cb]) > 0 else 0))
             for n in range(UNITS):
                 z_tick[(cb, n)] = tick
                 if tick <= last_x or n % 2 == 1:
@@ -472,11 +488,15 @@ def tile_parallelretention_pb_t_kernel(
             h, rest = divmod(tick - lag, 2)
             return [h] if rest == 0 and 0 <= h < N_HALVES else []
 
+        def stats_steps(time, x_tick):
+            for cb in range(N_CB):
+                first = 0 if len(BY_SCALAR[cb]) > 0 else 3
+                step = time - 2 * (x_tick[(cb, UNITS - 1)] + STATS_LAG) - 1 + first
+                if first <= step < STATS_STEPS:
+                    stats_step(step, cb)
+
         with tc.manual_schedule():
             for tick in range(max(z_tick.values()) + 3):
-                after = {}
-                for cb in range(N_CB):
-                    after[tick - x_tick[(cb, UNITS - 1)]] = cb
                 if 0 <= tick - 1 < N_GROUPS:
                     copy_group(tick - 1)
                 for h in half_at(A_LAG + 1):
@@ -495,11 +515,10 @@ def tile_parallelretention_pb_t_kernel(
                     quantise_ac(h)
                 for cb, n in units_at(x_tick, tick - 1):
                     prelu(cb, n)
+                stats_steps(2 * tick, x_tick)
                 for cb, n in units_at(x_tick, tick - 3):
                     statistics(cb, n)
-                for step, lag in enumerate(STATS_LAGS):
-                    if lag in after:
-                        stats_step(step, after[lag])
+                stats_steps(2 * tick + 1, x_tick)
                 for h in half_at(A_LAG + 1 + 1):
                     move_a(h)
                 for h in half_at(C_LAG + 1 + 1):
@@ -527,4 +546,4 @@ def tile_parallelretention_pb_t_kernel(
                     transpose_back(cb, n)
                 for cb, n in units_at(z_tick, tick + N_LEAD):
                     if n % 2 == 0:
-                        normalise(cb, n // 2, nc.vector if cb == N_CB - 1 else nc.gpsimd)
+                        normalise(cb, n // 2, nc.vector if cb == N_CB - 1 and n < 4 else nc.gpsimd)

@@ -45,7 +45,7 @@ I_LAG = 10
 STATS_LAG = 4
 STATS_STEPS = 12
 C_BY_SCALAR = [0] * 5 + [1] * 11
-TAIL_SHARE = 3
+TAIL_SHARE = 4
 STAGED_BUFS = 5
 BY_SCALAR = (range(0), range(1, 16, 2), range(0), range(0))
 BN_STATS_DIM = 6
@@ -225,7 +225,10 @@ def tile_parallelretention_pb_t_kernel(
 
         def interleave_ac(h):
             grouped = work.tile([P, HALF, PACK], BF16, tag="ac_grouped", align_bytes=64)
-            nc.vector.tensor_copy(out=grouped[:], in_=a_staged[h][:].rearrange("p t c -> p c t"))
+            nc.vector.tensor_copy(
+                out=grouped[:].rearrange("p (c i) t -> p c t i", i=4),
+                in_=a_staged[h][:].rearrange("p t (c i) -> p c t i", i=4),
+            )
             ac_grouped[h] = grouped
 
         def quantise_ac(h):
@@ -383,9 +386,9 @@ def tile_parallelretention_pb_t_kernel(
                 out=y[:], in0=y[:], scalar1=scale[:, 0:1], scalar2=shift[:, 0:1], op0=ALU.mult, op1=ALU.add
             )
 
-        def transpose_back(cb, n):
+        def transpose_back(cb, n, pool, tag):
             b, half = divmod(n, 2)
-            zt = ps_t.tile([P, HALF_TILES, P], F32, tag="t")
+            zt = pool.tile([P, HALF_TILES, P], F32, tag=tag)
             for j in range(HALF_TILES):
                 col = (HALF_TILES * half + j) * P
                 nc.tensor.transpose(zt[:, j, :], y_tiles[(cb, b)][:, col : col + P], ident[:])
@@ -410,7 +413,7 @@ def tile_parallelretention_pb_t_kernel(
                 )
 
         def prepare_weights(source, transposes, codes, scales):
-            grouped = work.tile([P, HALF * PACK], BF16, tag="h_grouped", align_bytes=64, bufs=3)
+            grouped = work.tile([P, HALF * PACK], BF16, tag="w_grouped", align_bytes=64, bufs=1)
             g32 = grouped[:].bitcast(F32).rearrange("p (c u) -> p c u", u=2)
             for pair in range(2):
                 bank = ps_t.tile([P, 2, PAIR], F32, tag="t")
@@ -543,7 +546,10 @@ def tile_parallelretention_pb_t_kernel(
                 for cb, n in units_at(x_tick, tick):
                     multiply_x(cb, n)
                 for cb, n in units_at(z_tick, tick):
-                    transpose_back(cb, n)
+                    if tick > last_x + 2 and n % 2 == 1:
+                        transpose_back(cb, n, ps_mx, "mx")
+                    else:
+                        transpose_back(cb, n, ps_t, "t")
                 for cb, n in units_at(z_tick, tick + N_LEAD):
                     if n % 2 == 0:
                         normalise(cb, n // 2, nc.vector if cb == N_CB - 1 and n < 4 else nc.gpsimd)

from contextlib import ExitStack

import concourse.mybir as mybir
from concourse.masks import make_identity

F32 = mybir.dt.float32
BF16 = mybir.dt.bfloat16
U32 = mybir.dt.uint32
U8 = mybir.dt.uint8
I32 = mybir.dt.int32
FP8X4 = mybir.dt.float8_e4m3fn_x4
ACT = mybir.ActivationFunctionType
ALU = mybir.AluOpType

P = 128
LOW = 64
PACK = 4
ROWS = 8192
K = 512
WORDS = K // 2
FEATURES = 256
CHANNELS = 512
GROUP = 32
EPS = 1e-5

BLOCK = 1024
TILES = BLOCK // P
N_BLOCKS = ROWS // BLOCK
HALF = 512
HALF_TILES = HALF // P
PAIR = 2 * P
N_CB = CHANNELS // P
N_HALVES = ROWS // HALF
N_GROUPS = 2 * N_HALVES
UNITS = 2 * N_BLOCKS
BLOCK32 = 16
A_LAG = 3
C_LAG = 4
X_LAG = 12
Z_LAG = 13
N_LEAD = 4
AHEAD = 7
WP_TICK = 5
I_LAG = 10
STATS_LAG = 4
STATS_STEPS = 12
C_BY_SCALAR = [0] * 5 + [1] * 11
TAIL_SHARE = 4
STAGED_BUFS = 5
BY_SCALAR = (range(0), range(1, 16, 2), range(0), range(0))
BN_STATS_DIM = 6

FLOPS = 2 * ROWS * (K * FEATURES * 2 + K * CHANNELS)


def transpose_row_tiles(nc, bank, words, first_tile, ident):
    for i in range(2):
        for u in range(2):
            start = (first_tile + i) * WORDS + u * P
            nc.tensor.transpose(bank[:, u, i * P : (i + 1) * P], words[:, start : start + P], ident[:])


def transpose_row_tiles_by_fours(nc, bank, words, first_tile, ident):
    for i in range(2):
        for u in range(2):
            start = (first_tile + i) * WORDS
            nc.tensor.transpose(
                bank[:, u, i * P : (i + 1) * P], words[:, start + u : start + WORDS : 2], ident[:]
            )


def tile_parallelretention_pb_t_kernel(
    tc, h_ret, h_prime, Wr, br, Wc, bc, Wp, bp, prelu_w, gn_w, gn_b, out
):
    nc = tc.nc
    with ExitStack() as pools:
        keep = pools.enter_context(tc.tile_pool(name="keep", bufs=1))
        streamed = pools.enter_context(tc.tile_pool(name="streamed", bufs=8))
        work = pools.enter_context(tc.tile_pool(name="work", bufs=2))
        quantised = pools.enter_context(tc.tile_pool(name="quantised", bufs=5))
        y_pool = pools.enter_context(tc.tile_pool(name="y_pool", bufs=20))
        small = pools.enter_context(tc.tile_pool(name="small", bufs=2))
        ps_t = pools.enter_context(tc.psum_pool(name="ps_t", bufs=4))
        ps_mx = pools.enter_context(tc.psum_pool(name="ps_mx", bufs=4))

        ident = keep.tile([P, P], F32)
        make_identity(nc, ident[:])
        warm = keep.tile([P, 1], F32)
        nc.vector.memset(warm[:], 0.0)
        nc.scalar.activation(out=warm[:], in_=warm[:], func=ACT.Gelu)
        channel_mv = keep.tile([P, GROUP], F32, align_bytes=64)
        nc.vector.memset(channel_mv[:], 0.0)
        neg_half = keep.tile([P, 1], F32)
        nc.vector.memset(neg_half[:], -0.5)
        rows_bf = keep.tile([P, P], BF16)
        nc.vector.memset(rows_bf[:], 0.0)

        w1_codes = keep.tile([P, 4 * P], U32, align_bytes=64)
        w1_scales = keep.tile([P, 4 * P], U8, align_bytes=64)
        wp_codes = keep.tile([P, CHANNELS], U32, align_bytes=64)
        wp_scales = keep.tile([P, CHANNELS], U8, align_bytes=64)
        ac_codes = {}
        ac_scales = {}
        for h in range(N_HALVES):
            ac_codes[h] = keep.tile([P, HALF], U32, name="ac_codes%d" % h, align_bytes=64)
            ac_scales[h] = keep.tile([P, HALF], U8, name="ac_scales%d" % h, align_bytes=64)
        bias1 = keep.tile([P, 4], F32)
        chan = keep.tile([P, 4 * N_CB], F32)
        neg_bp = keep.tile([P, N_CB], F32)
        one_minus_w = keep.tile([P, N_CB], F32)
        bp_c = chan[:, 0:N_CB]
        prelu_w_c = chan[:, N_CB : 2 * N_CB]
        gn_w_c = chan[:, 2 * N_CB : 3 * N_CB]
        gn_b_c = chan[:, 3 * N_CB : 4 * N_CB]

        sums = []
        squares = []
        minus_first = []
        for cb in range(N_CB):
            sums.append(keep.tile([P, UNITS], F32, name="sums%d" % cb))
            squares.append(keep.tile([P, UNITS], F32, name="squares%d" % cb))
            minus_first.append(keep.tile([P, 1], F32, name="minus_first%d" % cb))

        h_tiles = {}
        h_banks = {}
        h_grouped = {}
        h_quantised = {}
        ac_sums = {}
        a_staged = {}
        c_staged = {}
        ac_grouped = {}
        x_sums = {}
        negs = {}
        y_tiles = {}
        stats_tiles = {}
        stats_values = {}
        coefficients = {}
        z_banks = {}
        z_tiles = {}

        def load_group(g, pieces=1):
            h, i = divmod(g, 2)
            b, half = divmod(h, 2)
            source = (h_ret, h_prime)[i][b * BLOCK : (b + 1) * BLOCK, :].rearrange("(p j) k -> p j k", j=TILES)
            tile = streamed.tile([P, HALF_TILES * K], BF16, tag="rows")
            view = tile[:].rearrange("p (j k) -> p j k", j=HALF_TILES)
            step = HALF_TILES // pieces
            for j in range(0, HALF_TILES, step):
                nc.sync.dma_start(
                    out=view[:, j : j + step, :],
                    in_=source[:, HALF_TILES * half + j : HALF_TILES * half + j + step, :],
                )
            h_tiles[g] = tile

        def transpose_group(g):
            h_banks[g] = []
            for pair in range(2):
                bank = ps_t.tile([P, 2, PAIR], F32, tag="t")
                transpose_row_tiles(nc, bank, h_tiles[g][:].bitcast(F32), 2 * pair, ident)
                h_banks[g].append(bank)

        def copy_group(g):
            grouped = work.tile([P, HALF * PACK], BF16, tag="h_grouped", align_bytes=64, bufs=3)
            g32 = grouped[:].bitcast(F32).rearrange("p (c u) -> p c u", u=2)
            for pair in range(2):
                nc.scalar.copy(
                    out=g32[:, pair * PAIR : (pair + 1) * PAIR, :],
                    in_=h_banks[g][pair][:].rearrange("p u c -> p c u"),
                )
            h_grouped[g] = grouped

        def quantise_group(g):
            codes = quantised.tile([P, HALF], U32, tag="codes", align_bytes=64)
            scales = quantised.tile([P, HALF], U8, tag="scales", align_bytes=64)
            nc.vector.quantize_mx(out=codes[:].bitcast(FP8X4), scales=scales[:], in_=h_grouped[g][:])
            h_quantised[g] = (codes, scales)

        def multiply_ac(h, i):
            codes, scales = h_quantised[2 * h + i]
            for j in range(2):
                acc = ps_mx.tile([P, HALF], F32, tag="mx")
                w = slice((2 * i + j) * P, (2 * i + j + 1) * P)
                nc.tensor.matmul_mx(
                    out=acc[:],
                    lhsT=w1_codes[:, w].bitcast(FP8X4),
                    lhsT_scale=w1_scales[:, w],
                    rhs=codes[:].bitcast(FP8X4),
                    rhs_scale=scales[:],
                    start=True,
                    stop=True,
                )
                ac_sums[(h, i, j)] = acc

        def activate_a(h):
            staged = work.tile([P, PACK, HALF], BF16, tag="staged", bufs=STAGED_BUFS)
            for j in range(2):
                nc.scalar.activation(
                    out=staged[:, j, :], in_=ac_sums[(h, 0, j)][:], func=ACT.Gelu, bias=bias1[:, j : j + 1], scale=1.0
                )
            a_staged[h] = staged

        def activate_c(h):
            staged = work.tile([P, 2, HALF], BF16, tag="c_staged", bufs=3)
            c_staged[h] = staged
            for j in range(2):
                bias = bias1[:, 2 + j : 3 + j]
                if j < C_BY_SCALAR[h]:
                    nc.scalar.activation(
                        out=staged[:, j, :], in_=ac_sums[(h, 1, j)][:], func=ACT.Identity, bias=bias, scale=1.0
                    )
                else:
                    nc.vector.tensor_scalar(
                        out=staged[:, j, :], in0=ac_sums[(h, 1, j)][:], scalar1=bias, scalar2=None, op0=ALU.add
                    )

        def move_a(h):
            nc.sync.dma_start(out=a_staged[h][0:LOW, 2:4, :], in_=a_staged[h][LOW:P, 0:2, :])

        def move_c(h):
            nc.sync.dma_start(out=a_staged[h][LOW:P, 0:2, :], in_=c_staged[h][0:LOW, :, :])
            nc.gpsimd.tensor_scalar(
                out=a_staged[h][LOW:P, 2:4, :], in0=c_staged[h][LOW:P, :, :], scalar1=1.0, scalar2=0.0,
                op0=ALU.mult, op1=ALU.add,
            )

        def interleave_ac(h):
            grouped = work.tile([P, HALF, PACK], BF16, tag="ac_grouped", align_bytes=64)
            nc.vector.tensor_copy(
                out=grouped[:].rearrange("p (c i) t -> p c t i", i=4),
                in_=a_staged[h][:].rearrange("p t (c i) -> p c t i", i=4),
            )
            ac_grouped[h] = grouped

        def quantise_ac(h):
            nc.vector.quantize_mx(
                out=ac_codes[h][:].bitcast(FP8X4),
                scales=ac_scales[h][:],
                in_=ac_grouped[h][:].rearrange("p c t -> p (c t)"),
            )

        def multiply_x(cb, n):
            x = ps_mx.tile([P, HALF], F32, tag="mx")
            w = slice(cb * P, (cb + 1) * P)
            for repeat in range(2 if n % 2 == 0 or cb == 0 else 1):
                nc.tensor.matmul_mx(
                    out=x[:],
                    lhsT=wp_codes[:, w].bitcast(FP8X4),
                    lhsT_scale=wp_scales[:, w],
                    rhs=ac_codes[n][:].bitcast(FP8X4),
                    rhs_scale=ac_scales[n][:],
                    start=True,
                    stop=True,
                )
            x_sums[(cb, n)] = x

        def negative_part(cb, n):
            neg = work.tile([P, HALF], F32, tag="neg", bufs=6)
            nc.scalar.activation(
                out=neg[:], in_=x_sums[(cb, n)][:], func=ACT.Relu, bias=neg_bp[:, cb : cb + 1], scale=-1.0
            )
            negs[(cb, n)] = neg

        def prelu(cb, n):
            b, half = divmod(n, 2)
            if half == 0:
                y = y_pool.tile([P, BLOCK], F32, tag="y")
                y_tiles[(cb, b)] = y
            nc.vector.scalar_tensor_tensor(
                out=y_tiles[(cb, b)][:, half * HALF : (half + 1) * HALF],
                in0=negs[(cb, n)][:],
                scalar=one_minus_w[:, cb : cb + 1],
                in1=x_sums[(cb, n)][:],
                op0=ALU.mult,
                op1=ALU.add,
                accum_out=sums[cb][:, n : n + 1] if n in BY_SCALAR[cb] else None,
            )

        def statistics(cb, n):
            b, half = divmod(n, 2)
            y = y_tiles[(cb, b)][:, half * HALF : (half + 1) * HALF]
            if n == 0:
                stats = small.tile([P, UNITS, BN_STATS_DIM], F32)
                stats_tiles[cb] = stats
                if len(BY_SCALAR[cb]) > 0:
                    nc.gpsimd.memset(stats[:], 0.5 * HALF)
            if n in BY_SCALAR[cb]:
                unused = work.tile([P, HALF], BF16, tag="unused")
                nc.scalar.activation(
                    out=unused[:], in_=y, func=ACT.Square, bias=minus_first[cb][:], scale=1.0,
                    accum_out=squares[cb][:, n : n + 1],
                )
            else:
                nc.vector.bn_stats(out=stats_tiles[cb][:, n, :], in_=y)
            if n == 0 and len(BY_SCALAR[cb]) > 0:
                first = small.tile([P, 2], F32)
                nc.vector.bn_aggr(out=first[:], in_=stats_tiles[cb][:, 0, :])
                nc.vector.tensor_scalar(
                    out=minus_first[cb][:], in0=first[:, 0:1], scalar1=-1.0, scalar2=None, op0=ALU.mult
                )

        def sums_to_statistics(step, cb):
            rest = slice(BY_SCALAR[cb].start, BY_SCALAR[cb].stop, BY_SCALAR[cb].step)
            n = len(BY_SCALAR[cb])
            v = stats_values.setdefault(cb, {})
            halves = stats_tiles[cb][:, rest, :].rearrange("p n (e s) -> p e n s", e=2)
            if step == 0:
                dev = small.tile([P, n], F32)
                nc.vector.tensor_scalar(
                    out=dev[:], in0=sums[cb][:, rest], scalar1=1.0 / HALF, scalar2=minus_first[cb][:, 0:1],
                    op0=ALU.mult, op1=ALU.add,
                )
                v["unit_dev"] = dev
                nc.vector.tensor_scalar(
                    out=halves[:, :, :, 1], in0=sums[cb][:, rest].unsqueeze(1).to_broadcast([P, 2, n]),
                    scalar1=1.0 / HALF, scalar2=None, op0=ALU.mult,
                )
            elif step == 1:
                dev = v["unit_dev"]
                nc.vector.scalar_tensor_tensor(
                    out=dev[:], in0=dev[:], scalar=-0.5 * HALF, in1=dev[:], op0=ALU.mult, op1=ALU.mult
                )
            else:
                for e in range(2):
                    nc.vector.scalar_tensor_tensor(
                        out=halves[:, e, :, 2], in0=squares[cb][:, rest], scalar=0.5, in1=v["unit_dev"][:],
                        op0=ALU.mult, op1=ALU.add,
                    )

        def stats_step(step, cb):
            one = slice(cb, cb + 1)
            v = stats_values.setdefault(cb, {})
            if step < 3:
                if len(BY_SCALAR[cb]) > 0:
                    sums_to_statistics(step, cb)
            elif step == 3:
                nc.vector.bn_aggr(out=channel_mv[:, 0:2], in_=stats_tiles[cb][:].rearrange("p n s -> p (n s)"))
            elif step == 4:
                nc.vector.tensor_add(out=channel_mv[:, 0:1], in0=channel_mv[:, 0:1], in1=bp_c[:, one])
            elif step == 5:
                side_by_side = small.tile([P, GROUP], F32, align_bytes=64)
                nc.vector.transpose(out=side_by_side[:], in_=channel_mv[:])
                v["side"] = side_by_side
            elif step == 6:
                group_stats = small.tile([P, BN_STATS_DIM], F32)
                nc.vector.bn_stats(out=group_stats[:], in_=v["side"][:])
                v["stats"] = group_stats
            elif step == 7:
                group_mv = small.tile([P, 2], F32)
                nc.vector.bn_aggr(out=group_mv[:], in_=v["stats"][:])
                v["mv"] = group_mv
            elif step == 8:
                for i in range(2):
                    wide = small.tile([P, GROUP], F32, tag="wide%d" % i, align_bytes=64)
                    nc.vector.tensor_copy(out=wide[:], in_=v["mv"][:, i : i + 1].to_broadcast([P, GROUP]))
                    v["wide", i] = wide
            elif step == 9:
                for i in range(2):
                    spread = small.tile([P, GROUP], F32, tag="spread%d" % i, align_bytes=64)
                    nc.vector.transpose(out=spread[:], in_=v["wide", i][:])
                    v["spread", i] = spread
            elif step == 10:
                var_eps = small.tile([P, 1], F32)
                nc.vector.scalar_tensor_tensor(
                    out=var_eps[:], in0=v["spread", 1][:, 0:1], scalar=EPS, in1=v["spread", 0][:, 1:2],
                    op0=ALU.add, op1=ALU.add,
                )
                centre = small.tile([P, 1], F32)
                nc.vector.tensor_sub(out=centre[:], in0=bp_c[:, one], in1=v["spread", 0][:, 0:1])
                v["var_eps"], v["centre"] = var_eps, centre
            elif step == 11:
                rstd = small.tile([P, 1], F32)
                nc.gpsimd.tensor_tensor(out=rstd[:], in0=v["var_eps"][:], in1=neg_half[:], op=ALU.pow)
                scale = small.tile([P, 1], F32)
                nc.gpsimd.tensor_tensor(out=scale[:], in0=rstd[:], in1=gn_w_c[:, one], op=ALU.mult)
                shift = small.tile([P, 1], F32)
                nc.gpsimd.tensor_scalar(
                    out=shift[:], in0=v["centre"][:], scalar1=scale[:, 0:1], scalar2=gn_b_c[:, one],
                    op0=ALU.mult, op1=ALU.add,
                )
                coefficients[cb] = (scale, shift)

        def normalise(cb, b, engine):
            scale, shift = coefficients[cb]
            y = y_tiles[(cb, b)]
            engine.tensor_scalar(
                out=y[:], in0=y[:], scalar1=scale[:, 0:1], scalar2=shift[:, 0:1], op0=ALU.mult, op1=ALU.add
            )

        def transpose_back(cb, n, pool, tag):
            b, half = divmod(n, 2)
            zt = pool.tile([P, HALF_TILES, P], F32, tag=tag)
            for j in range(HALF_TILES):
                col = (HALF_TILES * half + j) * P
                nc.tensor.transpose(zt[:, j, :], y_tiles[(cb, b)][:, col : col + P], ident[:])
            z_banks[(cb, n)] = zt

        def copy_back(cb, n, on_vector):
            b, half = divmod(n, 2)
            if half == 0:
                z = streamed.tile([P, TILES, P], F32, tag="rows")
                z_tiles[(cb, b)] = z
            part = z_tiles[(cb, b)][:, HALF_TILES * half : HALF_TILES * (half + 1), :]
            if on_vector:
                nc.vector.tensor_copy(out=part, in_=z_banks[(cb, n)][:])
            else:
                nc.scalar.copy(out=part, in_=z_banks[(cb, n)][:])
            if half == 1:
                nc.sync.dma_start(
                    out=out[b * BLOCK : (b + 1) * BLOCK, cb * P : (cb + 1) * P].rearrange(
                        "(p j) c -> p j c", j=TILES
                    ),
                    in_=z_tiles[(cb, b)][:],
                )

        def prepare_weights(source, transposes, codes, scales):
            grouped = work.tile([P, HALF * PACK], BF16, tag="w_grouped", align_bytes=64, bufs=1)
            g32 = grouped[:].bitcast(F32).rearrange("p (c u) -> p c u", u=2)
            for pair in range(2):
                bank = ps_t.tile([P, 2, PAIR], F32, tag="t")
                transposes(nc, bank, source[:].bitcast(F32), 2 * pair, ident)
                nc.vector.tensor_copy(
                    out=g32[:, pair * PAIR : (pair + 1) * PAIR, :], in_=bank[:].rearrange("p u c -> p c u")
                )
            nc.vector.quantize_mx(out=codes[:].bitcast(FP8X4), scales=scales[:], in_=grouped[:])

        def prepare_bias1():
            for i in range(2):
                nc.vector.tensor_copy(out=bias1[:, 2 * i : 2 * i + 2], in_=bias_bf[:, i, 0:2])

        rows_f32 = keep.tile([P, P], F32)

        def prepare_channel_vectors():
            bank = ps_t.tile([P, P], F32, tag="t")
            nc.tensor.transpose(bank[:], rows_f32[:], ident[:])
            nc.vector.tensor_copy(out=chan[:], in_=bank[:, 0 : 4 * N_CB])
            nc.vector.tensor_scalar(out=neg_bp[:], in0=bp_c, scalar1=-1.0, scalar2=None, op0=ALU.mult)
            nc.vector.tensor_scalar(
                out=one_minus_w[:], in0=prelu_w_c, scalar1=-1.0, scalar2=1.0, op0=ALU.mult, op1=ALU.add
            )

        load_group(0, pieces=2)
        load_group(1)
        w1_sb = y_pool.tile([P, 4 * K], BF16, tag="y")
        bias_bf = keep.tile([P, 2, BLOCK32], BF16)
        for i, (weights, bias) in enumerate(((Wr, br), (Wc, bc))):
            for s in range(2):
                part = slice(s * LOW, (s + 1) * LOW)
                nc.sync.dma_start(
                    out=w1_sb[part, 2 * K * i : 2 * K * (i + 1)].rearrange("p (j k) -> p j k", j=2),
                    in_=weights.rearrange("(m s j) k -> s m j k", s=2, j=2)[s, :, :, :],
                )
                nc.scalar.dma_start(
                    out=bias_bf[part, i, 0:2], in_=bias.rearrange("(m s j) -> s m j", s=2, j=2)[s, :, :]
                )
        for v, vec in enumerate((bp, prelu_w, gn_w, gn_b)):
            nc.scalar.dma_start(
                out=rows_bf[N_CB * v : N_CB * (v + 1), :], in_=vec.rearrange("(c p) -> c p", p=P)
            )
        for g in range(2, 4):
            load_group(g)
        wp_sb = y_pool.tile([P, N_CB * K], BF16, tag="y")
        nc.sync.dma_start(
            out=wp_sb[:].rearrange("p (c k) -> p c k", c=N_CB), in_=Wp.rearrange("(c p) k -> p c k", p=P)
        )
        for g in range(4, AHEAD):
            load_group(g)

        x_tick = {}
        for n in range(UNITS):
            x_tick[(0, n)] = 2 * n + X_LAG
        tick = N_GROUPS
        for cb in range(1, N_CB):
            for n in range(UNITS):
                while tick in x_tick.values():
                    tick += 1
                x_tick[(cb, n)] = tick
        last_x = max(x_tick.values())
        z_tick = {}
        tick = 0
        for cb in range(N_CB):
            tick = max(tick, x_tick[(cb, UNITS - 1)] + Z_LAG + (2 if len(BY_SCALAR[cb]) > 0 else 0))
            for n in range(UNITS):
                z_tick[(cb, n)] = tick
                if tick <= last_x or n % 2 == 1:
                    tick += 1

        def units_at(ticks, tick):
            return [unit for unit in ticks if ticks[unit] == tick]

        def half_at(lag):
            h, rest = divmod(tick - lag, 2)
            return [h] if rest == 0 and 0 <= h < N_HALVES else []

        def stats_steps(time, x_tick):
            for cb in range(N_CB):
                first = 0 if len(BY_SCALAR[cb]) > 0 else 3
                step = time - 2 * (x_tick[(cb, UNITS - 1)] + STATS_LAG) - 1 + first
                if first <= step < STATS_STEPS:
                    stats_step(step, cb)

        with tc.manual_schedule():
            for tick in range(max(z_tick.values()) + 3):
                if 0 <= tick - 1 < N_GROUPS:
                    copy_group(tick - 1)
                for h in half_at(A_LAG + 1):
                    activate_a(h)
                for h in half_at(C_LAG + 1):
                    activate_c(h)
                for cb, n in units_at(x_tick, tick - 1):
                    negative_part(cb, n)
                for cb, n in units_at(z_tick, tick - 1):
                    copy_back(cb, n, tick - 1 > last_x and n % TAIL_SHARE == 1)
                if 0 <= tick - 2 < N_GROUPS:
                    quantise_group(tick - 2)
                for h in half_at(I_LAG):
                    interleave_ac(h)
                for h in half_at(I_LAG + 1):
                    quantise_ac(h)
                for cb, n in units_at(x_tick, tick - 1):
                    prelu(cb, n)
                stats_steps(2 * tick, x_tick)
                for cb, n in units_at(x_tick, tick - 3):
                    statistics(cb, n)
                stats_steps(2 * tick + 1, x_tick)
                for h in half_at(A_LAG + 1 + 1):
                    move_a(h)
                for h in half_at(C_LAG + 1 + 1):
                    move_c(h)
                if tick == 1:
                    prepare_bias1()
                    prepare_weights(w1_sb, transpose_row_tiles, w1_codes, w1_scales)
                if tick == 3:
                    nc.vector.tensor_copy(out=rows_f32[:], in_=rows_bf[:])
                if tick == WP_TICK:
                    prepare_weights(wp_sb, transpose_row_tiles_by_fours, wp_codes, wp_scales)
                if tick == WP_TICK + 1:
                    prepare_channel_vectors()
                if tick < N_GROUPS:
                    transpose_group(tick)
                    if tick + AHEAD < N_GROUPS:
                        load_group(tick + AHEAD)
                for h in half_at(A_LAG):
                    multiply_ac(h, 0)
                for h in half_at(C_LAG):
                    multiply_ac(h, 1)
                for cb, n in units_at(x_tick, tick):
                    multiply_x(cb, n)
                for cb, n in units_at(z_tick, tick):
                    if tick > last_x + 2 and n % 2 == 1:
                        transpose_back(cb, n, ps_mx, "mx")
                    else:
                        transpose_back(cb, n, ps_t, "t")
                for cb, n in units_at(z_tick, tick + N_LEAD):
                    if n % 2 == 0:
                        normalise(cb, n // 2, nc.vector if cb == N_CB - 1 and n < 4 else nc.gpsimd)
